import numpy as np
import ml_dtypes


def mxq(x, axis, fmt="e4m3"):
    dtype, down = {"e4m3": (ml_dtypes.float8_e4m3fn, 7), "e5m2": (ml_dtypes.float8_e5m2, 14)}[fmt]
    v = np.moveaxis(np.asarray(x, np.float32).astype(ml_dtypes.bfloat16).astype(np.float64), axis, -1)
    blocks = v.reshape(v.shape[:-1] + (-1, 32))
    amax = np.abs(blocks).max(-1, keepdims=True)
    byte = np.maximum(np.where(amax > 0, np.frexp(amax)[1] - 1 + 127, 0) - down, 1)
    scale = np.exp2(byte - 127.0)
    codes = (blocks / scale).astype(np.float32).astype(dtype).astype(np.float64)
    return np.moveaxis((codes * scale).reshape(v.shape), -1, axis)


WIDE = False


def mx_kscale(k):
    if not WIDE:
        return np.ones(k)
    levels = np.array([10, -10, 5, -5, 0])
    a = np.random.permutation(np.resize(levels, k // 512 * 4)).reshape(k // 512, 4)
    idx = np.arange(k)
    return np.exp2(a[idx // 512, idx % 128 // 32])


BF16 = ml_dtypes.bfloat16


def bf(x):
    return np.asarray(x, np.float32).astype(BF16)


def f64(x):
    return np.asarray(x).astype(np.float64)


B, S, HIDDEN, H, HKV, D = 1, 512, 2048, 16, 4, 128
REP = H // HKV
MASK_NEG = -2.3819763e38


def setup_inputs():
    t = mx_kscale(H * D).reshape(HKV, REP, D)[:, 0]
    sgn = np.where(np.random.standard_normal((HKV, D)) < 0.0, -1.0, 1.0)
    return {"q_rot": bf(np.random.standard_normal((B, S, H, D)) * 1.2),
            "k_rot": bf(np.random.standard_normal((B, S, HKV, D)) * 1.2),
            "v": bf((0.2 + 2.0 * np.random.random((B, S, HKV, D))) * sgn * t),
            "w_o": bf(np.random.standard_normal((HIDDEN, H * D)) * 2.0 / np.sqrt(H * D) / np.repeat(t, REP, axis=0).reshape(H * D))}


def reference(q_rot, k_rot, v, w_o):
    q = f64(q_rot).reshape(B, S, HKV, REP, D).transpose(0, 2, 3, 1, 4).reshape(B, HKV, REP * S, D)
    k = f64(k_rot).transpose(0, 2, 3, 1)
    s = (q @ k).reshape(B, HKV, REP, S, S) * D ** -0.5
    s = s + np.triu(np.full((S, S), MASK_NEG), k=1)
    e = np.exp(s - s.max(-1, keepdims=True))
    pv = mxq(e.reshape(B, HKV, REP * S, S), 3, "e4m3") @ mxq(f64(v).transpose(0, 2, 1, 3), 2, "e4m3")
    o = pv.reshape(B, HKV, REP, S, D) / e.sum(-1, keepdims=True)
    o = o.transpose(0, 3, 1, 2, 4).reshape(B, S, H * D)
    return mxq(o, 2, "e4m3") @ mxq(f64(w_o), 1, "e4m3").T

@@ -1,0 +1,340 @@
+from contextlib import ExitStack
+
+import concourse.mybir as mybir
+from concourse.masks import make_identity
+
+F32 = mybir.dt.float32
+BF16 = mybir.dt.bfloat16
+U32 = mybir.dt.uint32
+U8 = mybir.dt.uint8
+FP8X4 = mybir.dt.float8_e4m3fn_x4
+ACT = mybir.ActivationFunctionType
+ALU = mybir.AluOpType
+AXIS = mybir.AxisListType
+
+P = 128
+S = 512
+H = 16
+HKV = 4
+REP = H // HKV
+D = 128
+HIDDEN = 2048
+PACK = 4
+K_PASS = P * PACK
+BANK = 512
+CHUNKS = S // P
+N_BLOCKS = HIDDEN // BANK
+PASSES = HIDDEN // K_PASS
+UNITS = CHUNKS * H
+STEPS = CHUNKS * HKV
+OUT_BLOCKS = CHUNKS * N_BLOCKS
+W_BLOCKS = N_BLOCKS * PASSES
+SCALE = D**-0.5
+MASK_NEG = -2.3819763e38
+
+SCORE_AT = 0
+MAX_AT = SCORE_AT + 1
+EXP_AT = MAX_AT + 1
+TURN_E_AT = EXP_AT + 1
+COPY_E_AT = TURN_E_AT + 2
+QUANTISE_E_AT = COPY_E_AT + 3
+MULTIPLY_V_AT = QUANTISE_E_AT + 1
+NORMALISE_AT = MULTIPLY_V_AT + 1
+TURN_O_AT = NORMALISE_AT + 1
+COPY_O_AT = TURN_O_AT + 1
+QUANTISE_O_AT = COPY_O_AT + 4 * (HKV - 1) + 1
+TURN_Q_AT = SCORE_AT - 6
+COPY_Q_AT = TURN_Q_AT + 1
+QUANTISE_V_AT = SCORE_AT
+TURN_W_AT = 4
+COPY_W_AT = TURN_W_AT + 1
+QUANTISE_W_AT = COPY_W_AT + 2
+PROJECT_AT = QUANTISE_W_AT + 2 * (W_BLOCKS - 1) + 1
+PROJECT_EVERY = 3
+STORE_AT = PROJECT_AT + 1
+TICKS = STORE_AT + PROJECT_EVERY * (OUT_BLOCKS - 1) + 1
+
+FLOPS = 2 * H * S * S * D * 2 + 2 * S * HIDDEN * HIDDEN
+
+
+def run_if_due(stage_fn, tick, first, every, count):
+    piece, rest = divmod(tick - first, every)
+    if rest == 0 and 0 <= piece < count:
+        stage_fn(piece)
+
+
+def tile_gemmaattention_pb_kernel(tc, q_rot, k_rot, v, w_o, out):
+    nc = tc.nc
+    q_rows = q_rot.rearrange("b s h d -> (b s) (h d)")
+    out_rows = out.rearrange("b s n -> (b s) n")
+
+    with ExitStack() as ctx:
+        ctx.enter_context(tc.manual_schedule())
+        keep = ctx.enter_context(tc.tile_pool(name="keep", bufs=1))
+        stage = ctx.enter_context(tc.tile_pool(name="stage", bufs=2))
+        stats = ctx.enter_context(tc.tile_pool(name="stats", bufs=4))
+        results = ctx.enter_context(tc.tile_pool(name="results", bufs=4))
+        psum = ctx.enter_context(tc.psum_pool(name="psum", bufs=8))
+
+        e_tiles = [keep.tile([P, REP * S], BF16, name="e_sb%d" % b) for b in range(2)]
+        for e_sb in e_tiles:
+            nc.vector.memset(e_sb[:], 0.0)
+
+        ident_bf = keep.tile([P, P], BF16)
+        make_identity(nc, ident_bf[:])
+        ident_f32 = keep.tile([P, P], F32)
+        make_identity(nc, ident_f32[:])
+        mask_f32 = keep.tile([P, P], F32)
+        nc.gpsimd.memset(mask_f32[:], 0.0)
+        nc.gpsimd.affine_select(
+            out=mask_f32[:],
+            in_=mask_f32[:],
+            compare_op=ALU.is_ge,
+            fill=MASK_NEG,
+            base=0,
+            pattern=[[-1, P]],
+            channel_multiplier=1,
+        )
+        mask_bf = keep.tile([P, P], BF16)
+        nc.vector.tensor_copy(out=mask_bf[:], in_=mask_f32[:])
+
+        k_sb = keep.tile([P, CHUNKS, HKV * D], BF16)
+        nc.sync.dma_start(out=k_sb[:], in_=k_rot.rearrange("b (t p) g d -> p (b t) (g d)", p=P))
+        q_sb = [keep.tile([P, H * D], BF16, name="q_sb%d" % c) for c in range(CHUNKS)]
+        nc.sync.dma_start(out=q_sb[0][:], in_=q_rows[0:P, :])
+        v_sb = keep.tile([P, 2, 2 * HKV * D], BF16)
+        nc.sync.dma_start(out=v_sb[:], in_=v.rearrange("b (u p e) g d -> p (b u) (e g d)", u=2, e=2))
+        w_sb = [keep.tile([P, HIDDEN], BF16, name="w_sb%d" % nt) for nt in range(HIDDEN // P)]
+        for nb in range(N_BLOCKS):
+            for nt in range(4 * nb, 4 * nb + 4):
+                nc.sync.dma_start(out=w_sb[nt][:], in_=w_o[nt * P : (nt + 1) * P, :])
+            if nb + 1 < CHUNKS:
+                nc.sync.dma_start(out=q_sb[nb + 1][:], in_=q_rows[(nb + 1) * P : (nb + 2) * P, :])
+
+        kT = keep.tile([P, HKV, S], BF16)
+        qT = keep.tile([P, CHUNKS, H, P], BF16)
+        v_codes = keep.tile([P, HKV * D], U32, align_bytes=64)
+        v_scales = keep.tile([P, HKV * D], U8, align_bytes=64)
+        w_codes = keep.tile([P, PASSES, HIDDEN], U32, align_bytes=64)
+        w_scales = keep.tile([P, PASSES, HIDDEN], U8, align_bytes=64)
+        turned_q, scores_of, shift_of, rowsum_of, turned_e, e_grouped_of, e_operand = {}, {}, {}, {}, {}, {}, {}
+        pv_of, o_sb_of, turned_o, o_grouped_of, o_operand = {}, {}, {}, {}, {}
+        turned_w, w_grouped_of, acc_of = {}, {}, {}
+
+        def out_of_psum(index):
+            return nc.vector.tensor_copy if index % 2 == 0 else nc.scalar.copy
+
+        def turn_q(piece):
+            c, half = divmod(piece, 2)
+            turned_q[piece] = psum.tile([P, H // 2, P], BF16, tag="bank", name="turned_q")
+            for j in range(H // 2):
+                h = half * (H // 2) + j
+                nc.tensor.transpose(
+                    out=turned_q[piece][:, j, :], in_=q_sb[c][:, h * D : (h + 1) * D], identity=ident_bf[:]
+                )
+
+        def copy_q(piece):
+            c, half = divmod(piece, 2)
+            out_of_psum(piece)(out=qT[:, c, half * (H // 2) : (half + 1) * (H // 2), :], in_=turned_q[piece][:])
+
+        def score(unit):
+            c, h = divmod(unit, H)
+            n_keys = (c + 1) * P
+            scores = psum.tile([P, n_keys], F32, tag="bank")
+            nc.tensor.matmul(
+                out=scores[:], lhsT=qT[:, c, h, :], rhs=kT[:, h // REP, 0:n_keys], start=True, stop=False
+            )
+            nc.tensor.matmul(out=scores[:, c * P : n_keys], lhsT=ident_bf[:], rhs=mask_bf[:], start=False, stop=True)
+            scores_of[unit] = scores
+
+        def row_maximum(unit):
+            rowmax = stats.tile([P, 1], F32)
+            nc.vector.tensor_reduce(out=rowmax[:], in_=scores_of[unit][:], axis=AXIS.X, op=ALU.max)
+            shift = stats.tile([P, 1], F32)
+            nc.vector.tensor_scalar_mul(out=shift[:], in0=rowmax[:], scalar1=-SCALE)
+            shift_of[unit] = shift
+
+        def exponential(unit):
+            step, hh = divmod(unit, REP)
+            n_keys = (unit // H + 1) * P
+            if hh == 0:
+                rowsum_of[step] = stats.tile([P, REP], F32, name="rowsum")
+            nc.scalar.activation(
+                out=e_tiles[step % 2][:, hh * S : hh * S + n_keys],
+                in_=scores_of[unit][:],
+                func=ACT.Exp,
+                bias=shift_of[unit][:],
+                scale=SCALE,
+                accum_out=rowsum_of[step][:, hh : hh + 1],
+            )
+
+        def turn_e(unit):
+            pair, j = divmod(unit, 2)
+            step, hh = divmod(unit, REP)
+            if j == 0:
+                turned_e[pair] = psum.tile([P, 2, 2, P], F32, tag="bank", name="turned_e")
+            e_words = e_tiles[step % 2][:].bitcast(F32)
+            for u in range(2):
+                first = (hh * 2 + u) * P
+                nc.tensor.transpose(
+                    out=turned_e[pair][:, j, u, :], in_=e_words[:, first : first + P], identity=ident_f32[:]
+                )
+
+        def copy_e(pair):
+            step, half = divmod(pair, 2)
+            if half == 0:
+                e_grouped_of[step] = stage.tile([P, REP * P * PACK], BF16, align_bytes=64, name="e_grouped")
+            words = e_grouped_of[step][:].bitcast(F32).rearrange("p (h i u) -> p h i u", h=REP, u=2)
+            nc.scalar.copy(
+                out=words[:, 2 * half : 2 * half + 2, :, :], in_=turned_e[pair][:].rearrange("p h u i -> p h i u")
+            )
+
+        def quantise_e(step):
+            e_codes = stage.tile([P, REP * P], U32, align_bytes=64)
+            e_scales = stage.tile([P, REP * P], U8, align_bytes=64)
+            nc.vector.quantize_mx(out=e_codes[:].bitcast(FP8X4), scales=e_scales[:], in_=e_grouped_of[step][:])
+            e_operand[step] = (e_codes, e_scales)
+
+        def multiply_v(step):
+            g = step % HKV
+            e_codes, e_scales = e_operand[step]
+            pv = psum.tile([P, REP, D], F32, tag="bank")
+            for hh in range(REP):
+                queries = slice(hh * P, (hh + 1) * P)
+                nc.tensor.matmul_mx(
+                    out=pv[:, hh, :],
+                    lhsT=e_codes[:, queries].bitcast(FP8X4),
+                    lhsT_scale=e_scales[:, queries],
+                    rhs=v_codes[:, g * D : (g + 1) * D].bitcast(FP8X4),
+                    rhs_scale=v_scales[:, g * D : (g + 1) * D],
+                    start=True,
+                    stop=True,
+                )
+            pv_of[step] = pv
+
+        def normalise(step):
+            rinv = stats.tile([P, REP], F32)
+            nc.vector.reciprocal(out=rinv[:], in_=rowsum_of[step][:])
+            o_sb = stage.tile([P, REP * D], BF16)
+            nc.vector.tensor_tensor(
+                out=o_sb[:].rearrange("p (h d) -> p h d", h=REP),
+                in0=pv_of[step][:],
+                in1=rinv[:].unsqueeze(2).to_broadcast([P, REP, D]),
+                op=ALU.mult,
+            )
+            o_sb_of[step] = o_sb
+
+        def turn_o(step):
+            o_words = o_sb_of[step][:].bitcast(F32)
+            turned = psum.tile([P, 2, P], F32, tag="bank")
+            for u in range(2):
+                nc.tensor.transpose(out=turned[:, u, :], in_=o_words[:, u * P : (u + 1) * P], identity=ident_f32[:])
+            turned_o[step] = turned
+
+        def copy_o(step):
+            c, g = divmod(step, HKV)
+            if g == 0:
+                o_grouped_of[c] = stage.tile([P, PASSES * P * PACK], BF16, align_bytes=64, name="o_grouped")
+            words = o_grouped_of[c][:].bitcast(F32).rearrange("p (g i u) -> p g i u", g=PASSES, u=2)
+            nc.scalar.copy(out=words[:, g, :, :], in_=turned_o[step][:].rearrange("p u i -> p i u"))
+
+        def quantise_o(c):
+            o_codes = keep.tile([P, PASSES * P], U32, name="o_codes%d" % c, align_bytes=64)
+            o_scales = keep.tile([P, PASSES * P], U8, name="o_scales%d" % c, align_bytes=64)
+            nc.vector.quantize_mx(out=o_codes[:].bitcast(FP8X4), scales=o_scales[:], in_=o_grouped_of[c][:])
+            o_operand[c] = (o_codes, o_scales)
+
+        def quantise_v(piece):
+            v_grouped = keep.tile([P, HKV * D * PACK], BF16, align_bytes=64)
+            nc.vector.tensor_copy(
+                out=v_grouped[:].rearrange("p (c t) -> p c t", t=PACK),
+                in_=v_sb[:].rearrange("p u (e c) -> p c (u e)", e=2),
+            )
+            nc.vector.quantize_mx(out=v_codes[:].bitcast(FP8X4), scales=v_scales[:], in_=v_grouped[:])
+
+        def turn_w(piece):
+            block, half = divmod(piece, 2)
+            nb, g = divmod(block, PASSES)
+            turned = psum.tile([P, 2, 2, P], F32, tag="bank")
+            for j in range(2):
+                words = w_sb[4 * nb + 2 * half + j][:].bitcast(F32)
+                for u in range(2):
+                    first = (2 * g + u) * P
+                    nc.tensor.transpose(
+                        out=turned[:, j, u, :], in_=words[:, first : first + P], identity=ident_f32[:]
+                    )
+            turned_w[piece] = turned
+
+        def copy_w(piece):
+            block, half = divmod(piece, 2)
+            if half == 0:
+                w_grouped_of[block] = stage.tile([P, BANK * PACK], BF16, align_bytes=64, name="w_grouped")
+            words = w_grouped_of[block][:].bitcast(F32).rearrange("p (r n u) -> p r n u", r=4, u=2)
+            out_of_psum(piece)(
+                out=words[:, 2 * half : 2 * half + 2, :, :], in_=turned_w[piece][:].rearrange("p r u n -> p r n u")
+            )
+
+        def quantise_w(block):
+            nb, g = divmod(block, PASSES)
+            features = slice(nb * BANK, (nb + 1) * BANK)
+            nc.vector.quantize_mx(
+                out=w_codes[:, g, features].bitcast(FP8X4),
+                scales=w_scales[:, g, features],
+                in_=w_grouped_of[block][:],
+            )
+
+        def project(block):
+            c, nb = divmod(block, N_BLOCKS)
+            o_codes, o_scales = o_operand[c]
+            features = slice(nb * BANK, (nb + 1) * BANK)
+            acc = psum.tile([P, BANK], F32, tag="bank")
+            for g in range(PASSES):
+                queries = slice(g * P, (g + 1) * P)
+                nc.tensor.matmul_mx(
+                    out=acc[:],
+                    lhsT=o_codes[:, queries].bitcast(FP8X4),
+                    lhsT_scale=o_scales[:, queries],
+                    rhs=w_codes[:, g, features].bitcast(FP8X4),
+                    rhs_scale=w_scales[:, g, features],
+                    start=(g == 0),
+                    stop=(g == PASSES - 1),
+                )
+            acc_of[block] = acc
+
+        def store(block):
+            c, nb = divmod(block, N_BLOCKS)
+            result = results.tile([P, BANK], F32)
+            out_of_psum(block)(out=result[:], in_=acc_of[block][:])
+            nc.sync.dma_start(out=out_rows[c * P : (c + 1) * P, nb * BANK : (nb + 1) * BANK], in_=result[:])
+
+        for half in range(2):
+            turned_k = psum.tile([P, 2, CHUNKS, P], BF16, tag="bank")
+            for j in range(2):
+                g = 2 * half + j
+                for t in range(CHUNKS):
+                    nc.tensor.transpose(
+                        out=turned_k[:, j, t, :], in_=k_sb[:, t, g * D : (g + 1) * D], identity=ident_bf[:]
+                    )
+            out_of_psum(half)(
+                out=kT[:, 2 * half : 2 * half + 2, :], in_=turned_k[:].rearrange("p g t j -> p g (t j)")
+            )
+        for tick in range(TURN_Q_AT, TICKS):
+            run_if_due(row_maximum, tick, MAX_AT, 1, UNITS)
+            run_if_due(exponential, tick, EXP_AT, 1, UNITS)
+            run_if_due(copy_e, tick, COPY_E_AT, 2, UNITS // 2)
+            run_if_due(normalise, tick, NORMALISE_AT, 4, STEPS)
+            run_if_due(copy_o, tick, COPY_O_AT, 4, STEPS)
+            run_if_due(copy_w, tick, COPY_W_AT, 1, 2 * W_BLOCKS)
+            run_if_due(copy_q, tick, COPY_Q_AT, 8, UNITS // 8)
+            run_if_due(store, tick, STORE_AT, PROJECT_EVERY, OUT_BLOCKS)
+            run_if_due(quantise_e, tick, QUANTISE_E_AT, 4, STEPS)
+            run_if_due(quantise_o, tick, QUANTISE_O_AT, 16, CHUNKS)
+            run_if_due(quantise_w, tick, QUANTISE_W_AT, 2, W_BLOCKS)
+            run_if_due(quantise_v, tick, QUANTISE_V_AT, 1, 1)
+            run_if_due(turn_e, tick, TURN_E_AT, 1, UNITS)
+            run_if_due(turn_o, tick, TURN_O_AT, 4, STEPS)
+            run_if_due(turn_w, tick, TURN_W_AT, 1, 2 * W_BLOCKS)
+            run_if_due(turn_q, tick, TURN_Q_AT, 8, UNITS // 8)
+            run_if_due(score, tick, SCORE_AT, 1, UNITS)
+            run_if_due(multiply_v, tick, MULTIPLY_V_AT, 4, STEPS)
+            run_if_due(project, tick, PROJECT_AT, PROJECT_EVERY, OUT_BLOCKS)

@@ -35,7 +35,9 @@ MASK_NEG = -2.3819763e38
 SCORE_AT = 0
 MAX_AT = SCORE_AT + 1
 EXP_AT = MAX_AT + 1
+RECIPROCAL_AT = EXP_AT + REP
 TURN_E_AT = EXP_AT + 1
+CLEAR_E_AT = TURN_E_AT + REP
 COPY_E_AT = TURN_E_AT + 2
 QUANTISE_E_AT = COPY_E_AT + 3
 MULTIPLY_V_AT = QUANTISE_E_AT + 1
@@ -77,8 +79,6 @@ def tile_gemmaattention_pb_kernel(tc, q_rot, k_rot, v, w_o, out):
         psum = ctx.enter_context(tc.psum_pool(name="psum", bufs=8))
 
         e_tiles = [keep.tile([P, REP * S], BF16, name="e_sb%d" % b) for b in range(2)]
-        for e_sb in e_tiles:
-            nc.vector.memset(e_sb[:], 0.0)
 
         ident_bf = keep.tile([P, P], BF16)
         make_identity(nc, ident_bf[:])
@@ -101,15 +101,16 @@ def tile_gemmaattention_pb_kernel(tc, q_rot, k_rot, v, w_o, out):
         k_sb = keep.tile([P, CHUNKS, HKV * D], BF16)
         nc.sync.dma_start(out=k_sb[:], in_=k_rot.rearrange("b (t p) g d -> p (b t) (g d)", p=P))
         q_sb = [keep.tile([P, H * D], BF16, name="q_sb%d" % c) for c in range(CHUNKS)]
-        nc.sync.dma_start(out=q_sb[0][:], in_=q_rows[0:P, :])
+        nc.sync.dma_start(out=q_sb[CHUNKS - 1][:], in_=q_rows[(CHUNKS - 1) * P : CHUNKS * P, :])
         v_sb = keep.tile([P, 2, 2 * HKV * D], BF16)
         nc.sync.dma_start(out=v_sb[:], in_=v.rearrange("b (u p e) g d -> p (b u) (e g d)", u=2, e=2))
         w_sb = [keep.tile([P, HIDDEN], BF16, name="w_sb%d" % nt) for nt in range(HIDDEN // P)]
         for nb in range(N_BLOCKS):
             for nt in range(4 * nb, 4 * nb + 4):
                 nc.sync.dma_start(out=w_sb[nt][:], in_=w_o[nt * P : (nt + 1) * P, :])
-            if nb + 1 < CHUNKS:
-                nc.sync.dma_start(out=q_sb[nb + 1][:], in_=q_rows[(nb + 1) * P : (nb + 2) * P, :])
+            c = CHUNKS - 2 - nb
+            if c >= 0:
+                nc.sync.dma_start(out=q_sb[c][:], in_=q_rows[c * P : (c + 1) * P, :])
 
         kT = keep.tile([P, HKV, S], BF16)
         qT = keep.tile([P, CHUNKS, H, P], BF16)
@@ -118,14 +119,15 @@ def tile_gemmaattention_pb_kernel(tc, q_rot, k_rot, v, w_o, out):
         w_codes = keep.tile([P, PASSES, HIDDEN], U32, align_bytes=64)
         w_scales = keep.tile([P, PASSES, HIDDEN], U8, align_bytes=64)
         turned_q, scores_of, shift_of, rowsum_of, turned_e, e_grouped_of, e_operand = {}, {}, {}, {}, {}, {}, {}
-        pv_of, o_sb_of, turned_o, o_grouped_of, o_operand = {}, {}, {}, {}, {}
+        rinv_of, pv_of, o_sb_of, turned_o, o_grouped_of, o_operand = {}, {}, {}, {}, {}, {}
         turned_w, w_grouped_of, acc_of = {}, {}, {}
 
         def out_of_psum(index):
             return nc.vector.tensor_copy if index % 2 == 0 else nc.scalar.copy
 
         def turn_q(piece):
-            c, half = divmod(piece, 2)
+            place, half = divmod(piece, 2)
+            c = CHUNKS - 1 - place
             turned_q[piece] = psum.tile([P, H // 2, P], BF16, tag="bank", name="turned_q")
             for j in range(H // 2):
                 h = half * (H // 2) + j
@@ -134,11 +136,13 @@ def tile_gemmaattention_pb_kernel(tc, q_rot, k_rot, v, w_o, out):
                 )
 
         def copy_q(piece):
-            c, half = divmod(piece, 2)
+            place, half = divmod(piece, 2)
+            c = CHUNKS - 1 - place
             out_of_psum(piece)(out=qT[:, c, half * (H // 2) : (half + 1) * (H // 2), :], in_=turned_q[piece][:])
 
         def score(unit):
-            c, h = divmod(unit, H)
+            place, h = divmod(unit, H)
+            c = CHUNKS - 1 - place
             n_keys = (c + 1) * P
             scores = psum.tile([P, n_keys], F32, tag="bank")
             nc.tensor.matmul(
@@ -151,12 +155,14 @@ def tile_gemmaattention_pb_kernel(tc, q_rot, k_rot, v, w_o, out):
             rowmax = stats.tile([P, 1], F32)
             nc.vector.tensor_reduce(out=rowmax[:], in_=scores_of[unit][:], axis=AXIS.X, op=ALU.max)
             shift = stats.tile([P, 1], F32)
-            nc.vector.tensor_scalar_mul(out=shift[:], in0=rowmax[:], scalar1=-SCALE)
+            nc.gpsimd.tensor_scalar(
+                out=shift[:], in0=rowmax[:], scalar1=-SCALE, scalar2=0.0, op0=ALU.mult, op1=ALU.add
+            )
             shift_of[unit] = shift
 
         def exponential(unit):
             step, hh = divmod(unit, REP)
-            n_keys = (unit // H + 1) * P
+            n_keys = (CHUNKS - unit // H) * P
             if hh == 0:
                 rowsum_of[step] = stats.tile([P, REP], F32, name="rowsum")
             nc.scalar.activation(
@@ -167,6 +173,18 @@ def tile_gemmaattention_pb_kernel(tc, q_rot, k_rot, v, w_o, out):
                 scale=SCALE,
                 accum_out=rowsum_of[step][:, hh : hh + 1],
             )
+
+        def reciprocal(step):
+            rinv = stats.tile([P, REP], F32)
+            nc.vector.reciprocal(out=rinv[:], in_=rowsum_of[step][:])
+            rinv_of[step] = rinv
+
+        def clear_e(step):
+            place, g = divmod(step, HKV)
+            c = CHUNKS - 1 - place
+            if g >= HKV - 2 and c > 0:
+                e_heads = e_tiles[step % 2][:].rearrange("p (h k) -> p h k", h=REP)
+                nc.gpsimd.memset(e_heads[:, :, c * P : (c + 1) * P], 0.0)
 
         def turn_e(unit):
             pair, j = divmod(unit, 2)
@@ -213,13 +231,11 @@ def tile_gemmaattention_pb_kernel(tc, q_rot, k_rot, v, w_o, out):
             pv_of[step] = pv
 
         def normalise(step):
-            rinv = stats.tile([P, REP], F32)
-            nc.vector.reciprocal(out=rinv[:], in_=rowsum_of[step][:])
             o_sb = stage.tile([P, REP * D], BF16)
             nc.vector.tensor_tensor(
                 out=o_sb[:].rearrange("p (h d) -> p h d", h=REP),
                 in0=pv_of[step][:],
-                in1=rinv[:].unsqueeze(2).to_broadcast([P, REP, D]),
+                in1=rinv_of[step][:].unsqueeze(2).to_broadcast([P, REP, D]),
                 op=ALU.mult,
             )
             o_sb_of[step] = o_sb
@@ -232,17 +248,17 @@ def tile_gemmaattention_pb_kernel(tc, q_rot, k_rot, v, w_o, out):
             turned_o[step] = turned
 
         def copy_o(step):
-            c, g = divmod(step, HKV)
+            place, g = divmod(step, HKV)
             if g == 0:
-                o_grouped_of[c] = stage.tile([P, PASSES * P * PACK], BF16, align_bytes=64, name="o_grouped")
-            words = o_grouped_of[c][:].bitcast(F32).rearrange("p (g i u) -> p g i u", g=PASSES, u=2)
+                o_grouped_of[place] = stage.tile([P, PASSES * P * PACK], BF16, align_bytes=64, name="o_grouped")
+            words = o_grouped_of[place][:].bitcast(F32).rearrange("p (g i u) -> p g i u", g=PASSES, u=2)
             nc.scalar.copy(out=words[:, g, :, :], in_=turned_o[step][:].rearrange("p u i -> p i u"))
 
-        def quantise_o(c):
-            o_codes = keep.tile([P, PASSES * P], U32, name="o_codes%d" % c, align_bytes=64)
-            o_scales = keep.tile([P, PASSES * P], U8, name="o_scales%d" % c, align_bytes=64)
-            nc.vector.quantize_mx(out=o_codes[:].bitcast(FP8X4), scales=o_scales[:], in_=o_grouped_of[c][:])
-            o_operand[c] = (o_codes, o_scales)
+        def quantise_o(place):
+            o_codes = keep.tile([P, PASSES * P], U32, name="o_codes%d" % place, align_bytes=64)
+            o_scales = keep.tile([P, PASSES * P], U8, name="o_scales%d" % place, align_bytes=64)
+            nc.vector.quantize_mx(out=o_codes[:].bitcast(FP8X4), scales=o_scales[:], in_=o_grouped_of[place][:])
+            o_operand[place] = (o_codes, o_scales)
 
         def quantise_v(piece):
             v_grouped = keep.tile([P, HKV * D * PACK], BF16, align_bytes=64)
@@ -270,9 +286,8 @@ def tile_gemmaattention_pb_kernel(tc, q_rot, k_rot, v, w_o, out):
             if half == 0:
                 w_grouped_of[block] = stage.tile([P, BANK * PACK], BF16, align_bytes=64, name="w_grouped")
             words = w_grouped_of[block][:].bitcast(F32).rearrange("p (r n u) -> p r n u", r=4, u=2)
-            out_of_psum(piece)(
-                out=words[:, 2 * half : 2 * half + 2, :, :], in_=turned_w[piece][:].rearrange("p r u n -> p r n u")
-            )
+            copy = nc.vector.tensor_copy if piece % 3 == 0 else nc.scalar.copy
+            copy(out=words[:, 2 * half : 2 * half + 2, :, :], in_=turned_w[piece][:].rearrange("p r u n -> p r n u"))
 
         def quantise_w(block):
             nb, g = divmod(block, PASSES)
@@ -284,8 +299,8 @@ def tile_gemmaattention_pb_kernel(tc, q_rot, k_rot, v, w_o, out):
             )
 
         def project(block):
-            c, nb = divmod(block, N_BLOCKS)
-            o_codes, o_scales = o_operand[c]
+            place, nb = divmod(block, N_BLOCKS)
+            o_codes, o_scales = o_operand[place]
             features = slice(nb * BANK, (nb + 1) * BANK)
             acc = psum.tile([P, BANK], F32, tag="bank")
             for g in range(PASSES):
@@ -302,9 +317,10 @@ def tile_gemmaattention_pb_kernel(tc, q_rot, k_rot, v, w_o, out):
             acc_of[block] = acc
 
         def store(block):
-            c, nb = divmod(block, N_BLOCKS)
+            place, nb = divmod(block, N_BLOCKS)
+            c = CHUNKS - 1 - place
             result = results.tile([P, BANK], F32)
-            out_of_psum(block)(out=result[:], in_=acc_of[block][:])
+            nc.vector.tensor_copy(out=result[:], in_=acc_of[block][:])
             nc.sync.dma_start(out=out_rows[c * P : (c + 1) * P, nb * BANK : (nb + 1) * BANK], in_=result[:])
 
         for half in range(2):
@@ -321,6 +337,8 @@ def tile_gemmaattention_pb_kernel(tc, q_rot, k_rot, v, w_o, out):
         for tick in range(TURN_Q_AT, TICKS):
             run_if_due(row_maximum, tick, MAX_AT, 1, UNITS)
             run_if_due(exponential, tick, EXP_AT, 1, UNITS)
+            run_if_due(reciprocal, tick, RECIPROCAL_AT, 4, STEPS)
+            run_if_due(clear_e, tick, CLEAR_E_AT, 4, STEPS)
             run_if_due(copy_e, tick, COPY_E_AT, 2, UNITS // 2)
             run_if_due(normalise, tick, NORMALISE_AT, 4, STEPS)
             run_if_due(copy_o, tick, COPY_O_AT, 4, STEPS)

@@ -28,7 +28,7 @@ PASSES = HIDDEN // K_PASS
 UNITS = CHUNKS * H
 STEPS = CHUNKS * HKV
 OUT_BLOCKS = CHUNKS * N_BLOCKS
-W_BLOCKS = N_BLOCKS * PASSES
+W_PIECES = 2 * N_BLOCKS * PASSES
 SCALE = D**-0.5
 MASK_NEG = -2.3819763e38
 
@@ -47,13 +47,15 @@ COPY_O_AT = TURN_O_AT + 1
 QUANTISE_O_AT = COPY_O_AT + 4 * (HKV - 1) + 1
 TURN_Q_AT = SCORE_AT - 6
 COPY_Q_AT = TURN_Q_AT + 1
+TURN_K_AT = TURN_Q_AT - 1
+COPY_K_AT = TURN_K_AT + 1
 QUANTISE_V_AT = SCORE_AT
 TURN_W_AT = 4
 COPY_W_AT = TURN_W_AT + 1
 QUANTISE_W_AT = COPY_W_AT + 2
-PROJECT_AT = QUANTISE_W_AT + 2 * (W_BLOCKS - 1) + 1
-PROJECT_EVERY = 3
-STORE_AT = PROJECT_AT + 1
+PROJECT_AT = QUANTISE_O_AT + 4
+PROJECT_EVERY = 4
+STORE_AT = PROJECT_AT + 2
 TICKS = STORE_AT + PROJECT_EVERY * (OUT_BLOCKS - 1) + 1
 
 FLOPS = 2 * H * S * S * D * 2 + 2 * S * HIDDEN * HIDDEN
@@ -118,12 +120,26 @@ def tile_gemmaattention_pb_kernel(tc, q_rot, k_rot, v, w_o, out):
         v_scales = keep.tile([P, HKV * D], U8, align_bytes=64)
         w_codes = keep.tile([P, PASSES, HIDDEN], U32, align_bytes=64)
         w_scales = keep.tile([P, PASSES, HIDDEN], U8, align_bytes=64)
-        turned_q, scores_of, shift_of, rowsum_of, turned_e, e_grouped_of, e_operand = {}, {}, {}, {}, {}, {}, {}
+        turned_k, turned_q, scores_of, shift_of, rowsum_of, turned_e, e_grouped_of, e_operand = {}, {}, {}, {}, {}, {}, {}, {}
         rinv_of, pv_of, o_sb_of, turned_o, o_grouped_of, o_operand = {}, {}, {}, {}, {}, {}
         turned_w, w_grouped_of, acc_of = {}, {}, {}
 
         def out_of_psum(index):
             return nc.vector.tensor_copy if index % 2 == 0 else nc.scalar.copy
+
+        def turn_k(piece):
+            turned_k[piece] = psum.tile([P, 2, CHUNKS, P], BF16, tag="bank", name="turned_k")
+            for j in range(2):
+                g = 2 * piece + j
+                for t in range(CHUNKS):
+                    nc.tensor.transpose(
+                        out=turned_k[piece][:, j, t, :], in_=k_sb[:, t, g * D : (g + 1) * D], identity=ident_bf[:]
+                    )
+
+        def copy_k(piece):
+            out_of_psum(piece)(
+                out=kT[:, 2 * piece : 2 * piece + 2, :], in_=turned_k[piece][:].rearrange("p g t j -> p g (t j)")
+            )
 
         def turn_q(piece):
             place, half = divmod(piece, 2)
@@ -269,8 +285,8 @@ def tile_gemmaattention_pb_kernel(tc, q_rot, k_rot, v, w_o, out):
             nc.vector.quantize_mx(out=v_codes[:].bitcast(FP8X4), scales=v_scales[:], in_=v_grouped[:])
 
         def turn_w(piece):
-            block, half = divmod(piece, 2)
-            nb, g = divmod(block, PASSES)
+            nb, rest = divmod(piece, 2 * PASSES)
+            g, half = divmod(rest, 2)
             turned = psum.tile([P, 2, 2, P], F32, tag="bank")
             for j in range(2):
                 words = w_sb[4 * nb + 2 * half + j][:].bitcast(F32)
@@ -282,20 +298,19 @@ def tile_gemmaattention_pb_kernel(tc, q_rot, k_rot, v, w_o, out):
             turned_w[piece] = turned
 
         def copy_w(piece):
-            block, half = divmod(piece, 2)
-            if half == 0:
-                w_grouped_of[block] = stage.tile([P, BANK * PACK], BF16, align_bytes=64, name="w_grouped")
-            words = w_grouped_of[block][:].bitcast(F32).rearrange("p (r n u) -> p r n u", r=4, u=2)
-            copy = nc.vector.tensor_copy if piece % 3 == 0 else nc.scalar.copy
-            copy(out=words[:, 2 * half : 2 * half + 2, :, :], in_=turned_w[piece][:].rearrange("p r u n -> p r n u"))
+            w_grouped = stage.tile([P, 2 * P * PACK], BF16, align_bytes=64, bufs=4)
+            words = w_grouped[:].bitcast(F32).rearrange("p (r n u) -> p r n u", r=2, u=2)
+            out_of_psum(piece)(out=words, in_=turned_w[piece][:].rearrange("p r u n -> p r n u"))
+            w_grouped_of[piece] = w_grouped
 
-        def quantise_w(block):
-            nb, g = divmod(block, PASSES)
-            features = slice(nb * BANK, (nb + 1) * BANK)
+        def quantise_w(piece):
+            nb, rest = divmod(piece, 2 * PASSES)
+            g, half = divmod(rest, 2)
+            features = slice(nb * BANK + half * 2 * P, nb * BANK + (half + 1) * 2 * P)
             nc.vector.quantize_mx(
                 out=w_codes[:, g, features].bitcast(FP8X4),
                 scales=w_scales[:, g, features],
-                in_=w_grouped_of[block][:],
+                in_=w_grouped_of[piece][:],
             )
 
         def project(block):
@@ -323,35 +338,26 @@ def tile_gemmaattention_pb_kernel(tc, q_rot, k_rot, v, w_o, out):
             nc.vector.tensor_copy(out=result[:], in_=acc_of[block][:])
             nc.sync.dma_start(out=out_rows[c * P : (c + 1) * P, nb * BANK : (nb + 1) * BANK], in_=result[:])
 
-        for half in range(2):
-            turned_k = psum.tile([P, 2, CHUNKS, P], BF16, tag="bank")
-            for j in range(2):
-                g = 2 * half + j
-                for t in range(CHUNKS):
-                    nc.tensor.transpose(
-                        out=turned_k[:, j, t, :], in_=k_sb[:, t, g * D : (g + 1) * D], identity=ident_bf[:]
-                    )
-            out_of_psum(half)(
-                out=kT[:, 2 * half : 2 * half + 2, :], in_=turned_k[:].rearrange("p g t j -> p g (t j)")
-            )
-        for tick in range(TURN_Q_AT, TICKS):
+        for tick in range(TURN_K_AT, TICKS):
             run_if_due(row_maximum, tick, MAX_AT, 1, UNITS)
-            run_if_due(exponential, tick, EXP_AT, 1, UNITS)
             run_if_due(reciprocal, tick, RECIPROCAL_AT, 4, STEPS)
             run_if_due(clear_e, tick, CLEAR_E_AT, 4, STEPS)
             run_if_due(copy_e, tick, COPY_E_AT, 2, UNITS // 2)
             run_if_due(normalise, tick, NORMALISE_AT, 4, STEPS)
             run_if_due(copy_o, tick, COPY_O_AT, 4, STEPS)
-            run_if_due(copy_w, tick, COPY_W_AT, 1, 2 * W_BLOCKS)
+            run_if_due(copy_w, tick, COPY_W_AT, 1, W_PIECES)
+            run_if_due(copy_k, tick, COPY_K_AT, 8, HKV // 2)
             run_if_due(copy_q, tick, COPY_Q_AT, 8, UNITS // 8)
             run_if_due(store, tick, STORE_AT, PROJECT_EVERY, OUT_BLOCKS)
+            run_if_due(exponential, tick, EXP_AT, 1, UNITS)
             run_if_due(quantise_e, tick, QUANTISE_E_AT, 4, STEPS)
             run_if_due(quantise_o, tick, QUANTISE_O_AT, 16, CHUNKS)
-            run_if_due(quantise_w, tick, QUANTISE_W_AT, 2, W_BLOCKS)
+            run_if_due(quantise_w, tick, QUANTISE_W_AT, 1, W_PIECES)
             run_if_due(quantise_v, tick, QUANTISE_V_AT, 1, 1)
             run_if_due(turn_e, tick, TURN_E_AT, 1, UNITS)
             run_if_due(turn_o, tick, TURN_O_AT, 4, STEPS)
-            run_if_due(turn_w, tick, TURN_W_AT, 1, 2 * W_BLOCKS)
+            run_if_due(turn_w, tick, TURN_W_AT, 1, W_PIECES)
+            run_if_due(turn_k, tick, TURN_K_AT, 8, HKV // 2)
             run_if_due(turn_q, tick, TURN_Q_AT, 8, UNITS // 8)
             run_if_due(score, tick, SCORE_AT, 1, UNITS)
             run_if_due(multiply_v, tick, MULTIPLY_V_AT, 4, STEPS)

@@ -32,31 +32,34 @@ W_PIECES = 2 * N_BLOCKS * PASSES
 SCALE = D**-0.5
 MASK_NEG = -2.3819763e38
 
+FROM_PSUM = 1
+FROM_SBUF = 3
 SCORE_AT = 0
-MAX_AT = SCORE_AT + 1
+MAX_AT = SCORE_AT + FROM_PSUM
 EXP_AT = MAX_AT + 1
 RECIPROCAL_AT = EXP_AT + REP
-TURN_E_AT = EXP_AT + 1
+TURN_E_AT = EXP_AT + FROM_SBUF
 CLEAR_E_AT = TURN_E_AT + REP
-COPY_E_AT = TURN_E_AT + 2
-QUANTISE_E_AT = COPY_E_AT + 3
-MULTIPLY_V_AT = QUANTISE_E_AT + 1
-NORMALISE_AT = MULTIPLY_V_AT + 1
-TURN_O_AT = NORMALISE_AT + 1
-COPY_O_AT = TURN_O_AT + 1
-QUANTISE_O_AT = COPY_O_AT + 4 * (HKV - 1) + 1
+COPY_E_AT = TURN_E_AT + 1 + FROM_PSUM
+QUANTISE_E_AT = COPY_E_AT + 2 + FROM_SBUF
+MULTIPLY_V_AT = QUANTISE_E_AT + FROM_SBUF
+NORMALISE_AT = MULTIPLY_V_AT + FROM_PSUM
+TURN_O_AT = NORMALISE_AT + FROM_SBUF
+COPY_O_AT = TURN_O_AT + FROM_PSUM
+QUANTISE_O_AT = COPY_O_AT + 4 * (HKV - 1) + FROM_SBUF
 TURN_Q_AT = SCORE_AT - 6
-COPY_Q_AT = TURN_Q_AT + 1
+COPY_Q_AT = TURN_Q_AT + FROM_PSUM
 TURN_K_AT = TURN_Q_AT - 1
-COPY_K_AT = TURN_K_AT + 1
+COPY_K_AT = TURN_K_AT + FROM_PSUM
 QUANTISE_V_AT = SCORE_AT
 TURN_W_AT = 4
-COPY_W_AT = TURN_W_AT + 1
-QUANTISE_W_AT = COPY_W_AT + 2
-PROJECT_AT = QUANTISE_O_AT + 4
+COPY_W_AT = TURN_W_AT + FROM_PSUM
+QUANTISE_W_AT = COPY_W_AT + FROM_SBUF
 PROJECT_EVERY = 4
+PROJECT_AT = MULTIPLY_V_AT + PROJECT_EVERY * ((QUANTISE_O_AT - MULTIPLY_V_AT) // PROJECT_EVERY + 1)
 STORE_AT = PROJECT_AT + 2
 TICKS = STORE_AT + PROJECT_EVERY * (OUT_BLOCKS - 1) + 1
+assert PROJECT_AT > QUANTISE_W_AT + 7
 
 FLOPS = 2 * H * S * S * D * 2 + 2 * S * HIDDEN * HIDDEN
 
@@ -298,7 +301,7 @@ def tile_gemmaattention_pb_kernel(tc, q_rot, k_rot, v, w_o, out):
             turned_w[piece] = turned
 
         def copy_w(piece):
-            w_grouped = stage.tile([P, 2 * P * PACK], BF16, align_bytes=64, bufs=4)
+            w_grouped = stage.tile([P, 2 * P * PACK], BF16, align_bytes=64, bufs=FROM_SBUF + 2)
             words = w_grouped[:].bitcast(F32).rearrange("p (r n u) -> p r n u", r=2, u=2)
             out_of_psum(piece)(out=words, in_=turned_w[piece][:].rearrange("p r u n -> p r n u"))
             w_grouped_of[piece] = w_grouped

@@ -25,49 +25,103 @@ BANK = 512
 CHUNKS = S // P
 N_BLOCKS = HIDDEN // BANK
 PASSES = HIDDEN // K_PASS
-UNITS = CHUNKS * H
-STEPS = CHUNKS * HKV
+ROWS = 64
+RB = S // ROWS
+UNITS = 8 * RB
+QUAD = 4
+STEPS = UNITS // QUAD
 OUT_BLOCKS = CHUNKS * N_BLOCKS
 W_PIECES = 2 * N_BLOCKS * PASSES
 SCALE = D**-0.5
 MASK_NEG = -2.3819763e38
 
+ORDER = [7, 6, 5, 4, 3, 2, 1, 0]
+HALF_TICKS = [1, 1, 1, 1, 2, 2, 2, 2]
+PER = [4, 4, 2, 2, 1, 1, 1, 1]
+LOW = 4
 FROM_PSUM = 1
-FROM_SBUF = 3
-SCORE_AT = 0
-MAX_AT = SCORE_AT + FROM_PSUM
-EXP_AT = MAX_AT + 1
-RECIPROCAL_AT = EXP_AT + REP
-TURN_E_AT = EXP_AT + FROM_SBUF
-CLEAR_E_AT = TURN_E_AT + REP
-COPY_E_AT = TURN_E_AT + 1 + FROM_PSUM
-QUANTISE_E_AT = COPY_E_AT + 2 + FROM_SBUF
-MULTIPLY_V_AT = QUANTISE_E_AT + FROM_SBUF
+EXP_GAP = 1
+L_ET = 4
+L_EQ = 1
+L_QM = 3
+L_NT = 2
+L_OQ = 2
+L_WQ = 3
+TURN_Q_AHEAD = 5
+TURN_K_AT = [-7, -1]
+QUANTISE_V_AT = 0
+TURN_W_AT = 5
+PROJECT_GAP = 0
+STORE_LAG = 3
+O_LAG = 2
+W_NUM = 1
+W_DEN = 1
+P_GRID = 3
+P_GRID2 = 2
+P_SWITCH = 46
+E_BANKS = 2
+E_TILES = 4
+SKIP_UPPER = True
+ST_ALT = False
+W_V_DEN = 3
+W_V_OFF = 0
+Q_V = True
+
+
+def block_of(unit):
+    return ORDER[unit // 8]
+
+
+def unit_tick(unit):
+    place, rest = divmod(unit, 8)
+    return (sum(8 * HALF_TICKS[r] for r in ORDER[:place]) + rest * HALF_TICKS[ORDER[place]]) // 2
+
+
+def step_tick(step):
+    return unit_tick(QUAD * step + QUAD - 1)
+
+
+MAX_AT = FROM_PSUM
+EXP_AT = MAX_AT + EXP_GAP
+RECIPROCAL_AT = EXP_AT + 1
+TURN_E_AT = EXP_AT + L_ET
+COPY_E_AT = TURN_E_AT + FROM_PSUM
+QUANTISE_E_AT = COPY_E_AT + L_EQ
+MULTIPLY_V_AT = QUANTISE_E_AT + L_QM
 NORMALISE_AT = MULTIPLY_V_AT + FROM_PSUM
-TURN_O_AT = NORMALISE_AT + FROM_SBUF
+TURN_O_AT = NORMALISE_AT + L_NT
 COPY_O_AT = TURN_O_AT + FROM_PSUM
-QUANTISE_O_AT = COPY_O_AT + 4 * (HKV - 1) + FROM_SBUF
-TURN_Q_AT = SCORE_AT - 6
-COPY_Q_AT = TURN_Q_AT + FROM_PSUM
-TURN_K_AT = TURN_Q_AT - 1
-COPY_K_AT = TURN_K_AT + FROM_PSUM
-QUANTISE_V_AT = SCORE_AT
-TURN_W_AT = 4
+QUANTISE_O_AT = COPY_O_AT + L_OQ
 COPY_W_AT = TURN_W_AT + FROM_PSUM
-QUANTISE_W_AT = COPY_W_AT + FROM_SBUF
-PROJECT_EVERY = 4
-PROJECT_AT = MULTIPLY_V_AT + PROJECT_EVERY * ((QUANTISE_O_AT - MULTIPLY_V_AT) // PROJECT_EVERY + 1)
-STORE_AT = PROJECT_AT + 2
-TICKS = STORE_AT + PROJECT_EVERY * (OUT_BLOCKS - 1) + 1
-assert PROJECT_AT > QUANTISE_W_AT + 7
+QUANTISE_W_AT = COPY_W_AT + L_WQ
+
+
+def w_tick(piece):
+    return piece * W_NUM // W_DEN
+
+
+def o_ready(place, gp):
+    return QUANTISE_O_AT + step_tick(4 * place + 2 + gp)
+
+
+def w_ready(nb):
+    return QUANTISE_W_AT + w_tick(8 * nb + 7)
+
+
+def project_ticks():
+    ticks = {}
+    tick = -100
+    ready = {b: max(o_ready(b // N_BLOCKS, 1), w_ready(b % N_BLOCKS)) for b in range(OUT_BLOCKS - N_BLOCKS)}
+    for block in sorted(ready, key=lambda b: (ready[b], b)):
+        tick = max(tick + (P_GRID if tick < P_SWITCH else P_GRID2), ready[block] + PROJECT_GAP)
+        ticks[block] = tick
+    return ticks
+
+
+PROJECT_TICK = project_ticks()
+LAST_AT = MULTIPLY_V_AT + step_tick(STEPS - 1)
 
 FLOPS = 2 * H * S * S * D * 2 + 2 * S * HIDDEN * HIDDEN
-
-
-def run_if_due(stage_fn, tick, first, every, count):
-    piece, rest = divmod(tick - first, every)
-    if rest == 0 and 0 <= piece < count:
-        stage_fn(piece)
 
 
 def tile_gemmaattention_pb_kernel(tc, q_rot, k_rot, v, w_o, out):
@@ -78,170 +132,200 @@ def tile_gemmaattention_pb_kernel(tc, q_rot, k_rot, v, w_o, out):
     with ExitStack() as ctx:
         ctx.enter_context(tc.manual_schedule())
         keep = ctx.enter_context(tc.tile_pool(name="keep", bufs=1))
-        stage = ctx.enter_context(tc.tile_pool(name="stage", bufs=2))
-        stats = ctx.enter_context(tc.tile_pool(name="stats", bufs=4))
-        results = ctx.enter_context(tc.tile_pool(name="results", bufs=4))
-        psum = ctx.enter_context(tc.psum_pool(name="psum", bufs=8))
+        stage = ctx.enter_context(tc.tile_pool(name="stage", bufs=4))
+        stats = ctx.enter_context(tc.tile_pool(name="stats", bufs=8))
+        results = ctx.enter_context(tc.tile_pool(name="results", bufs=5))
+        psum = ctx.enter_context(tc.psum_pool(name="psum", bufs=1))
+        free_banks = [psum.tile([P, BANK], F32, name="bank%d" % b) for b in range(8)]
+        bank_of = {}
+        e_banks = []
 
-        e_tiles = [keep.tile([P, REP * S], BF16, name="e_sb%d" % b) for b in range(2)]
+        def take(owner):
+            bank_of[owner] = free_banks.pop(0)
+            return bank_of[owner][:]
 
+        def give(owner):
+            free_banks.append(bank_of.pop(owner))
+
+        e_tiles = [keep.tile([P, QUAD * S], BF16, name="e_sb%d" % b) for b in range(E_TILES)]
         ident_bf = keep.tile([P, P], BF16)
         make_identity(nc, ident_bf[:])
-        ident_f32 = keep.tile([P, P], F32)
-        make_identity(nc, ident_f32[:])
         mask_f32 = keep.tile([P, P], F32)
         nc.gpsimd.memset(mask_f32[:], 0.0)
-        nc.gpsimd.affine_select(
-            out=mask_f32[:],
-            in_=mask_f32[:],
-            compare_op=ALU.is_ge,
-            fill=MASK_NEG,
-            base=0,
-            pattern=[[-1, P]],
-            channel_multiplier=1,
-        )
-        mask_bf = keep.tile([P, P], BF16)
-        nc.vector.tensor_copy(out=mask_bf[:], in_=mask_f32[:])
+        nc.gpsimd.affine_select(out=mask_f32[:], in_=mask_f32[:], compare_op=ALU.is_ge, fill=MASK_NEG, base=0,
+                                pattern=[[-1, P]], channel_multiplier=1)
+        mask_bf = keep.tile([P, ROWS], BF16)
+        for u in range(2):
+            nc.gpsimd.tensor_copy(out=mask_bf[u * ROWS : (u + 1) * ROWS, :], in_=mask_f32[u * ROWS : (u + 1) * ROWS, u * ROWS : (u + 1) * ROWS])
+        ident_f32 = keep.tile([P, P], F32)
+        make_identity(nc, ident_f32[:])
 
         k_sb = keep.tile([P, CHUNKS, HKV * D], BF16)
         nc.sync.dma_start(out=k_sb[:], in_=k_rot.rearrange("b (t p) g d -> p (b t) (g d)", p=P))
         q_sb = [keep.tile([P, H * D], BF16, name="q_sb%d" % c) for c in range(CHUNKS)]
-        nc.sync.dma_start(out=q_sb[CHUNKS - 1][:], in_=q_rows[(CHUNKS - 1) * P : CHUNKS * P, :])
+        c = ORDER[0] // 2
+        nc.sync.dma_start(out=q_sb[c][:], in_=q_rows[c * P : (c + 1) * P, :])
         v_sb = keep.tile([P, 2, 2 * HKV * D], BF16)
         nc.sync.dma_start(out=v_sb[:], in_=v.rearrange("b (u p e) g d -> p (b u) (e g d)", u=2, e=2))
         w_sb = [keep.tile([P, HIDDEN], BF16, name="w_sb%d" % nt) for nt in range(HIDDEN // P)]
         for nb in range(N_BLOCKS):
             for nt in range(4 * nb, 4 * nb + 4):
                 nc.sync.dma_start(out=w_sb[nt][:], in_=w_o[nt * P : (nt + 1) * P, :])
-            c = CHUNKS - 2 - nb
-            if c >= 0:
+            if nb + 1 < CHUNKS:
+                c = ORDER[2 * nb + 2] // 2
                 nc.sync.dma_start(out=q_sb[c][:], in_=q_rows[c * P : (c + 1) * P, :])
 
         kT = keep.tile([P, HKV, S], BF16)
-        qT = keep.tile([P, CHUNKS, H, P], BF16)
+        qT = keep.tile([P, CHUNKS, HKV, 4, 2, ROWS], BF16)
         v_codes = keep.tile([P, HKV * D], U32, align_bytes=64)
         v_scales = keep.tile([P, HKV * D], U8, align_bytes=64)
         w_codes = keep.tile([P, PASSES, HIDDEN], U32, align_bytes=64)
         w_scales = keep.tile([P, PASSES, HIDDEN], U8, align_bytes=64)
-        turned_k, turned_q, scores_of, shift_of, rowsum_of, turned_e, e_grouped_of, e_operand = {}, {}, {}, {}, {}, {}, {}, {}
-        rinv_of, pv_of, o_sb_of, turned_o, o_grouped_of, o_operand = {}, {}, {}, {}, {}, {}
+        o_codes = [keep.tile([P, PASSES * P], U32, name="o_codes%d" % i, align_bytes=64) for i in range(CHUNKS)]
+        o_scales = [keep.tile([P, PASSES * P], U8, name="o_scales%d" % i, align_bytes=64) for i in range(CHUNKS)]
+        turned_k, turned_q, shift_of, rowsum_of, turned_e, e_grouped_of, e_operand = {}, {}, {}, {}, {}, {}, {}
+        rinv_of, pv_of, o_sb_of, turned_o, o_grouped_of = {}, {}, {}, {}, {}
         turned_w, w_grouped_of, acc_of = {}, {}, {}
 
-        def out_of_psum(index):
-            return nc.vector.tensor_copy if index % 2 == 0 else nc.scalar.copy
+        def copier(on_vector):
+            return nc.vector.tensor_copy if on_vector else nc.scalar.copy
 
         def turn_k(piece):
-            turned_k[piece] = psum.tile([P, 2, CHUNKS, P], BF16, tag="bank", name="turned_k")
+            turned_k[piece] = take(("k", piece)).bitcast(BF16).rearrange("p (g t j) -> p g t j", g=2, t=CHUNKS)
             for j in range(2):
                 g = 2 * piece + j
                 for t in range(CHUNKS):
-                    nc.tensor.transpose(
-                        out=turned_k[piece][:, j, t, :], in_=k_sb[:, t, g * D : (g + 1) * D], identity=ident_bf[:]
-                    )
+                    nc.tensor.transpose(out=turned_k[piece][:, j, t, :], in_=k_sb[:, t, g * D : (g + 1) * D], identity=ident_bf[:])
 
         def copy_k(piece):
-            out_of_psum(piece)(
-                out=kT[:, 2 * piece : 2 * piece + 2, :], in_=turned_k[piece][:].rearrange("p g t j -> p g (t j)")
-            )
+            copier(piece == 0)(out=kT[:, 2 * piece : 2 * piece + 2, :], in_=turned_k[piece].rearrange("p g t j -> p g (t j)"))
+            give(("k", piece))
 
         def turn_q(piece):
             place, half = divmod(piece, 2)
-            c = CHUNKS - 1 - place
-            turned_q[piece] = psum.tile([P, H // 2, P], BF16, tag="bank", name="turned_q")
-            for j in range(H // 2):
-                h = half * (H // 2) + j
-                nc.tensor.transpose(
-                    out=turned_q[piece][:, j, :], in_=q_sb[c][:, h * D : (h + 1) * D], identity=ident_bf[:]
-                )
+            c = ORDER[2 * place] // 2
+            turned_q[piece] = take(("q", piece)).bitcast(BF16).rearrange("p (g h i) -> p g h i", g=2, i=P)
+            for j in range(8):
+                h = half * 8 + j
+                nc.tensor.transpose(out=turned_q[piece][:, j // 4, j % 4, :], in_=q_sb[c][:, h * D : (h + 1) * D], identity=ident_bf[:])
 
         def copy_q(piece):
             place, half = divmod(piece, 2)
-            c = CHUNKS - 1 - place
-            out_of_psum(piece)(out=qT[:, c, half * (H // 2) : (half + 1) * (H // 2), :], in_=turned_q[piece][:])
+            c = ORDER[2 * place] // 2
+            for j in range(2):
+                copier(Q_V and piece % 2 == 0)(out=qT[:, c, 2 * half + j].rearrange("p m u q -> p u m q"),
+                                      in_=turned_q[piece][:, j].rearrange("p (u x) (r q) -> p u (x r) q", u=2, r=2))
+            give(("q", piece))
 
-        def score(unit):
-            place, h = divmod(unit, H)
-            c = CHUNKS - 1 - place
-            n_keys = (c + 1) * P
-            scores = psum.tile([P, n_keys], F32, tag="bank")
-            nc.tensor.matmul(
-                out=scores[:], lhsT=qT[:, c, h, :], rhs=kT[:, h // REP, 0:n_keys], start=True, stop=False
-            )
-            nc.tensor.matmul(out=scores[:, c * P : n_keys], lhsT=ident_bf[:], rhs=mask_bf[:], start=False, stop=True)
-            scores_of[unit] = scores
+        def score(unit, lead=True):
+            r = block_of(unit)
+            per = PER[r]
+            if lead and unit % per:
+                return
+            if lead:
+                take(("s", unit // per))
+                for other in range(unit + 1, unit + per):
+                    score(other, False)
+            n_keys = (r + 1) * ROWS
+            first = (unit % per) * n_keys
+            scores = bank_of["s", unit // per][:, first : first + n_keys]
+            g, x = divmod(unit % 8, 2)
+            nc.tensor.matmul(out=scores, lhsT=qT[:, r // 2, g, 2 * x + r % 2].rearrange("p u q -> p (u q)"), rhs=kT[:, g, 0:n_keys], start=True, stop=False)
+            nc.tensor.matmul(out=scores[:, r * ROWS : n_keys], lhsT=ident_bf[:], rhs=mask_bf[:], start=False, stop=True)
 
         def row_maximum(unit):
-            rowmax = stats.tile([P, 1], F32)
-            nc.vector.tensor_reduce(out=rowmax[:], in_=scores_of[unit][:], axis=AXIS.X, op=ALU.max)
-            shift = stats.tile([P, 1], F32)
-            nc.gpsimd.tensor_scalar(
-                out=shift[:], in0=rowmax[:], scalar1=-SCALE, scalar2=0.0, op0=ALU.mult, op1=ALU.add
-            )
-            shift_of[unit] = shift
+            r = block_of(unit)
+            per = PER[r]
+            if unit % per:
+                return
+            rowmax = stats.tile([P, per], F32, name="rowmax%d" % per)
+            nc.vector.tensor_reduce(out=rowmax[:], in_=bank_of["s", unit // per][:, 0 : per * (r + 1) * ROWS].rearrange("p (h k) -> p h k", h=per), axis=AXIS.X, op=ALU.max)
+            shift = stats.tile([P, per], F32, name="shift%d" % per)
+            nc.gpsimd.tensor_scalar(out=shift[:], in0=rowmax[:], scalar1=-SCALE, scalar2=0.0, op0=ALU.mult, op1=ALU.add)
+            shift_of[unit // per] = shift
 
         def exponential(unit):
-            step, hh = divmod(unit, REP)
-            n_keys = (CHUNKS - unit // H) * P
-            if hh == 0:
-                rowsum_of[step] = stats.tile([P, REP], F32, name="rowsum")
+            step, j = divmod(unit, QUAD)
+            r = block_of(unit)
+            per = PER[r]
+            n_keys = (r + 1) * ROWS
+            if j == 0:
+                rowsum_of[step] = stats.tile([P, QUAD], F32, name="rowsum")
             nc.scalar.activation(
-                out=e_tiles[step % 2][:, hh * S : hh * S + n_keys],
-                in_=scores_of[unit][:],
+                out=e_tiles[step % E_TILES][:, j * S : j * S + n_keys],
+                in_=bank_of["s", unit // per][:, unit % per * n_keys : (unit % per + 1) * n_keys],
                 func=ACT.Exp,
-                bias=shift_of[unit][:],
+                bias=shift_of[unit // per][:, unit % per : unit % per + 1],
                 scale=SCALE,
-                accum_out=rowsum_of[step][:, hh : hh + 1],
+                accum_out=rowsum_of[step][:, j : j + 1],
             )
+            if (unit + 1) % per == 0:
+                give(("s", unit // per))
 
         def reciprocal(step):
-            rinv = stats.tile([P, REP], F32)
+            rinv = stats.tile([P, QUAD], F32)
             nc.vector.reciprocal(out=rinv[:], in_=rowsum_of[step][:])
             rinv_of[step] = rinv
 
+        dirty = [set(range(RB)) for b in range(E_TILES)]
+
         def clear_e(step):
-            place, g = divmod(step, HKV)
-            c = CHUNKS - 1 - place
-            if g >= HKV - 2 and c > 0:
-                e_heads = e_tiles[step % 2][:].rearrange("p (h k) -> p h k", h=REP)
-                nc.gpsimd.memset(e_heads[:, :, c * P : (c + 1) * P], 0.0)
+            b = step % E_TILES
+            if step >= 0:
+                dirty[b] |= set(range(ORDER[step // 2] + 1))
+            follower = step + E_TILES
+            if follower >= STEPS:
+                return
+            r = ORDER[follower // 2]
+            top = RB if r >= LOW or not SKIP_UPPER or QUAD // 2 * (follower - 2 * ORDER.index(LOW - 1)) < E_BANKS else LOW
+            keys = [k for k in range(r + 1, top) if k in dirty[b]]
+            if keys:
+                e_units = e_tiles[b][:].rearrange("p (h k) -> p h k", h=QUAD)
+                nc.gpsimd.memset(e_units[:, :, keys[0] * ROWS : (keys[-1] + 1) * ROWS], 0.0)
+                dirty[b] -= set(keys)
 
         def turn_e(unit):
             pair, j = divmod(unit, 2)
-            step, hh = divmod(unit, REP)
+            step, jj = divmod(unit, QUAD)
+            low_pair = pair - 4 * ORDER.index(LOW - 1)
             if j == 0:
-                turned_e[pair] = psum.tile([P, 2, 2, P], F32, tag="bank", name="turned_e")
-            e_words = e_tiles[step % 2][:].bitcast(F32)
-            for u in range(2):
-                first = (hh * 2 + u) * P
-                nc.tensor.transpose(
-                    out=turned_e[pair][:, j, u, :], in_=e_words[:, first : first + P], identity=ident_f32[:]
-                )
+                if SKIP_UPPER and low_pair >= 0:
+                    if len(e_banks) < E_BANKS:
+                        e_banks.append(take(("pin", pair)))
+                    turned_e[pair] = e_banks[low_pair % E_BANKS]
+                else:
+                    turned_e[pair] = take(("e", pair))
+                turned_e[pair] = turned_e[pair].rearrange("p (h u i) -> p h u i", h=2, u=2)
+            e_words = e_tiles[step % E_TILES][:].bitcast(F32)
+            for u in range(1 if SKIP_UPPER and low_pair >= E_BANKS else 2):
+                first = (jj * 2 + u) * P
+                nc.tensor.transpose(out=turned_e[pair][:, j, u, :], in_=e_words[:, first : first + P], identity=ident_f32[:])
 
         def copy_e(pair):
             step, half = divmod(pair, 2)
             if half == 0:
-                e_grouped_of[step] = stage.tile([P, REP * P * PACK], BF16, align_bytes=64, name="e_grouped")
-            words = e_grouped_of[step][:].bitcast(F32).rearrange("p (h i u) -> p h i u", h=REP, u=2)
-            nc.scalar.copy(
-                out=words[:, 2 * half : 2 * half + 2, :, :], in_=turned_e[pair][:].rearrange("p h u i -> p h i u")
-            )
+                e_grouped_of[step] = stage.tile([P, QUAD * P * PACK], BF16, align_bytes=64, name="e_grouped", bufs=3)
+            words = e_grouped_of[step][:].bitcast(F32).rearrange("p (h i u) -> p h i u", h=QUAD, u=2)
+            nc.scalar.copy(out=words[:, 2 * half : 2 * half + 2, :, :], in_=turned_e[pair].rearrange("p h u i -> p h i u"))
+            if ("e", pair) in bank_of:
+                give(("e", pair))
 
         def quantise_e(step):
-            e_codes = stage.tile([P, REP * P], U32, align_bytes=64)
-            e_scales = stage.tile([P, REP * P], U8, align_bytes=64)
+            e_codes = stage.tile([P, QUAD * P], U32, align_bytes=64)
+            e_scales = stage.tile([P, QUAD * P], U8, align_bytes=64)
             nc.vector.quantize_mx(out=e_codes[:].bitcast(FP8X4), scales=e_scales[:], in_=e_grouped_of[step][:])
             e_operand[step] = (e_codes, e_scales)
 
         def multiply_v(step):
-            g = step % HKV
             e_codes, e_scales = e_operand[step]
-            pv = psum.tile([P, REP, D], F32, tag="bank")
-            for hh in range(REP):
-                queries = slice(hh * P, (hh + 1) * P)
+            pv = take(("pv", step)).rearrange("p (h d) -> p h d", h=QUAD)
+            for j in range(QUAD):
+                g = 2 * (step % 2) + j // 2
+                rows = slice(j * P, (j + 1) * P)
                 nc.tensor.matmul_mx(
-                    out=pv[:, hh, :],
-                    lhsT=e_codes[:, queries].bitcast(FP8X4),
-                    lhsT_scale=e_scales[:, queries],
+                    out=pv[:, j, :],
+                    lhsT=e_codes[:, rows].bitcast(FP8X4),
+                    lhsT_scale=e_scales[:, rows],
                     rhs=v_codes[:, g * D : (g + 1) * D].bitcast(FP8X4),
                     rhs_scale=v_scales[:, g * D : (g + 1) * D],
                     start=True,
@@ -250,118 +334,140 @@ def tile_gemmaattention_pb_kernel(tc, q_rot, k_rot, v, w_o, out):
             pv_of[step] = pv
 
         def normalise(step):
-            o_sb = stage.tile([P, REP * D], BF16)
+            o_sb = stage.tile([P, QUAD * D], BF16)
             nc.vector.tensor_tensor(
-                out=o_sb[:].rearrange("p (h d) -> p h d", h=REP),
-                in0=pv_of[step][:],
-                in1=rinv_of[step][:].unsqueeze(2).to_broadcast([P, REP, D]),
+                out=o_sb[:].rearrange("p (h d) -> p h d", h=QUAD),
+                in0=pv_of[step],
+                in1=rinv_of[step][:].unsqueeze(2).to_broadcast([P, QUAD, D]),
                 op=ALU.mult,
             )
             o_sb_of[step] = o_sb
+            give(("pv", step))
 
         def turn_o(step):
             o_words = o_sb_of[step][:].bitcast(F32)
-            turned = psum.tile([P, 2, P], F32, tag="bank")
-            for u in range(2):
-                nc.tensor.transpose(out=turned[:, u, :], in_=o_words[:, u * P : (u + 1) * P], identity=ident_f32[:])
+            turned = take(("o", step))[:, 0 : 2 * P].rearrange("p (g i) -> p g i", g=2)
+            for j in range(2):
+                nc.tensor.transpose(out=turned[:, j, :], in_=o_words[:, j * P : (j + 1) * P], identity=ident_f32[:])
             turned_o[step] = turned
 
         def copy_o(step):
-            place, g = divmod(step, HKV)
-            if g == 0:
-                o_grouped_of[place] = stage.tile([P, PASSES * P * PACK], BF16, align_bytes=64, name="o_grouped")
-            words = o_grouped_of[place][:].bitcast(F32).rearrange("p (g i u) -> p g i u", g=PASSES, u=2)
-            nc.scalar.copy(out=words[:, g, :, :], in_=turned_o[step][:].rearrange("p u i -> p i u"))
+            place, rest = divmod(step, 4)
+            r = ORDER[step // 2]
+            gp = step % 2
+            if rest < 2:
+                o_grouped_of[place, gp] = stage.tile([P, 2 * P * PACK], BF16, align_bytes=64, name="o_grouped")
+            words = o_grouped_of[place, gp][:].bitcast(F32).rearrange("p (g r q u) -> p g r q u", g=2, r=2, u=2)
+            nc.scalar.copy(out=words[:, :, r % 2, :, :], in_=turned_o[step].rearrange("p g (u q) -> p g q u", u=2))
+            give(("o", step))
 
-        def quantise_o(place):
-            o_codes = keep.tile([P, PASSES * P], U32, name="o_codes%d" % place, align_bytes=64)
-            o_scales = keep.tile([P, PASSES * P], U8, name="o_scales%d" % place, align_bytes=64)
-            nc.vector.quantize_mx(out=o_codes[:].bitcast(FP8X4), scales=o_scales[:], in_=o_grouped_of[place][:])
-            o_operand[place] = (o_codes, o_scales)
+        def quantise_o(piece):
+            place, gp = divmod(piece, 2)
+            rows = slice(gp * 2 * P, (gp + 1) * 2 * P)
+            nc.vector.quantize_mx(out=o_codes[place][:, rows].bitcast(FP8X4), scales=o_scales[place][:, rows], in_=o_grouped_of[place, gp][:])
 
         def quantise_v(piece):
             v_grouped = keep.tile([P, HKV * D * PACK], BF16, align_bytes=64)
-            nc.vector.tensor_copy(
-                out=v_grouped[:].rearrange("p (c t) -> p c t", t=PACK),
-                in_=v_sb[:].rearrange("p u (e c) -> p c (u e)", e=2),
-            )
+            nc.vector.tensor_copy(out=v_grouped[:].rearrange("p (c t) -> p c t", t=PACK), in_=v_sb[:].rearrange("p u (e c) -> p c (u e)", e=2))
             nc.vector.quantize_mx(out=v_codes[:].bitcast(FP8X4), scales=v_scales[:], in_=v_grouped[:])
 
         def turn_w(piece):
             nb, rest = divmod(piece, 2 * PASSES)
             g, half = divmod(rest, 2)
-            turned = psum.tile([P, 2, 2, P], F32, tag="bank")
+            turned = take(("w", piece)).rearrange("p (r u n) -> p r u n", r=2, u=2)
             for j in range(2):
                 words = w_sb[4 * nb + 2 * half + j][:].bitcast(F32)
                 for u in range(2):
                     first = (2 * g + u) * P
-                    nc.tensor.transpose(
-                        out=turned[:, j, u, :], in_=words[:, first : first + P], identity=ident_f32[:]
-                    )
+                    nc.tensor.transpose(out=turned[:, j, u, :], in_=words[:, first : first + P], identity=ident_f32[:])
             turned_w[piece] = turned
 
         def copy_w(piece):
-            w_grouped = stage.tile([P, 2 * P * PACK], BF16, align_bytes=64, bufs=FROM_SBUF + 2)
+            w_grouped = stage.tile([P, 2 * P * PACK], BF16, align_bytes=64, bufs=5)
             words = w_grouped[:].bitcast(F32).rearrange("p (r n u) -> p r n u", r=2, u=2)
-            out_of_psum(piece)(out=words, in_=turned_w[piece][:].rearrange("p r u n -> p r n u"))
+            copier(piece % W_V_DEN == W_V_OFF)(out=words, in_=turned_w[piece].rearrange("p r u n -> p r n u"))
             w_grouped_of[piece] = w_grouped
+            give(("w", piece))
 
         def quantise_w(piece):
             nb, rest = divmod(piece, 2 * PASSES)
             g, half = divmod(rest, 2)
             features = slice(nb * BANK + half * 2 * P, nb * BANK + (half + 1) * 2 * P)
-            nc.vector.quantize_mx(
-                out=w_codes[:, g, features].bitcast(FP8X4),
-                scales=w_scales[:, g, features],
-                in_=w_grouped_of[piece][:],
+            nc.vector.quantize_mx(out=w_codes[:, g, features].bitcast(FP8X4), scales=w_scales[:, g, features], in_=w_grouped_of[piece][:])
+
+        def project_pass(block, g):
+            place, nb = divmod(block, N_BLOCKS)
+            features = slice(nb * BANK, (nb + 1) * BANK)
+            if g == 0:
+                if place == CHUNKS - 1 and nb < len(e_banks):
+                    acc_of[block] = e_banks[nb]
+                else:
+                    acc_of[block] = take(("acc", block))
+            rows = slice(g * P, (g + 1) * P)
+            nc.tensor.matmul_mx(
+                out=acc_of[block],
+                lhsT=o_codes[place][:, rows].bitcast(FP8X4),
+                lhsT_scale=o_scales[place][:, rows],
+                rhs=w_codes[:, g, features].bitcast(FP8X4),
+                rhs_scale=w_scales[:, g, features],
+                start=(g == 0),
+                stop=(g == PASSES - 1),
             )
 
         def project(block):
-            place, nb = divmod(block, N_BLOCKS)
-            o_codes, o_scales = o_operand[place]
-            features = slice(nb * BANK, (nb + 1) * BANK)
-            acc = psum.tile([P, BANK], F32, tag="bank")
             for g in range(PASSES):
-                queries = slice(g * P, (g + 1) * P)
-                nc.tensor.matmul_mx(
-                    out=acc[:],
-                    lhsT=o_codes[:, queries].bitcast(FP8X4),
-                    lhsT_scale=o_scales[:, queries],
-                    rhs=w_codes[:, g, features].bitcast(FP8X4),
-                    rhs_scale=w_scales[:, g, features],
-                    start=(g == 0),
-                    stop=(g == PASSES - 1),
-                )
-            acc_of[block] = acc
+                project_pass(block, g)
 
         def store(block):
             place, nb = divmod(block, N_BLOCKS)
-            c = CHUNKS - 1 - place
+            c = ORDER[2 * place] // 2
             result = results.tile([P, BANK], F32)
-            nc.vector.tensor_copy(out=result[:], in_=acc_of[block][:])
+            copier(not ST_ALT or nb % 2 == 0)(out=result[:], in_=acc_of[block])
+            if ("acc", block) in bank_of:
+                give(("acc", block))
             nc.sync.dma_start(out=out_rows[c * P : (c + 1) * P, nb * BANK : (nb + 1) * BANK], in_=result[:])
 
-        for tick in range(TURN_K_AT, TICKS):
-            run_if_due(row_maximum, tick, MAX_AT, 1, UNITS)
-            run_if_due(reciprocal, tick, RECIPROCAL_AT, 4, STEPS)
-            run_if_due(clear_e, tick, CLEAR_E_AT, 4, STEPS)
-            run_if_due(copy_e, tick, COPY_E_AT, 2, UNITS // 2)
-            run_if_due(normalise, tick, NORMALISE_AT, 4, STEPS)
-            run_if_due(copy_o, tick, COPY_O_AT, 4, STEPS)
-            run_if_due(copy_w, tick, COPY_W_AT, 1, W_PIECES)
-            run_if_due(copy_k, tick, COPY_K_AT, 8, HKV // 2)
-            run_if_due(copy_q, tick, COPY_Q_AT, 8, UNITS // 8)
-            run_if_due(store, tick, STORE_AT, PROJECT_EVERY, OUT_BLOCKS)
-            run_if_due(exponential, tick, EXP_AT, 1, UNITS)
-            run_if_due(quantise_e, tick, QUANTISE_E_AT, 4, STEPS)
-            run_if_due(quantise_o, tick, QUANTISE_O_AT, 16, CHUNKS)
-            run_if_due(quantise_w, tick, QUANTISE_W_AT, 1, W_PIECES)
-            run_if_due(quantise_v, tick, QUANTISE_V_AT, 1, 1)
-            run_if_due(turn_e, tick, TURN_E_AT, 1, UNITS)
-            run_if_due(turn_o, tick, TURN_O_AT, 4, STEPS)
-            run_if_due(turn_w, tick, TURN_W_AT, 1, W_PIECES)
-            run_if_due(turn_k, tick, TURN_K_AT, 8, HKV // 2)
-            run_if_due(turn_q, tick, TURN_Q_AT, 8, UNITS // 8)
-            run_if_due(score, tick, SCORE_AT, 1, UNITS)
-            run_if_due(multiply_v, tick, MULTIPLY_V_AT, 4, STEPS)
-            run_if_due(project, tick, PROJECT_AT, PROJECT_EVERY, OUT_BLOCKS)
+        by_tick = {}
+
+        def due(tick, fn, *piece):
+            by_tick.setdefault(tick, []).append((fn, piece))
+
+        def every(fn, count, at):
+            for piece in range(count):
+                due(at(piece), fn, piece)
+
+        every(row_maximum, UNITS, lambda u: unit_tick(u) + MAX_AT)
+        every(reciprocal, STEPS, lambda s: step_tick(s) + RECIPROCAL_AT)
+        for b in range(E_TILES):
+            due(-100, clear_e, b - E_TILES)
+        every(clear_e, STEPS, lambda s: step_tick(s) + TURN_E_AT + 1)
+        every(copy_e, UNITS // 2, lambda p: unit_tick(2 * p + 1) + COPY_E_AT)
+        every(normalise, STEPS, lambda s: step_tick(s) + NORMALISE_AT)
+        every(copy_o, STEPS, lambda s: step_tick(s) + COPY_O_AT)
+        every(copy_w, W_PIECES, lambda w: w_tick(w) + COPY_W_AT)
+        every(copy_k, HKV // 2, lambda k: TURN_K_AT[k] + FROM_PSUM)
+        every(copy_q, 2 * CHUNKS, lambda q: unit_tick(16 * (q // 2) + 4 * (q % 2)) - TURN_Q_AHEAD + FROM_PSUM)
+        for block in range(OUT_BLOCKS - N_BLOCKS):
+            due(PROJECT_TICK[block] + STORE_LAG, store, block)
+        for nb in range(N_BLOCKS):
+            due(o_ready(CHUNKS - 1, 1) + O_LAG + 1, store, OUT_BLOCKS - N_BLOCKS + nb)
+        every(exponential, UNITS, lambda u: unit_tick(u) + EXP_AT)
+        every(quantise_e, STEPS, lambda s: step_tick(s) + QUANTISE_E_AT)
+        every(quantise_o, 2 * CHUNKS, lambda i: o_ready(i // 2, i % 2))
+        every(quantise_w, W_PIECES, lambda w: w_tick(w) + QUANTISE_W_AT)
+        due(QUANTISE_V_AT, quantise_v, 0)
+        every(turn_e, UNITS, lambda u: unit_tick(u) + TURN_E_AT)
+        every(turn_o, STEPS, lambda s: step_tick(s) + TURN_O_AT)
+        every(turn_w, W_PIECES, lambda w: w_tick(w) + TURN_W_AT)
+        every(turn_k, HKV // 2, lambda k: TURN_K_AT[k])
+        every(turn_q, 2 * CHUNKS, lambda q: unit_tick(16 * (q // 2) + 4 * (q % 2)) - TURN_Q_AHEAD)
+        every(score, UNITS, lambda u: unit_tick(u))
+        every(multiply_v, STEPS, lambda s: step_tick(s) + MULTIPLY_V_AT)
+        for block in range(OUT_BLOCKS - N_BLOCKS):
+            due(PROJECT_TICK[block], project, block)
+        for g in range(PASSES):
+            for nb in range(N_BLOCKS):
+                due(max(LAST_AT, o_ready(CHUNKS - 1, g // 2) + O_LAG), project_pass, OUT_BLOCKS - N_BLOCKS + nb, g)
+        for tick in sorted(by_tick):
+            for fn, piece in by_tick[tick]:
+                fn(*piece)

@@ -41,31 +41,35 @@ PER = [4, 4, 2, 2, 1, 1, 1, 1]
 LOW = 4
 FROM_PSUM = 1
 EXP_GAP = 1
-L_ET = 4
+L_ET = 6
+R_EARLY = 3
 L_EQ = 1
-L_QM = 3
+L_QM = 4
 L_NT = 2
 L_OQ = 2
-L_WQ = 3
-TURN_Q_AHEAD = 5
-TURN_K_AT = [-7, -1]
+L_WQ = 2
+TURN_Q_AHEAD = 7
+LOWQ_AHEAD = 6
+E_V = 0
+O_V = 0
+S_V_DEN = 1
+TURN_K_AT = [-7, 2]
 QUANTISE_V_AT = 0
 TURN_W_AT = 5
-PROJECT_GAP = 0
-STORE_LAG = 3
-O_LAG = 2
-W_NUM = 1
-W_DEN = 1
-P_GRID = 3
-P_GRID2 = 2
+PROJECT_GAP = 2
+STORE_LAG = 2
+O_LAG = 3
+W_NUM = 4
+W_DEN = 4
+P_GRID = 5
+P_GRID2 = 4
 P_SWITCH = 46
 E_BANKS = 2
 E_TILES = 4
-SKIP_UPPER = True
-ST_ALT = False
-W_V_DEN = 3
+SKIP_UPPER = False
+W_V_DEN = 4
 W_V_OFF = 0
-Q_V = True
+Q_V = False
 
 
 def block_of(unit):
@@ -83,17 +87,21 @@ def step_tick(step):
 
 MAX_AT = FROM_PSUM
 EXP_AT = MAX_AT + EXP_GAP
-RECIPROCAL_AT = EXP_AT + 1
 TURN_E_AT = EXP_AT + L_ET
 COPY_E_AT = TURN_E_AT + FROM_PSUM
 QUANTISE_E_AT = COPY_E_AT + L_EQ
 MULTIPLY_V_AT = QUANTISE_E_AT + L_QM
 NORMALISE_AT = MULTIPLY_V_AT + FROM_PSUM
+RECIPROCAL_AT = NORMALISE_AT - R_EARLY
 TURN_O_AT = NORMALISE_AT + L_NT
 COPY_O_AT = TURN_O_AT + FROM_PSUM
 QUANTISE_O_AT = COPY_O_AT + L_OQ
 COPY_W_AT = TURN_W_AT + FROM_PSUM
 QUANTISE_W_AT = COPY_W_AT + L_WQ
+
+
+def q_tick(piece):
+    return unit_tick(16 * (piece // 2) + 4 * (piece % 2)) - (TURN_Q_AHEAD if piece < 4 else LOWQ_AHEAD)
 
 
 def w_tick(piece):
@@ -134,7 +142,7 @@ def tile_gemmaattention_pb_kernel(tc, q_rot, k_rot, v, w_o, out):
         keep = ctx.enter_context(tc.tile_pool(name="keep", bufs=1))
         stage = ctx.enter_context(tc.tile_pool(name="stage", bufs=4))
         stats = ctx.enter_context(tc.tile_pool(name="stats", bufs=8))
-        results = ctx.enter_context(tc.tile_pool(name="results", bufs=5))
+        results = ctx.enter_context(tc.tile_pool(name="results", bufs=4))
         psum = ctx.enter_context(tc.psum_pool(name="psum", bufs=1))
         free_banks = [psum.tile([P, BANK], F32, name="bank%d" % b) for b in range(8)]
         bank_of = {}
@@ -236,13 +244,13 @@ def tile_gemmaattention_pb_kernel(tc, q_rot, k_rot, v, w_o, out):
         def row_maximum(unit):
             r = block_of(unit)
             per = PER[r]
-            if unit % per:
-                return
-            rowmax = stats.tile([P, per], F32, name="rowmax%d" % per)
-            nc.vector.tensor_reduce(out=rowmax[:], in_=bank_of["s", unit // per][:, 0 : per * (r + 1) * ROWS].rearrange("p (h k) -> p h k", h=per), axis=AXIS.X, op=ALU.max)
-            shift = stats.tile([P, per], F32, name="shift%d" % per)
-            nc.gpsimd.tensor_scalar(out=shift[:], in0=rowmax[:], scalar1=-SCALE, scalar2=0.0, op0=ALU.mult, op1=ALU.add)
-            shift_of[unit // per] = shift
+            n_keys = (r + 1) * ROWS
+            first = unit % per * n_keys
+            scaled = stage.tile([P, S], BF16, name="scaled", bufs=2)
+            shift = stats.tile([P, 1], F32, name="shift", bufs=12)
+            nc.vector.tensor_scalar(out=scaled[:, 0:n_keys], in0=bank_of["s", unit // per][:, first : first + n_keys],
+                                    scalar1=-SCALE, scalar2=3.0e38, op0=ALU.mult, op1=ALU.min, accum_out=shift[:])
+            shift_of[unit] = shift
 
         def exponential(unit):
             step, j = divmod(unit, QUAD)
@@ -255,7 +263,7 @@ def tile_gemmaattention_pb_kernel(tc, q_rot, k_rot, v, w_o, out):
                 out=e_tiles[step % E_TILES][:, j * S : j * S + n_keys],
                 in_=bank_of["s", unit // per][:, unit % per * n_keys : (unit % per + 1) * n_keys],
                 func=ACT.Exp,
-                bias=shift_of[unit // per][:, unit % per : unit % per + 1],
+                bias=shift_of[unit][:],
                 scale=SCALE,
                 accum_out=rowsum_of[step][:, j : j + 1],
             )
@@ -306,7 +314,7 @@ def tile_gemmaattention_pb_kernel(tc, q_rot, k_rot, v, w_o, out):
             if half == 0:
                 e_grouped_of[step] = stage.tile([P, QUAD * P * PACK], BF16, align_bytes=64, name="e_grouped", bufs=3)
             words = e_grouped_of[step][:].bitcast(F32).rearrange("p (h i u) -> p h i u", h=QUAD, u=2)
-            nc.scalar.copy(out=words[:, 2 * half : 2 * half + 2, :, :], in_=turned_e[pair].rearrange("p h u i -> p h i u"))
+            copier(pair % 4 < E_V)(out=words[:, 2 * half : 2 * half + 2, :, :], in_=turned_e[pair].rearrange("p h u i -> p h i u"))
             if ("e", pair) in bank_of:
                 give(("e", pair))
 
@@ -358,7 +366,7 @@ def tile_gemmaattention_pb_kernel(tc, q_rot, k_rot, v, w_o, out):
             if rest < 2:
                 o_grouped_of[place, gp] = stage.tile([P, 2 * P * PACK], BF16, align_bytes=64, name="o_grouped")
             words = o_grouped_of[place, gp][:].bitcast(F32).rearrange("p (g r q u) -> p g r q u", g=2, r=2, u=2)
-            nc.scalar.copy(out=words[:, :, r % 2, :, :], in_=turned_o[step].rearrange("p g (u q) -> p g q u", u=2))
+            copier(step % 4 < O_V)(out=words[:, :, r % 2, :, :], in_=turned_o[step].rearrange("p g (u q) -> p g q u", u=2))
             give(("o", step))
 
         def quantise_o(piece):
@@ -373,7 +381,7 @@ def tile_gemmaattention_pb_kernel(tc, q_rot, k_rot, v, w_o, out):
 
         def turn_w(piece):
             nb, rest = divmod(piece, 2 * PASSES)
-            g, half = divmod(rest, 2)
+            half, g = divmod(rest, PASSES)
             turned = take(("w", piece)).rearrange("p (r u n) -> p r u n", r=2, u=2)
             for j in range(2):
                 words = w_sb[4 * nb + 2 * half + j][:].bitcast(F32)
@@ -391,7 +399,7 @@ def tile_gemmaattention_pb_kernel(tc, q_rot, k_rot, v, w_o, out):
 
         def quantise_w(piece):
             nb, rest = divmod(piece, 2 * PASSES)
-            g, half = divmod(rest, 2)
+            half, g = divmod(rest, PASSES)
             features = slice(nb * BANK + half * 2 * P, nb * BANK + (half + 1) * 2 * P)
             nc.vector.quantize_mx(out=w_codes[:, g, features].bitcast(FP8X4), scales=w_scales[:, g, features], in_=w_grouped_of[piece][:])
 
@@ -422,7 +430,7 @@ def tile_gemmaattention_pb_kernel(tc, q_rot, k_rot, v, w_o, out):
             place, nb = divmod(block, N_BLOCKS)
             c = ORDER[2 * place] // 2
             result = results.tile([P, BANK], F32)
-            copier(not ST_ALT or nb % 2 == 0)(out=result[:], in_=acc_of[block])
+            copier(nb % S_V_DEN == 0)(out=result[:], in_=acc_of[block])
             if ("acc", block) in bank_of:
                 give(("acc", block))
             nc.sync.dma_start(out=out_rows[c * P : (c + 1) * P, nb * BANK : (nb + 1) * BANK], in_=result[:])
@@ -446,7 +454,7 @@ def tile_gemmaattention_pb_kernel(tc, q_rot, k_rot, v, w_o, out):
         every(copy_o, STEPS, lambda s: step_tick(s) + COPY_O_AT)
         every(copy_w, W_PIECES, lambda w: w_tick(w) + COPY_W_AT)
         every(copy_k, HKV // 2, lambda k: TURN_K_AT[k] + FROM_PSUM)
-        every(copy_q, 2 * CHUNKS, lambda q: unit_tick(16 * (q // 2) + 4 * (q % 2)) - TURN_Q_AHEAD + FROM_PSUM)
+        every(copy_q, 2 * CHUNKS, lambda q: q_tick(q) + FROM_PSUM)
         for block in range(OUT_BLOCKS - N_BLOCKS):
             due(PROJECT_TICK[block] + STORE_LAG, store, block)
         for nb in range(N_BLOCKS):
@@ -460,7 +468,7 @@ def tile_gemmaattention_pb_kernel(tc, q_rot, k_rot, v, w_o, out):
         every(turn_o, STEPS, lambda s: step_tick(s) + TURN_O_AT)
         every(turn_w, W_PIECES, lambda w: w_tick(w) + TURN_W_AT)
         every(turn_k, HKV // 2, lambda k: TURN_K_AT[k])
-        every(turn_q, 2 * CHUNKS, lambda q: unit_tick(16 * (q // 2) + 4 * (q % 2)) - TURN_Q_AHEAD)
+        every(turn_q, 2 * CHUNKS, q_tick)
         every(score, UNITS, lambda u: unit_tick(u))
         every(multiply_v, STEPS, lambda s: step_tick(s) + MULTIPLY_V_AT)
         for block in range(OUT_BLOCKS - N_BLOCKS):

@@ -6,6 +6,7 @@ from concourse.masks import make_identity
 F32 = mybir.dt.float32
 BF16 = mybir.dt.bfloat16
 U32 = mybir.dt.uint32
+I32 = mybir.dt.int32
 U8 = mybir.dt.uint8
 FP8X4 = mybir.dt.float8_e4m3fn_x4
 ACT = mybir.ActivationFunctionType
@@ -41,35 +42,36 @@ PER = [4, 4, 2, 2, 1, 1, 1, 1]
 LOW = 4
 FROM_PSUM = 1
 EXP_GAP = 1
-L_ET = 6
-R_EARLY = 3
+L_ET = 3
+R_EARLY = 1
 L_EQ = 1
-L_QM = 4
+L_QM = 3
 L_NT = 2
 L_OQ = 2
-L_WQ = 2
+L_WQ = 1
 TURN_Q_AHEAD = 7
-LOWQ_AHEAD = 6
+LOWQ_AHEAD = 9
 E_V = 0
 O_V = 0
-S_V_DEN = 1
-TURN_K_AT = [-7, 2]
+S_V_DEN = 2
+TURN_K_AT = [-7, 1]
 QUANTISE_V_AT = 0
-TURN_W_AT = 5
+TURN_W_AT = 4
 PROJECT_GAP = 2
 STORE_LAG = 2
-O_LAG = 3
+O_LAG = 4
 W_NUM = 4
 W_DEN = 4
-P_GRID = 5
+P_GRID = 4
 P_GRID2 = 4
-P_SWITCH = 46
-E_BANKS = 2
+P_SWITCH = 45
 E_TILES = 4
-SKIP_UPPER = False
-W_V_DEN = 4
-W_V_OFF = 0
-Q_V = False
+W_V_DEN = 7
+W_V_OFF = 1
+Q_V = True
+LOADS = ["k", "q0", "v", "w0", "q1", "w1", "half", "q2", "w2", "q3", "w3"]
+HALF_AT = 14
+HALF_EVERY = 2
 
 
 def block_of(unit):
@@ -79,6 +81,14 @@ def block_of(unit):
 def unit_tick(unit):
     place, rest = divmod(unit, 8)
     return (sum(8 * HALF_TICKS[r] for r in ORDER[:place]) + rest * HALF_TICKS[ORDER[place]]) // 2
+
+
+def keys_of(r):
+    return S // 2 if r == 2 else (r + 1) * ROWS
+
+
+def width(r):
+    return S if r >= LOW else S // 2
 
 
 def step_tick(step):
@@ -142,11 +152,11 @@ def tile_gemmaattention_pb_kernel(tc, q_rot, k_rot, v, w_o, out):
         keep = ctx.enter_context(tc.tile_pool(name="keep", bufs=1))
         stage = ctx.enter_context(tc.tile_pool(name="stage", bufs=4))
         stats = ctx.enter_context(tc.tile_pool(name="stats", bufs=8))
-        results = ctx.enter_context(tc.tile_pool(name="results", bufs=4))
+        results = ctx.enter_context(tc.tile_pool(name="results", bufs=5))
+        weights = ctx.enter_context(tc.tile_pool(name="weights", bufs=12))
         psum = ctx.enter_context(tc.psum_pool(name="psum", bufs=1))
         free_banks = [psum.tile([P, BANK], F32, name="bank%d" % b) for b in range(8)]
         bank_of = {}
-        e_banks = []
 
         def take(owner):
             bank_of[owner] = free_banks.pop(0)
@@ -162,29 +172,46 @@ def tile_gemmaattention_pb_kernel(tc, q_rot, k_rot, v, w_o, out):
         nc.gpsimd.memset(mask_f32[:], 0.0)
         nc.gpsimd.affine_select(out=mask_f32[:], in_=mask_f32[:], compare_op=ALU.is_ge, fill=MASK_NEG, base=0,
                                 pattern=[[-1, P]], channel_multiplier=1)
-        mask_bf = keep.tile([P, ROWS], BF16)
+        mask_bf = keep.tile([P, 2 * ROWS], BF16)
+        nc.gpsimd.memset(mask_bf[:, ROWS : 2 * ROWS], MASK_NEG)
         for u in range(2):
-            nc.gpsimd.tensor_copy(out=mask_bf[u * ROWS : (u + 1) * ROWS, :], in_=mask_f32[u * ROWS : (u + 1) * ROWS, u * ROWS : (u + 1) * ROWS])
+            nc.gpsimd.tensor_copy(out=mask_bf[u * ROWS : (u + 1) * ROWS, 0:ROWS], in_=mask_f32[u * ROWS : (u + 1) * ROWS, u * ROWS : (u + 1) * ROWS])
         ident_f32 = keep.tile([P, P], F32)
         make_identity(nc, ident_f32[:])
 
         k_sb = keep.tile([P, CHUNKS, HKV * D], BF16)
-        nc.sync.dma_start(out=k_sb[:], in_=k_rot.rearrange("b (t p) g d -> p (b t) (g d)", p=P))
         q_sb = [keep.tile([P, H * D], BF16, name="q_sb%d" % c) for c in range(CHUNKS)]
-        c = ORDER[0] // 2
-        nc.sync.dma_start(out=q_sb[c][:], in_=q_rows[c * P : (c + 1) * P, :])
         v_sb = keep.tile([P, 2, 2 * HKV * D], BF16)
-        nc.sync.dma_start(out=v_sb[:], in_=v.rearrange("b (u p e) g d -> p (b u) (e g d)", u=2, e=2))
-        w_sb = [keep.tile([P, HIDDEN], BF16, name="w_sb%d" % nt) for nt in range(HIDDEN // P)]
-        for nb in range(N_BLOCKS):
-            for nt in range(4 * nb, 4 * nb + 4):
-                nc.sync.dma_start(out=w_sb[nt][:], in_=w_o[nt * P : (nt + 1) * P, :])
-            if nb + 1 < CHUNKS:
-                c = ORDER[2 * nb + 2] // 2
+        half_sb = keep.tile([P, PACK, HKV * D], BF16)
+        w_sb = {}
+
+        def load(what):
+            if what == "k":
+                nc.sync.dma_start(out=k_sb[:], in_=k_rot.rearrange("b (t p) g d -> p (b t) (g d)", p=P))
+            elif what == "v":
+                nc.sync.dma_start(out=v_sb[:], in_=v.rearrange("b (u p e) g d -> p (b u) (e g d)", u=2, e=2))
+            elif what == "half":
+                for x in range(2):
+                    nc.sync.dma_start(out=half_sb[x * ROWS : (x + 1) * ROWS, :, :].rearrange("p (u e) n -> p u (e n)", u=2), in_=v[:, 0 : 4 * ROWS].rearrange("b (u p e) g d -> p (b u) (e g d)", u=2, e=2))
+            elif what[0] == "q":
+                c = ORDER[2 * int(what[1])] // 2
                 nc.sync.dma_start(out=q_sb[c][:], in_=q_rows[c * P : (c + 1) * P, :])
+            else:
+                for nt in range(4 * int(what[1]), 4 * int(what[1]) + 4):
+                    w_sb[nt] = weights.tile([P, HIDDEN], BF16, name="w_sb")
+                    nc.sync.dma_start(out=w_sb[nt][:], in_=w_o[nt * P : (nt + 1) * P, :])
+
+        for what in LOADS[:-1]:
+            load(what)
 
         kT = keep.tile([P, HKV, S], BF16)
         qT = keep.tile([P, CHUNKS, HKV, 4, 2, ROWS], BF16)
+        pair_codes = keep.tile([P, HKV * 2 * D], U32, align_bytes=64)
+        nc.gpsimd.memset(pair_codes[:].bitcast(I32), 0)
+        half_codes = keep.tile([P, HKV * D], U32, align_bytes=64)
+        half_scales = keep.tile([P, HKV * D], U8, align_bytes=64)
+        half_grouped = {}
+        pair_scales = keep.tile([P, HKV * 2 * D], U8, align_bytes=64)
         v_codes = keep.tile([P, HKV * D], U32, align_bytes=64)
         v_scales = keep.tile([P, HKV * D], U8, align_bytes=64)
         w_codes = keep.tile([P, PASSES, HIDDEN], U32, align_bytes=64)
@@ -234,17 +261,17 @@ def tile_gemmaattention_pb_kernel(tc, q_rot, k_rot, v, w_o, out):
                 take(("s", unit // per))
                 for other in range(unit + 1, unit + per):
                     score(other, False)
-            n_keys = (r + 1) * ROWS
+            n_keys = keys_of(r)
             first = (unit % per) * n_keys
             scores = bank_of["s", unit // per][:, first : first + n_keys]
             g, x = divmod(unit % 8, 2)
             nc.tensor.matmul(out=scores, lhsT=qT[:, r // 2, g, 2 * x + r % 2].rearrange("p u q -> p (u q)"), rhs=kT[:, g, 0:n_keys], start=True, stop=False)
-            nc.tensor.matmul(out=scores[:, r * ROWS : n_keys], lhsT=ident_bf[:], rhs=mask_bf[:], start=False, stop=True)
+            nc.tensor.matmul(out=scores[:, r * ROWS : n_keys], lhsT=ident_bf[:], rhs=mask_bf[:, 0 : n_keys - r * ROWS], start=False, stop=True)
 
         def row_maximum(unit):
             r = block_of(unit)
             per = PER[r]
-            n_keys = (r + 1) * ROWS
+            n_keys = keys_of(r)
             first = unit % per * n_keys
             scaled = stage.tile([P, S], BF16, name="scaled", bufs=2)
             shift = stats.tile([P, 1], F32, name="shift", bufs=12)
@@ -256,12 +283,18 @@ def tile_gemmaattention_pb_kernel(tc, q_rot, k_rot, v, w_o, out):
             step, j = divmod(unit, QUAD)
             r = block_of(unit)
             per = PER[r]
-            n_keys = (r + 1) * ROWS
+            n_keys = keys_of(r)
             if j == 0:
                 rowsum_of[step] = stats.tile([P, QUAD], F32, name="rowsum")
+            if r >= LOW:
+                halves = 1
+                e_out = e_tiles[step % E_TILES][:, j * S : j * S + n_keys].rearrange("p (h k) -> p h k", h=1)
+            else:
+                halves = max(1, n_keys // P)
+                e_out = e_tiles[step % E_TILES][:, j // 2 * S : (j // 2 + 1) * S].rearrange("p (h x k) -> p h x k", h=2, x=2)[:, 0:halves, j % 2, 0 : n_keys // halves]
             nc.scalar.activation(
-                out=e_tiles[step % E_TILES][:, j * S : j * S + n_keys],
-                in_=bank_of["s", unit // per][:, unit % per * n_keys : (unit % per + 1) * n_keys],
+                out=e_out,
+                in_=bank_of["s", unit // per][:, unit % per * n_keys : (unit % per + 1) * n_keys].rearrange("p (h k) -> p h k", h=halves),
                 func=ACT.Exp,
                 bias=shift_of[unit][:],
                 scale=SCALE,
@@ -275,71 +308,74 @@ def tile_gemmaattention_pb_kernel(tc, q_rot, k_rot, v, w_o, out):
             nc.vector.reciprocal(out=rinv[:], in_=rowsum_of[step][:])
             rinv_of[step] = rinv
 
-        dirty = [set(range(RB)) for b in range(E_TILES)]
-
         def clear_e(step):
-            b = step % E_TILES
-            if step >= 0:
-                dirty[b] |= set(range(ORDER[step // 2] + 1))
-            follower = step + E_TILES
-            if follower >= STEPS:
+            if step + E_TILES >= STEPS:
                 return
-            r = ORDER[follower // 2]
-            top = RB if r >= LOW or not SKIP_UPPER or QUAD // 2 * (follower - 2 * ORDER.index(LOW - 1)) < E_BANKS else LOW
-            keys = [k for k in range(r + 1, top) if k in dirty[b]]
-            if keys:
-                e_units = e_tiles[b][:].rearrange("p (h k) -> p h k", h=QUAD)
-                nc.gpsimd.memset(e_units[:, :, keys[0] * ROWS : (keys[-1] + 1) * ROWS], 0.0)
-                dirty[b] -= set(keys)
+            r = ORDER[(step + E_TILES) // 2]
+            e_tile = e_tiles[step % E_TILES][:]
+            if LOW <= r < RB - 1:
+                nc.gpsimd.memset(e_tile.rearrange("p (j k) -> p j k", j=QUAD)[:, :, (r + 1) * ROWS : min(S, (r + 3) * ROWS)], 0.0)
+            elif r < 2:
+                halves = e_tile[:, 0 : 2 * S].rearrange("p (g h k) -> p g h k", g=2, h=2)
+                nc.gpsimd.memset(halves[:, :, 1, :], 0.0)
+                if r == 0:
+                    nc.gpsimd.memset(halves[:, :, 0, :].rearrange("p g (x k) -> p g x k", x=2)[:, :, :, ROWS:P], 0.0)
 
-        def turn_e(unit):
-            pair, j = divmod(unit, 2)
-            step, jj = divmod(unit, QUAD)
-            low_pair = pair - 4 * ORDER.index(LOW - 1)
-            if j == 0:
-                if SKIP_UPPER and low_pair >= 0:
-                    if len(e_banks) < E_BANKS:
-                        e_banks.append(take(("pin", pair)))
-                    turned_e[pair] = e_banks[low_pair % E_BANKS]
-                else:
-                    turned_e[pair] = take(("e", pair))
-                turned_e[pair] = turned_e[pair].rearrange("p (h u i) -> p h u i", h=2, u=2)
+        def turn_e(pair):
+            step, half = divmod(pair, 2)
+            low = ORDER[step // 2] < LOW
+            bank = step if low else ("half", pair)
+            if not low or half == 0:
+                turned_e[bank] = take(("e", bank)).rearrange("p (h u i) -> p h u i", h=2, u=2)
             e_words = e_tiles[step % E_TILES][:].bitcast(F32)
-            for u in range(1 if SKIP_UPPER and low_pair >= E_BANKS else 2):
-                first = (jj * 2 + u) * P
-                nc.tensor.transpose(out=turned_e[pair][:, j, u, :], in_=e_words[:, first : first + P], identity=ident_f32[:])
+            if low:
+                for u in range(2):
+                    first = (2 * half + u) * P
+                    nc.tensor.transpose(out=turned_e[bank][:, half, u, :], in_=e_words[:, first : first + P], identity=ident_f32[:])
+            else:
+                for j in range(2):
+                    for u in range(2):
+                        first = ((2 * half + j) * 2 + u) * P
+                        nc.tensor.transpose(out=turned_e[bank][:, j, u, :], in_=e_words[:, first : first + P], identity=ident_f32[:])
 
         def copy_e(pair):
             step, half = divmod(pair, 2)
-            if half == 0:
-                e_grouped_of[step] = stage.tile([P, QUAD * P * PACK], BF16, align_bytes=64, name="e_grouped", bufs=3)
-            words = e_grouped_of[step][:].bitcast(F32).rearrange("p (h i u) -> p h i u", h=QUAD, u=2)
-            copier(pair % 4 < E_V)(out=words[:, 2 * half : 2 * half + 2, :, :], in_=turned_e[pair].rearrange("p h u i -> p h i u"))
-            if ("e", pair) in bank_of:
-                give(("e", pair))
+            low = ORDER[step // 2] < LOW
+            if low and half == 0:
+                return
+            bank = step if low else ("half", pair)
+            if low or half == 0:
+                e_grouped_of[step] = stage.tile([P, 2 if low else QUAD, P * PACK], BF16, align_bytes=64, name="e_grouped", bufs=3)
+            words = e_grouped_of[step][:].rearrange("p h t -> p (h t)").bitcast(F32).rearrange("p (h i u) -> p h i u", i=P, u=2)
+            first = 0 if low else 2 * half
+            copier(pair % 4 < E_V)(out=words[:, first : first + 2, :, :], in_=turned_e[bank].rearrange("p h u i -> p h i u"))
+            give(("e", bank))
 
         def quantise_e(step):
-            e_codes = stage.tile([P, QUAD * P], U32, align_bytes=64)
-            e_scales = stage.tile([P, QUAD * P], U8, align_bytes=64)
-            nc.vector.quantize_mx(out=e_codes[:].bitcast(FP8X4), scales=e_scales[:], in_=e_grouped_of[step][:])
+            n = (2 if ORDER[step // 2] < LOW else QUAD) * P
+            e_codes = stage.tile([P, n], U32, align_bytes=64, name="e_codes")
+            e_scales = stage.tile([P, n], U8, align_bytes=64, name="e_scales")
+            nc.vector.quantize_mx(out=e_codes[:].bitcast(FP8X4), scales=e_scales[:], in_=e_grouped_of[step][:].rearrange("p h t -> p (h t)"))
             e_operand[step] = (e_codes, e_scales)
 
         def multiply_v(step):
             e_codes, e_scales = e_operand[step]
-            pv = take(("pv", step)).rearrange("p (h d) -> p h d", h=QUAD)
-            for j in range(QUAD):
-                g = 2 * (step % 2) + j // 2
+            pv = take(("pv", step))
+            low = ORDER[step // 2] < LOW
+            codes, scales, n = (pair_codes, pair_scales, 2 * D) if low else (v_codes, v_scales, D)
+            for j in range(2 if low else QUAD):
+                g = 2 * (step % 2) + (j if low else j // 2)
                 rows = slice(j * P, (j + 1) * P)
                 nc.tensor.matmul_mx(
-                    out=pv[:, j, :],
+                    out=pv[:, j * n : (j + 1) * n],
                     lhsT=e_codes[:, rows].bitcast(FP8X4),
                     lhsT_scale=e_scales[:, rows],
-                    rhs=v_codes[:, g * D : (g + 1) * D].bitcast(FP8X4),
-                    rhs_scale=v_scales[:, g * D : (g + 1) * D],
+                    rhs=codes[:, g * n : (g + 1) * n].bitcast(FP8X4),
+                    rhs_scale=scales[:, g * n : (g + 1) * n],
                     start=True,
                     stop=True,
                 )
-            pv_of[step] = pv
+            pv_of[step] = pv.rearrange("p (h d) -> p h d", h=QUAD)
 
         def normalise(step):
             o_sb = stage.tile([P, QUAD * D], BF16)
@@ -375,9 +411,26 @@ def tile_gemmaattention_pb_kernel(tc, q_rot, k_rot, v, w_o, out):
             nc.vector.quantize_mx(out=o_codes[place][:, rows].bitcast(FP8X4), scales=o_scales[place][:, rows], in_=o_grouped_of[place, gp][:])
 
         def quantise_v(piece):
-            v_grouped = keep.tile([P, HKV * D * PACK], BF16, align_bytes=64)
+            v_grouped = stage.tile([P, HKV * D * PACK], BF16, align_bytes=64, name="grouped", bufs=1)
             nc.vector.tensor_copy(out=v_grouped[:].rearrange("p (c t) -> p c t", t=PACK), in_=v_sb[:].rearrange("p u (e c) -> p c (u e)", e=2))
             nc.vector.quantize_mx(out=v_codes[:].bitcast(FP8X4), scales=v_scales[:], in_=v_grouped[:])
+
+        def group_half(piece):
+            half_grouped["in"] = stage.tile([P, HKV * D * PACK], BF16, align_bytes=64, name="grouped", bufs=1)
+            nc.vector.tensor_copy(out=half_grouped["in"][:].rearrange("p (c t) -> p c t", t=PACK), in_=half_sb[:].rearrange("p t c -> p c t"))
+
+        def quantise_half(piece):
+            nc.vector.quantize_mx(out=half_codes[:].bitcast(FP8X4), scales=half_scales[:], in_=half_grouped["in"][:])
+
+        def place_half(piece):
+            to = pair_codes[:].bitcast(I32).rearrange("p (g x d) -> p g x d", g=HKV, x=2)
+            of = half_codes[:].bitcast(I32).rearrange("p (g d) -> p g d", g=HKV)
+            for x in range(2):
+                rows = slice(x * ROWS, (x + 1) * ROWS)
+                nc.vector.tensor_copy(out=to[rows, :, x, :], in_=of[rows, :, :])
+            for x in range(2):
+                nc.vector.tensor_copy(out=pair_scales[:].bitcast(I32).rearrange("p (g x d) -> p g x d", g=HKV, x=2)[:, :, x, :],
+                                      in_=half_scales[:].bitcast(I32).rearrange("p (g d) -> p g d", g=HKV))
 
         def turn_w(piece):
             nb, rest = divmod(piece, 2 * PASSES)
@@ -407,10 +460,7 @@ def tile_gemmaattention_pb_kernel(tc, q_rot, k_rot, v, w_o, out):
             place, nb = divmod(block, N_BLOCKS)
             features = slice(nb * BANK, (nb + 1) * BANK)
             if g == 0:
-                if place == CHUNKS - 1 and nb < len(e_banks):
-                    acc_of[block] = e_banks[nb]
-                else:
-                    acc_of[block] = take(("acc", block))
+                acc_of[block] = take(("acc", block))
             rows = slice(g * P, (g + 1) * P)
             nc.tensor.matmul_mx(
                 out=acc_of[block],
@@ -431,8 +481,7 @@ def tile_gemmaattention_pb_kernel(tc, q_rot, k_rot, v, w_o, out):
             c = ORDER[2 * place] // 2
             result = results.tile([P, BANK], F32)
             copier(nb % S_V_DEN == 0)(out=result[:], in_=acc_of[block])
-            if ("acc", block) in bank_of:
-                give(("acc", block))
+            give(("acc", block))
             nc.sync.dma_start(out=out_rows[c * P : (c + 1) * P, nb * BANK : (nb + 1) * BANK], in_=result[:])
 
         by_tick = {}
@@ -464,7 +513,10 @@ def tile_gemmaattention_pb_kernel(tc, q_rot, k_rot, v, w_o, out):
         every(quantise_o, 2 * CHUNKS, lambda i: o_ready(i // 2, i % 2))
         every(quantise_w, W_PIECES, lambda w: w_tick(w) + QUANTISE_W_AT)
         due(QUANTISE_V_AT, quantise_v, 0)
-        every(turn_e, UNITS, lambda u: unit_tick(u) + TURN_E_AT)
+        due(HALF_AT, group_half, 0)
+        due(HALF_AT + 2, quantise_half, 0)
+        due(HALF_AT + 4, place_half, 0)
+        every(turn_e, UNITS // 2, lambda p: unit_tick(2 * p + 1) + TURN_E_AT)
         every(turn_o, STEPS, lambda s: step_tick(s) + TURN_O_AT)
         every(turn_w, W_PIECES, lambda w: w_tick(w) + TURN_W_AT)
         every(turn_k, HKV // 2, lambda k: TURN_K_AT[k])
@@ -476,6 +528,7 @@ def tile_gemmaattention_pb_kernel(tc, q_rot, k_rot, v, w_o, out):
         for g in range(PASSES):
             for nb in range(N_BLOCKS):
                 due(max(LAST_AT, o_ready(CHUNKS - 1, g // 2) + O_LAG), project_pass, OUT_BLOCKS - N_BLOCKS + nb, g)
+        due(TURN_W_AT + w_tick(7) + 1, load, LOADS[-1])
         for tick in sorted(by_tick):
             for fn, piece in by_tick[tick]:
                 fn(*piece)

@@ -40,6 +40,7 @@ ORDER = [7, 6, 5, 4, 3, 2, 1, 0]
 HALF_TICKS = [1, 1, 1, 1, 2, 2, 2, 2]
 PER = [4, 4, 2, 2, 1, 1, 1, 1]
 LOW = 4
+WIDE = 192
 FROM_PSUM = 1
 EXP_GAP = 1
 L_ET = 3
@@ -172,10 +173,11 @@ def tile_gemmaattention_pb_kernel(tc, q_rot, k_rot, v, w_o, out):
         nc.gpsimd.memset(mask_f32[:], 0.0)
         nc.gpsimd.affine_select(out=mask_f32[:], in_=mask_f32[:], compare_op=ALU.is_ge, fill=MASK_NEG, base=0,
                                 pattern=[[-1, P]], channel_multiplier=1)
-        mask_bf = keep.tile([P, 2 * ROWS], BF16)
-        nc.gpsimd.memset(mask_bf[:, ROWS : 2 * ROWS], MASK_NEG)
+        mask_bf = keep.tile([P, WIDE + 2 * ROWS], BF16)
+        nc.gpsimd.memset(mask_bf[:, 0:WIDE], 0.0)
+        nc.gpsimd.memset(mask_bf[:, WIDE + ROWS : WIDE + 2 * ROWS], MASK_NEG)
         for u in range(2):
-            nc.gpsimd.tensor_copy(out=mask_bf[u * ROWS : (u + 1) * ROWS, 0:ROWS], in_=mask_f32[u * ROWS : (u + 1) * ROWS, u * ROWS : (u + 1) * ROWS])
+            nc.gpsimd.tensor_copy(out=mask_bf[u * ROWS : (u + 1) * ROWS, WIDE : WIDE + ROWS], in_=mask_f32[u * ROWS : (u + 1) * ROWS, u * ROWS : (u + 1) * ROWS])
         ident_f32 = keep.tile([P, P], F32)
         make_identity(nc, ident_f32[:])
 
@@ -266,7 +268,8 @@ def tile_gemmaattention_pb_kernel(tc, q_rot, k_rot, v, w_o, out):
             scores = bank_of["s", unit // per][:, first : first + n_keys]
             g, x = divmod(unit % 8, 2)
             nc.tensor.matmul(out=scores, lhsT=qT[:, r // 2, g, 2 * x + r % 2].rearrange("p u q -> p (u q)"), rhs=kT[:, g, 0:n_keys], start=True, stop=False)
-            nc.tensor.matmul(out=scores[:, r * ROWS : n_keys], lhsT=ident_bf[:], rhs=mask_bf[:, 0 : n_keys - r * ROWS], start=False, stop=True)
+            before = WIDE if r >= LOW else 0
+            nc.tensor.matmul(out=scores[:, r * ROWS - before : n_keys], lhsT=ident_bf[:], rhs=mask_bf[:, WIDE - before : WIDE + n_keys - r * ROWS], start=False, stop=True)
 
         def row_maximum(unit):
             r = block_of(unit)

@@ -41,37 +41,42 @@ HALF_TICKS = [1, 1, 1, 1, 2, 2, 2, 2]
 PER = [4, 4, 2, 2, 1, 1, 1, 1]
 LOW = 4
 WIDE = 192
+WARM = 20
 FROM_PSUM = 1
 EXP_GAP = 1
 L_ET = 3
-R_EARLY = 1
-L_EQ = 1
+R_EARLY = 2
+L_EQ = 0
 L_QM = 3
 L_NT = 2
 L_OQ = 2
 L_WQ = 1
-TURN_Q_AHEAD = 7
-LOWQ_AHEAD = 9
+TURN_Q_AHEAD = 3
+LOWQ_AHEAD = 7
 E_V = 0
 O_V = 0
-S_V_DEN = 2
-TURN_K_AT = [-7, 1]
-QUANTISE_V_AT = 0
-TURN_W_AT = 4
+S_V_DEN = 4
+TURN_K_AT = [-7, -1, 2, 3]
+QUANTISE_V_AT = 8
+TURN_W_AT = 3
 PROJECT_GAP = 2
-STORE_LAG = 2
+STORE_LAG = 1
 O_LAG = 4
-W_NUM = 4
+W_NUM = 3
 W_DEN = 4
 P_GRID = 4
 P_GRID2 = 4
-P_SWITCH = 45
+P_SWITCH = 44
 E_TILES = 4
-W_V_DEN = 7
-W_V_OFF = 1
-Q_V = True
-LOADS = ["k", "q0", "v", "w0", "q1", "w1", "half", "q2", "w2", "q3", "w3"]
-HALF_AT = 14
+W_V_DEN = 8
+W_V_OFF = 4
+Q_V_DEN = 1
+Q_V_OFF = 2
+K_V = [True, False, True, False]
+Q0_AT = [-7, 0, 1, 3]
+SPLIT = 4
+LOADS = ["k", "q0a", "q0b", "w0", "v", "q1", "w1", "half", "q2", "w2", "q3", "w3"]
+HALF_AT = 15
 HALF_EVERY = 2
 
 
@@ -112,7 +117,10 @@ QUANTISE_W_AT = COPY_W_AT + L_WQ
 
 
 def q_tick(piece):
-    return unit_tick(16 * (piece // 2) + 4 * (piece % 2)) - (TURN_Q_AHEAD if piece < 4 else LOWQ_AHEAD)
+    place, g = divmod(piece, HKV)
+    if place == 0:
+        return Q0_AT[g]
+    return unit_tick(16 * place + 2 * g) - (TURN_Q_AHEAD if place == 1 else LOWQ_AHEAD)
 
 
 def w_tick(piece):
@@ -197,7 +205,8 @@ def tile_gemmaattention_pb_kernel(tc, q_rot, k_rot, v, w_o, out):
                     nc.sync.dma_start(out=half_sb[x * ROWS : (x + 1) * ROWS, :, :].rearrange("p (u e) n -> p u (e n)", u=2), in_=v[:, 0 : 4 * ROWS].rearrange("b (u p e) g d -> p (b u) (e g d)", u=2, e=2))
             elif what[0] == "q":
                 c = ORDER[2 * int(what[1])] // 2
-                nc.sync.dma_start(out=q_sb[c][:], in_=q_rows[c * P : (c + 1) * P, :])
+                part = slice(0, H * D) if len(what) == 2 else (slice(0, SPLIT * D) if what[2] == "a" else slice(SPLIT * D, H * D))
+                nc.sync.dma_start(out=q_sb[c][:, part], in_=q_rows[c * P : (c + 1) * P, part])
             else:
                 for nt in range(4 * int(what[1]), 4 * int(what[1]) + 4):
                     w_sb[nt] = weights.tile([P, HIDDEN], BF16, name="w_sb")
@@ -227,31 +236,33 @@ def tile_gemmaattention_pb_kernel(tc, q_rot, k_rot, v, w_o, out):
         def copier(on_vector):
             return nc.vector.tensor_copy if on_vector else nc.scalar.copy
 
-        def turn_k(piece):
-            turned_k[piece] = take(("k", piece)).bitcast(BF16).rearrange("p (g t j) -> p g t j", g=2, t=CHUNKS)
-            for j in range(2):
-                g = 2 * piece + j
-                for t in range(CHUNKS):
-                    nc.tensor.transpose(out=turned_k[piece][:, j, t, :], in_=k_sb[:, t, g * D : (g + 1) * D], identity=ident_bf[:])
+        warm_bank = take("warm")
+        for i in range(WARM):
+            nc.tensor.matmul(out=warm_bank[:, 0:P], lhsT=ident_bf[:], rhs=ident_bf[:], start=True, stop=True)
+        give("warm")
 
-        def copy_k(piece):
-            copier(piece == 0)(out=kT[:, 2 * piece : 2 * piece + 2, :], in_=turned_k[piece].rearrange("p g t j -> p g (t j)"))
-            give(("k", piece))
+        def turn_k(g):
+            turned_k[g] = take(("k", g)).bitcast(BF16)[:, 0:S].rearrange("p (t j) -> p t j", t=CHUNKS)
+            for t in range(CHUNKS):
+                nc.tensor.transpose(out=turned_k[g][:, t, :], in_=k_sb[:, t, g * D : (g + 1) * D], identity=ident_bf[:])
+
+        def copy_k(g):
+            copier(K_V[g])(out=kT[:, g, :], in_=turned_k[g].rearrange("p t j -> p (t j)"))
+            give(("k", g))
 
         def turn_q(piece):
-            place, half = divmod(piece, 2)
+            place, g = divmod(piece, HKV)
             c = ORDER[2 * place] // 2
-            turned_q[piece] = take(("q", piece)).bitcast(BF16).rearrange("p (g h i) -> p g h i", g=2, i=P)
-            for j in range(8):
-                h = half * 8 + j
-                nc.tensor.transpose(out=turned_q[piece][:, j // 4, j % 4, :], in_=q_sb[c][:, h * D : (h + 1) * D], identity=ident_bf[:])
+            turned_q[piece] = take(("q", piece)).bitcast(BF16)[:, 0 : REP * P].rearrange("p (h i) -> p h i", i=P)
+            for j in range(REP):
+                h = REP * g + j
+                nc.tensor.transpose(out=turned_q[piece][:, j, :], in_=q_sb[c][:, h * D : (h + 1) * D], identity=ident_bf[:])
 
         def copy_q(piece):
-            place, half = divmod(piece, 2)
+            place, g = divmod(piece, HKV)
             c = ORDER[2 * place] // 2
-            for j in range(2):
-                copier(Q_V and piece % 2 == 0)(out=qT[:, c, 2 * half + j].rearrange("p m u q -> p u m q"),
-                                      in_=turned_q[piece][:, j].rearrange("p (u x) (r q) -> p u (x r) q", u=2, r=2))
+            copier(piece % Q_V_DEN == Q_V_OFF)(out=qT[:, c, g].rearrange("p m u q -> p u m q"),
+                                         in_=turned_q[piece].rearrange("p (u x) (r q) -> p u (x r) q", u=2, r=2))
             give(("q", piece))
 
         def score(unit, lead=True):
@@ -483,7 +494,7 @@ def tile_gemmaattention_pb_kernel(tc, q_rot, k_rot, v, w_o, out):
             place, nb = divmod(block, N_BLOCKS)
             c = ORDER[2 * place] // 2
             result = results.tile([P, BANK], F32)
-            copier(nb % S_V_DEN == 0)(out=result[:], in_=acc_of[block])
+            copier(nb % (2 if place == CHUNKS - 1 else S_V_DEN) == 0)(out=result[:], in_=acc_of[block])
             give(("acc", block))
             nc.sync.dma_start(out=out_rows[c * P : (c + 1) * P, nb * BANK : (nb + 1) * BANK], in_=result[:])
 
@@ -505,8 +516,8 @@ def tile_gemmaattention_pb_kernel(tc, q_rot, k_rot, v, w_o, out):
         every(normalise, STEPS, lambda s: step_tick(s) + NORMALISE_AT)
         every(copy_o, STEPS, lambda s: step_tick(s) + COPY_O_AT)
         every(copy_w, W_PIECES, lambda w: w_tick(w) + COPY_W_AT)
-        every(copy_k, HKV // 2, lambda k: TURN_K_AT[k] + FROM_PSUM)
-        every(copy_q, 2 * CHUNKS, lambda q: q_tick(q) + FROM_PSUM)
+        every(copy_k, HKV, lambda k: TURN_K_AT[k] + FROM_PSUM)
+        every(copy_q, 4 * CHUNKS, lambda q: q_tick(q) + FROM_PSUM)
         for block in range(OUT_BLOCKS - N_BLOCKS):
             due(PROJECT_TICK[block] + STORE_LAG, store, block)
         for nb in range(N_BLOCKS):
@@ -522,8 +533,8 @@ def tile_gemmaattention_pb_kernel(tc, q_rot, k_rot, v, w_o, out):
         every(turn_e, UNITS // 2, lambda p: unit_tick(2 * p + 1) + TURN_E_AT)
         every(turn_o, STEPS, lambda s: step_tick(s) + TURN_O_AT)
         every(turn_w, W_PIECES, lambda w: w_tick(w) + TURN_W_AT)
-        every(turn_k, HKV // 2, lambda k: TURN_K_AT[k])
-        every(turn_q, 2 * CHUNKS, q_tick)
+        every(turn_k, HKV, lambda k: TURN_K_AT[k])
+        every(turn_q, 4 * CHUNKS, q_tick)
         every(score, UNITS, lambda u: unit_tick(u))
         every(multiply_v, STEPS, lambda s: step_tick(s) + MULTIPLY_V_AT)
         for block in range(OUT_BLOCKS - N_BLOCKS):

@@ -40,43 +40,43 @@ ORDER = [7, 6, 5, 4, 3, 2, 1, 0]
 HALF_TICKS = [1, 1, 1, 1, 2, 2, 2, 2]
 PER = [4, 4, 2, 2, 1, 1, 1, 1]
 LOW = 4
-WIDE = 192
 WARM = 20
 FROM_PSUM = 1
 EXP_GAP = 1
-L_ET = 3
+L_ET = 4
 R_EARLY = 2
-L_EQ = 0
-L_QM = 3
+L_EQ = 1
+L_QM = 2
 L_NT = 2
-L_OQ = 2
-L_WQ = 1
-TURN_Q_AHEAD = 3
+L_OQ = 0
+L_WQ = 2
+TURN_Q_AHEAD = 8
 LOWQ_AHEAD = 7
 E_V = 0
+O_V_LATE = 0
 O_V = 0
-S_V_DEN = 4
-TURN_K_AT = [-7, -1, 2, 3]
+S_V_DEN = 1
+TURN_K_AT = [-7, -1, 2, 4]
 QUANTISE_V_AT = 8
 TURN_W_AT = 3
 PROJECT_GAP = 2
 STORE_LAG = 1
 O_LAG = 4
-W_NUM = 3
+W_NUM = 4
 W_DEN = 4
 P_GRID = 4
-P_GRID2 = 4
-P_SWITCH = 44
+P_GRID2 = 2
+P_SWITCH = 45
 E_TILES = 4
-W_V_DEN = 8
-W_V_OFF = 4
-Q_V_DEN = 1
+W_V_DEN = 7
+W_V_OFF = 1
+Q_V_DEN = 3
 Q_V_OFF = 2
 K_V = [True, False, True, False]
-Q0_AT = [-7, 0, 1, 3]
+Q0_AT = [-7, 1, 2, 4]
 SPLIT = 4
 LOADS = ["k", "q0a", "q0b", "w0", "v", "q1", "w1", "half", "q2", "w2", "q3", "w3"]
-HALF_AT = 15
+HALF_AT = 17
 HALF_EVERY = 2
 
 
@@ -181,11 +181,10 @@ def tile_gemmaattention_pb_kernel(tc, q_rot, k_rot, v, w_o, out):
         nc.gpsimd.memset(mask_f32[:], 0.0)
         nc.gpsimd.affine_select(out=mask_f32[:], in_=mask_f32[:], compare_op=ALU.is_ge, fill=MASK_NEG, base=0,
                                 pattern=[[-1, P]], channel_multiplier=1)
-        mask_bf = keep.tile([P, WIDE + 2 * ROWS], BF16)
-        nc.gpsimd.memset(mask_bf[:, 0:WIDE], 0.0)
-        nc.gpsimd.memset(mask_bf[:, WIDE + ROWS : WIDE + 2 * ROWS], MASK_NEG)
+        mask_bf = keep.tile([P, 2 * ROWS], BF16)
+        nc.gpsimd.memset(mask_bf[:, ROWS : 2 * ROWS], MASK_NEG)
         for u in range(2):
-            nc.gpsimd.tensor_copy(out=mask_bf[u * ROWS : (u + 1) * ROWS, WIDE : WIDE + ROWS], in_=mask_f32[u * ROWS : (u + 1) * ROWS, u * ROWS : (u + 1) * ROWS])
+            nc.gpsimd.tensor_copy(out=mask_bf[u * ROWS : (u + 1) * ROWS, 0:ROWS], in_=mask_f32[u * ROWS : (u + 1) * ROWS, u * ROWS : (u + 1) * ROWS])
         ident_f32 = keep.tile([P, P], F32)
         make_identity(nc, ident_f32[:])
 
@@ -231,7 +230,7 @@ def tile_gemmaattention_pb_kernel(tc, q_rot, k_rot, v, w_o, out):
         o_scales = [keep.tile([P, PASSES * P], U8, name="o_scales%d" % i, align_bytes=64) for i in range(CHUNKS)]
         turned_k, turned_q, shift_of, rowsum_of, turned_e, e_grouped_of, e_operand = {}, {}, {}, {}, {}, {}, {}
         rinv_of, pv_of, o_sb_of, turned_o, o_grouped_of = {}, {}, {}, {}, {}
-        turned_w, w_grouped_of, acc_of = {}, {}, {}
+        turned_w, w_grouped_of, acc_of, rowmax_of = {}, {}, {}, {}
 
         def copier(on_vector):
             return nc.vector.tensor_copy if on_vector else nc.scalar.copy
@@ -279,19 +278,32 @@ def tile_gemmaattention_pb_kernel(tc, q_rot, k_rot, v, w_o, out):
             scores = bank_of["s", unit // per][:, first : first + n_keys]
             g, x = divmod(unit % 8, 2)
             nc.tensor.matmul(out=scores, lhsT=qT[:, r // 2, g, 2 * x + r % 2].rearrange("p u q -> p (u q)"), rhs=kT[:, g, 0:n_keys], start=True, stop=False)
-            before = WIDE if r >= LOW else 0
-            nc.tensor.matmul(out=scores[:, r * ROWS - before : n_keys], lhsT=ident_bf[:], rhs=mask_bf[:, WIDE - before : WIDE + n_keys - r * ROWS], start=False, stop=True)
+            nc.tensor.matmul(out=scores[:, r * ROWS : n_keys], lhsT=ident_bf[:], rhs=mask_bf[:, 0 : n_keys - r * ROWS], start=False, stop=True)
 
         def row_maximum(unit):
             r = block_of(unit)
             per = PER[r]
             n_keys = keys_of(r)
-            first = unit % per * n_keys
-            scaled = stage.tile([P, S], BF16, name="scaled", bufs=2)
-            shift = stats.tile([P, 1], F32, name="shift", bufs=12)
-            nc.vector.tensor_scalar(out=scaled[:, 0:n_keys], in0=bank_of["s", unit // per][:, first : first + n_keys],
-                                    scalar1=-SCALE, scalar2=3.0e38, op0=ALU.mult, op1=ALU.min, accum_out=shift[:])
-            shift_of[unit] = shift
+            scores = bank_of["s", unit // per]
+            if r >= LOW:
+                scaled = stage.tile([P, S], BF16, name="scaled", bufs=2)
+                shift = stats.tile([P, 1], F32, name="shift1")
+                nc.vector.tensor_scalar(out=scaled[:, 0:n_keys], in0=scores[:, 0:n_keys],
+                                        scalar1=-SCALE, scalar2=3.0e38, op0=ALU.mult, op1=ALU.min, accum_out=shift[:])
+                shift_of[unit] = shift[:]
+            elif unit % per == 0:
+                rowmax = stats.tile([P, per], F32, name="rowmax%d" % per)
+                nc.vector.tensor_reduce(out=rowmax[:], in_=scores[:, 0 : per * n_keys].rearrange("p (h k) -> p h k", h=per), axis=AXIS.X, op=ALU.max)
+                rowmax_of[unit] = rowmax
+
+        def scale_maximum(unit):
+            r = block_of(unit)
+            per = PER[r]
+            if r < LOW and unit % per == 0:
+                shift = stats.tile([P, per], F32, name="shift%d" % per)
+                nc.scalar.activation(out=shift[:], in_=rowmax_of[unit][:], func=ACT.Copy, scale=-SCALE)
+                for j in range(per):
+                    shift_of[unit + j] = shift[:, j : j + 1]
 
         def exponential(unit):
             step, j = divmod(unit, QUAD)
@@ -310,7 +322,7 @@ def tile_gemmaattention_pb_kernel(tc, q_rot, k_rot, v, w_o, out):
                 out=e_out,
                 in_=bank_of["s", unit // per][:, unit % per * n_keys : (unit % per + 1) * n_keys].rearrange("p (h k) -> p h k", h=halves),
                 func=ACT.Exp,
-                bias=shift_of[unit][:],
+                bias=shift_of[unit],
                 scale=SCALE,
                 accum_out=rowsum_of[step][:, j : j + 1],
             )
@@ -416,7 +428,7 @@ def tile_gemmaattention_pb_kernel(tc, q_rot, k_rot, v, w_o, out):
             if rest < 2:
                 o_grouped_of[place, gp] = stage.tile([P, 2 * P * PACK], BF16, align_bytes=64, name="o_grouped")
             words = o_grouped_of[place, gp][:].bitcast(F32).rearrange("p (g r q u) -> p g r q u", g=2, r=2, u=2)
-            copier(step % 4 < O_V)(out=words[:, :, r % 2, :, :], in_=turned_o[step].rearrange("p g (u q) -> p g q u", u=2))
+            copier(step % 4 < (O_V if step < STEPS // 2 else O_V_LATE))(out=words[:, :, r % 2, :, :], in_=turned_o[step].rearrange("p g (u q) -> p g q u", u=2))
             give(("o", step))
 
         def quantise_o(piece):
@@ -523,6 +535,7 @@ def tile_gemmaattention_pb_kernel(tc, q_rot, k_rot, v, w_o, out):
         for nb in range(N_BLOCKS):
             due(o_ready(CHUNKS - 1, 1) + O_LAG + 1, store, OUT_BLOCKS - N_BLOCKS + nb)
         every(exponential, UNITS, lambda u: unit_tick(u) + EXP_AT)
+        every(scale_maximum, UNITS, lambda u: unit_tick(u) + MAX_AT)
         every(quantise_e, STEPS, lambda s: step_tick(s) + QUANTISE_E_AT)
         every(quantise_o, 2 * CHUNKS, lambda i: o_ready(i // 2, i % 2))
         every(quantise_w, W_PIECES, lambda w: w_tick(w) + QUANTISE_W_AT)

@@ -23,130 +23,108 @@ HIDDEN = 2048
 PACK = 4
 K_PASS = P * PACK
 BANK = 512
+BANKS = 8
 CHUNKS = S // P
-N_BLOCKS = HIDDEN // BANK
-PASSES = HIDDEN // K_PASS
-ROWS = 64
-RB = S // ROWS
-UNITS = 8 * RB
+STRIP = 64
+STRIPS = S // STRIP
+LOWER = STRIPS // 2
+UNITS_PER_STRIP = 2 * HKV
+UNITS = UNITS_PER_STRIP * STRIPS
 QUAD = 4
 STEPS = UNITS // QUAD
-OUT_BLOCKS = CHUNKS * N_BLOCKS
-W_PIECES = 2 * N_BLOCKS * PASSES
+PAIRS = UNITS // 2
+SLABS = HIDDEN // BANK
+PASSES = HIDDEN // K_PASS
+BLOCKS = CHUNKS * SLABS
+W_PIECES = 2 * SLABS * PASSES
 SCALE = D**-0.5
 MASK_NEG = -2.3819763e38
+HUGE = 3.0e38
 
-ORDER = [7, 6, 5, 4, 3, 2, 1, 0]
+CHUNK_ORDER = [2, 1, 3, 0]
+STRIP_ORDER = [2 * c + i for c in CHUNK_ORDER for i in (1, 0)]
+UNITS_PER_BANK = [4, 4, 2, 2, 1, 1, 1, 1]
 HALF_TICKS = [1, 1, 1, 1, 2, 2, 2, 2]
-PER = [4, 4, 2, 2, 1, 1, 1, 1]
-LOW = 4
-WARM = 20
-FROM_PSUM = 1
-EXP_GAP = 1
-L_ET = 4
-R_EARLY = 2
-L_EQ = 1
-L_QM = 2
-L_NT = 2
-L_OQ = 0
-L_WQ = 2
-TURN_Q_AHEAD = 8
-LOWQ_AHEAD = 7
-E_V = 0
-O_V_LATE = 0
-O_V = 0
-S_V_DEN = 1
-TURN_K_AT = [-7, -1, 2, 4]
-QUANTISE_V_AT = 8
-TURN_W_AT = 3
-PROJECT_GAP = 2
-STORE_LAG = 1
-O_LAG = 4
-W_NUM = 4
-W_DEN = 4
-P_GRID = 4
-P_GRID2 = 2
-P_SWITCH = 45
+
 E_TILES = 4
-W_V_DEN = 7
-W_V_OFF = 1
-Q_V_DEN = 3
-Q_V_OFF = 2
-K_V = [True, False, True, False]
-Q0_AT = [-7, 1, 2, 4]
-SPLIT = 4
-LOADS = ["k", "q0a", "q0b", "w0", "v", "q1", "w1", "half", "q2", "w2", "q3", "w3"]
-HALF_AT = 17
-HALF_EVERY = 2
+WARM_UP = 20
 
 
-def block_of(unit):
-    return ORDER[unit // 8]
-
-
-def unit_tick(unit):
-    place, rest = divmod(unit, 8)
-    return (sum(8 * HALF_TICKS[r] for r in ORDER[:place]) + rest * HALF_TICKS[ORDER[place]]) // 2
+def strip_of(unit):
+    return STRIP_ORDER[unit // UNITS_PER_STRIP]
 
 
 def keys_of(r):
-    return S // 2 if r == 2 else (r + 1) * ROWS
+    return 2 * P if r == 2 else (r + 1) * STRIP
 
 
-def width(r):
-    return S if r >= LOW else S // 2
+def unit_tick(unit):
+    place, rest = divmod(unit, UNITS_PER_STRIP)
+    before = sum(UNITS_PER_STRIP * HALF_TICKS[r] for r in STRIP_ORDER[:place])
+    return (before + rest * HALF_TICKS[STRIP_ORDER[place]]) // 2
+
+
+def pair_tick(pair):
+    return unit_tick(2 * pair + 1)
 
 
 def step_tick(step):
     return unit_tick(QUAD * step + QUAD - 1)
 
 
+FROM_PSUM = 1
+FROM_SBUF = 3
 MAX_AT = FROM_PSUM
-EXP_AT = MAX_AT + EXP_GAP
-TURN_E_AT = EXP_AT + L_ET
+EXP_AT = MAX_AT + 1
+TURN_E_AT = EXP_AT + FROM_SBUF
+CLEAR_E_AT = TURN_E_AT + 1
 COPY_E_AT = TURN_E_AT + FROM_PSUM
-QUANTISE_E_AT = COPY_E_AT + L_EQ
-MULTIPLY_V_AT = QUANTISE_E_AT + L_QM
+QUANTISE_E_AT = COPY_E_AT
+MULTIPLY_V_AT = QUANTISE_E_AT + FROM_SBUF
 NORMALISE_AT = MULTIPLY_V_AT + FROM_PSUM
-RECIPROCAL_AT = NORMALISE_AT - R_EARLY
-TURN_O_AT = NORMALISE_AT + L_NT
+RECIPROCAL_AT = NORMALISE_AT - 2
+TURN_O_AT = NORMALISE_AT + 2
 COPY_O_AT = TURN_O_AT + FROM_PSUM
-QUANTISE_O_AT = COPY_O_AT + L_OQ
+QUANTISE_O_AT = COPY_O_AT
+TURN_W_AT = 3
 COPY_W_AT = TURN_W_AT + FROM_PSUM
-QUANTISE_W_AT = COPY_W_AT + L_WQ
+QUANTISE_W_AT = COPY_W_AT + 1
+LAST_W_LOAD_AT = TURN_W_AT + 2 * PASSES
+QUANTISE_V_AT = step_tick(0) + MULTIPLY_V_AT - FROM_SBUF - 1
+PLACE_PAIR_AT = step_tick(STEPS // CHUNKS) + MULTIPLY_V_AT - FROM_SBUF
+QUANTISE_PAIR_AT = PLACE_PAIR_AT - 2
+GROUP_PAIR_AT = QUANTISE_PAIR_AT - 2
+SCORE_TICKS = sum(UNITS_PER_STRIP * HALF_TICKS[r] for r in STRIP_ORDER) // 2
 
 
-def q_tick(piece):
+def turn_q_tick(piece):
     place, g = divmod(piece, HKV)
-    if place == 0:
-        return Q0_AT[g]
-    return unit_tick(16 * place + 2 * g) - (TURN_Q_AHEAD if place == 1 else LOWQ_AHEAD)
+    return unit_tick(2 * UNITS_PER_STRIP * place + 2 * g) - (FROM_SBUF if place == 0 else 2 * FROM_SBUF)
 
 
-def w_tick(piece):
-    return piece * W_NUM // W_DEN
+def turn_k_tick(g):
+    return turn_q_tick(g)
 
 
-def o_ready(place, gp):
-    return QUANTISE_O_AT + step_tick(4 * place + 2 + gp)
-
-
-def w_ready(nb):
-    return QUANTISE_W_AT + w_tick(8 * nb + 7)
+def quantise_o_tick(half):
+    place, pair_of_g = divmod(half, 2)
+    return QUANTISE_O_AT + step_tick(4 * place + 2 + pair_of_g)
 
 
 def project_ticks():
+    ready = {}
+    for block in range(BLOCKS - SLABS):
+        place, slab = divmod(block, SLABS)
+        ready[block] = max(quantise_o_tick(2 * place + 1), QUANTISE_W_AT + 2 * PASSES * (slab + 1) - 1)
     ticks = {}
-    tick = -100
-    ready = {b: max(o_ready(b // N_BLOCKS, 1), w_ready(b % N_BLOCKS)) for b in range(OUT_BLOCKS - N_BLOCKS)}
+    free = 0
     for block in sorted(ready, key=lambda b: (ready[b], b)):
-        tick = max(tick + (P_GRID if tick < P_SWITCH else P_GRID2), ready[block] + PROJECT_GAP)
-        ticks[block] = tick
+        ticks[block] = max(free, ready[block])
+        free = ticks[block] + (4 if ticks[block] <= SCORE_TICKS else 2)
     return ticks
 
 
 PROJECT_TICK = project_ticks()
-LAST_AT = MULTIPLY_V_AT + step_tick(STEPS - 1)
 
 FLOPS = 2 * H * S * S * D * 2 + 2 * S * HIDDEN * HIDDEN
 
@@ -164,7 +142,8 @@ def tile_gemmaattention_pb_kernel(tc, q_rot, k_rot, v, w_o, out):
         results = ctx.enter_context(tc.tile_pool(name="results", bufs=5))
         weights = ctx.enter_context(tc.tile_pool(name="weights", bufs=12))
         psum = ctx.enter_context(tc.psum_pool(name="psum", bufs=1))
-        free_banks = [psum.tile([P, BANK], F32, name="bank%d" % b) for b in range(8)]
+
+        free_banks = [psum.tile([P, BANK], F32, name="bank%d" % b) for b in range(BANKS)]
         bank_of = {}
 
         def take(owner):
@@ -175,159 +154,208 @@ def tile_gemmaattention_pb_kernel(tc, q_rot, k_rot, v, w_o, out):
             free_banks.append(bank_of.pop(owner))
 
         e_tiles = [keep.tile([P, QUAD * S], BF16, name="e_sb%d" % b) for b in range(E_TILES)]
+
         ident_bf = keep.tile([P, P], BF16)
         make_identity(nc, ident_bf[:])
-        mask_f32 = keep.tile([P, P], F32)
-        nc.gpsimd.memset(mask_f32[:], 0.0)
-        nc.gpsimd.affine_select(out=mask_f32[:], in_=mask_f32[:], compare_op=ALU.is_ge, fill=MASK_NEG, base=0,
-                                pattern=[[-1, P]], channel_multiplier=1)
-        mask_bf = keep.tile([P, 2 * ROWS], BF16)
-        nc.gpsimd.memset(mask_bf[:, ROWS : 2 * ROWS], MASK_NEG)
+        causal = keep.tile([P, P], F32)
+        nc.gpsimd.memset(causal[:], 0.0)
+        nc.gpsimd.affine_select(
+            out=causal[:],
+            in_=causal[:],
+            compare_op=ALU.is_ge,
+            fill=MASK_NEG,
+            base=0,
+            pattern=[[-1, P]],
+            channel_multiplier=1,
+        )
+        mask = keep.tile([P, 2 * STRIP], BF16)
+        nc.gpsimd.memset(mask[:, STRIP : 2 * STRIP], MASK_NEG)
         for u in range(2):
-            nc.gpsimd.tensor_copy(out=mask_bf[u * ROWS : (u + 1) * ROWS, 0:ROWS], in_=mask_f32[u * ROWS : (u + 1) * ROWS, u * ROWS : (u + 1) * ROWS])
+            half = slice(u * STRIP, (u + 1) * STRIP)
+            nc.gpsimd.tensor_copy(out=mask[half, 0:STRIP], in_=causal[half, half])
         ident_f32 = keep.tile([P, P], F32)
         make_identity(nc, ident_f32[:])
 
         k_sb = keep.tile([P, CHUNKS, HKV * D], BF16)
         q_sb = [keep.tile([P, H * D], BF16, name="q_sb%d" % c) for c in range(CHUNKS)]
-        v_sb = keep.tile([P, 2, 2 * HKV * D], BF16)
-        half_sb = keep.tile([P, PACK, HKV * D], BF16)
+        v_sb = keep.tile([P, PACK, HKV * D], BF16)
+        pair_sb = keep.tile([P, PACK, HKV * D], BF16)
         w_sb = {}
 
-        def load(what):
-            if what == "k":
-                nc.sync.dma_start(out=k_sb[:], in_=k_rot.rearrange("b (t p) g d -> p (b t) (g d)", p=P))
-            elif what == "v":
-                nc.sync.dma_start(out=v_sb[:], in_=v.rearrange("b (u p e) g d -> p (b u) (e g d)", u=2, e=2))
-            elif what == "half":
-                for x in range(2):
-                    nc.sync.dma_start(out=half_sb[x * ROWS : (x + 1) * ROWS, :, :].rearrange("p (u e) n -> p u (e n)", u=2), in_=v[:, 0 : 4 * ROWS].rearrange("b (u p e) g d -> p (b u) (e g d)", u=2, e=2))
-            elif what[0] == "q":
-                c = ORDER[2 * int(what[1])] // 2
-                part = slice(0, H * D) if len(what) == 2 else (slice(0, SPLIT * D) if what[2] == "a" else slice(SPLIT * D, H * D))
-                nc.sync.dma_start(out=q_sb[c][:, part], in_=q_rows[c * P : (c + 1) * P, part])
-            else:
-                for nt in range(4 * int(what[1]), 4 * int(what[1]) + 4):
-                    w_sb[nt] = weights.tile([P, HIDDEN], BF16, name="w_sb")
-                    nc.sync.dma_start(out=w_sb[nt][:], in_=w_o[nt * P : (nt + 1) * P, :])
+        def load_q(place, heads):
+            c = CHUNK_ORDER[place]
+            columns = slice(heads.start * D, heads.stop * D)
+            nc.sync.dma_start(out=q_sb[c][:, columns], in_=q_rows[c * P : (c + 1) * P, columns])
 
-        for what in LOADS[:-1]:
-            load(what)
+        def load_w(slab):
+            for nt in range(4 * slab, 4 * slab + 4):
+                w_sb[nt] = weights.tile([P, HIDDEN], BF16, name="w_sb")
+                nc.sync.dma_start(out=w_sb[nt][:], in_=w_o[nt * P : (nt + 1) * P, :])
+
+        nc.sync.dma_start(out=k_sb[:], in_=k_rot.rearrange("b (t p) g d -> p (b t) (g d)", p=P))
+        load_q(0, slice(0, REP))
+        load_q(0, slice(REP, H))
+        load_w(0)
+        nc.sync.dma_start(
+            out=v_sb[:].rearrange("p (u e) n -> p u (e n)", u=2),
+            in_=v.rearrange("b (u p e) g d -> p (b u) (e g d)", u=2, e=2),
+        )
+        load_q(1, slice(0, H))
+        load_w(1)
+        for x in range(2):
+            nc.sync.dma_start(
+                out=pair_sb[x * STRIP : (x + 1) * STRIP, :, :].rearrange("p (u e) n -> p u (e n)", u=2),
+                in_=v[:, 0 : 2 * P].rearrange("b (u p e) g d -> p (b u) (e g d)", u=2, e=2),
+            )
+        load_q(2, slice(0, H))
+        load_w(2)
+        load_q(3, slice(0, H))
 
         kT = keep.tile([P, HKV, S], BF16)
-        qT = keep.tile([P, CHUNKS, HKV, 4, 2, ROWS], BF16)
-        pair_codes = keep.tile([P, HKV * 2 * D], U32, align_bytes=64)
-        nc.gpsimd.memset(pair_codes[:].bitcast(I32), 0)
-        half_codes = keep.tile([P, HKV * D], U32, align_bytes=64)
-        half_scales = keep.tile([P, HKV * D], U8, align_bytes=64)
-        half_grouped = {}
-        pair_scales = keep.tile([P, HKV * 2 * D], U8, align_bytes=64)
+        qT = keep.tile([P, CHUNKS, HKV, 4, 2, STRIP], BF16)
         v_codes = keep.tile([P, HKV * D], U32, align_bytes=64)
         v_scales = keep.tile([P, HKV * D], U8, align_bytes=64)
+        once_codes = keep.tile([P, HKV * D], U32, align_bytes=64)
+        once_scales = keep.tile([P, HKV * D], U8, align_bytes=64)
+        pair_codes = keep.tile([P, HKV * 2 * D], U32, align_bytes=64)
+        pair_scales = keep.tile([P, HKV * 2 * D], U8, align_bytes=64)
+        nc.gpsimd.memset(pair_codes[:].bitcast(I32), 0)
         w_codes = keep.tile([P, PASSES, HIDDEN], U32, align_bytes=64)
         w_scales = keep.tile([P, PASSES, HIDDEN], U8, align_bytes=64)
         o_codes = [keep.tile([P, PASSES * P], U32, name="o_codes%d" % i, align_bytes=64) for i in range(CHUNKS)]
         o_scales = [keep.tile([P, PASSES * P], U8, name="o_scales%d" % i, align_bytes=64) for i in range(CHUNKS)]
-        turned_k, turned_q, shift_of, rowsum_of, turned_e, e_grouped_of, e_operand = {}, {}, {}, {}, {}, {}, {}
-        rinv_of, pv_of, o_sb_of, turned_o, o_grouped_of = {}, {}, {}, {}, {}
-        turned_w, w_grouped_of, acc_of, rowmax_of = {}, {}, {}, {}
+        turned_k, turned_q, rowmax_of, shift_of, rowsum_of, rinv_of = {}, {}, {}, {}, {}, {}
+        turned_e, e_grouped_of, e_operand, pv_of, o_sb_of, turned_o, o_grouped_of = {}, {}, {}, {}, {}, {}, {}
+        pair_grouped_of, turned_w, w_grouped_of, acc_of = {}, {}, {}, {}
 
         def copier(on_vector):
             return nc.vector.tensor_copy if on_vector else nc.scalar.copy
 
-        warm_bank = take("warm")
-        for i in range(WARM):
-            nc.tensor.matmul(out=warm_bank[:, 0:P], lhsT=ident_bf[:], rhs=ident_bf[:], start=True, stop=True)
-        give("warm")
+        def warm_up():
+            bank = take("warm-up")
+            for i in range(WARM_UP):
+                nc.tensor.matmul(out=bank[:, 0:P], lhsT=ident_bf[:], rhs=ident_bf[:], start=True, stop=True)
+            give("warm-up")
 
         def turn_k(g):
             turned_k[g] = take(("k", g)).bitcast(BF16)[:, 0:S].rearrange("p (t j) -> p t j", t=CHUNKS)
             for t in range(CHUNKS):
-                nc.tensor.transpose(out=turned_k[g][:, t, :], in_=k_sb[:, t, g * D : (g + 1) * D], identity=ident_bf[:])
+                nc.tensor.transpose(
+                    out=turned_k[g][:, t, :], in_=k_sb[:, t, g * D : (g + 1) * D], identity=ident_bf[:]
+                )
 
         def copy_k(g):
-            copier(K_V[g])(out=kT[:, g, :], in_=turned_k[g].rearrange("p t j -> p (t j)"))
+            copier(g % 2 == 0)(out=kT[:, g, :], in_=turned_k[g].rearrange("p t j -> p (t j)"))
             give(("k", g))
 
         def turn_q(piece):
             place, g = divmod(piece, HKV)
-            c = ORDER[2 * place] // 2
             turned_q[piece] = take(("q", piece)).bitcast(BF16)[:, 0 : REP * P].rearrange("p (h i) -> p h i", i=P)
             for j in range(REP):
                 h = REP * g + j
-                nc.tensor.transpose(out=turned_q[piece][:, j, :], in_=q_sb[c][:, h * D : (h + 1) * D], identity=ident_bf[:])
+                nc.tensor.transpose(
+                    out=turned_q[piece][:, j, :],
+                    in_=q_sb[CHUNK_ORDER[place]][:, h * D : (h + 1) * D],
+                    identity=ident_bf[:],
+                )
 
         def copy_q(piece):
             place, g = divmod(piece, HKV)
-            c = ORDER[2 * place] // 2
-            copier(piece % Q_V_DEN == Q_V_OFF)(out=qT[:, c, g].rearrange("p m u q -> p u m q"),
-                                         in_=turned_q[piece].rearrange("p (u x) (r q) -> p u (x r) q", u=2, r=2))
+            copier(g == 0)(
+                out=qT[:, CHUNK_ORDER[place], g].rearrange("p m u q -> p u m q"),
+                in_=turned_q[piece].rearrange("p (u x) (r q) -> p u (x r) q", u=2, r=2),
+            )
             give(("q", piece))
 
-        def score(unit, lead=True):
-            r = block_of(unit)
-            per = PER[r]
-            if lead and unit % per:
+        def score(unit):
+            r = strip_of(unit)
+            per_bank = UNITS_PER_BANK[r]
+            if unit % per_bank:
                 return
-            if lead:
-                take(("s", unit // per))
-                for other in range(unit + 1, unit + per):
-                    score(other, False)
             n_keys = keys_of(r)
-            first = (unit % per) * n_keys
-            scores = bank_of["s", unit // per][:, first : first + n_keys]
-            g, x = divmod(unit % 8, 2)
-            nc.tensor.matmul(out=scores, lhsT=qT[:, r // 2, g, 2 * x + r % 2].rearrange("p u q -> p (u q)"), rhs=kT[:, g, 0:n_keys], start=True, stop=False)
-            nc.tensor.matmul(out=scores[:, r * ROWS : n_keys], lhsT=ident_bf[:], rhs=mask_bf[:, 0 : n_keys - r * ROWS], start=False, stop=True)
+            bank = take(("scores", unit // per_bank))
+            for j in range(per_bank):
+                g, x = divmod((unit + j) % UNITS_PER_STRIP, 2)
+                scores = bank[:, j * n_keys : (j + 1) * n_keys]
+                nc.tensor.matmul(
+                    out=scores,
+                    lhsT=qT[:, r // 2, g, 2 * x + r % 2].rearrange("p u q -> p (u q)"),
+                    rhs=kT[:, g, 0:n_keys],
+                    start=True,
+                    stop=False,
+                )
+                nc.tensor.matmul(
+                    out=scores[:, r * STRIP : n_keys],
+                    lhsT=ident_bf[:],
+                    rhs=mask[:, 0 : n_keys - r * STRIP],
+                    start=False,
+                    stop=True,
+                )
 
         def row_maximum(unit):
-            r = block_of(unit)
-            per = PER[r]
+            r = strip_of(unit)
+            per_bank = UNITS_PER_BANK[r]
             n_keys = keys_of(r)
-            scores = bank_of["s", unit // per]
-            if r >= LOW:
+            bank = bank_of["scores", unit // per_bank]
+            if r >= LOWER:
                 scaled = stage.tile([P, S], BF16, name="scaled", bufs=2)
                 shift = stats.tile([P, 1], F32, name="shift1")
-                nc.vector.tensor_scalar(out=scaled[:, 0:n_keys], in0=scores[:, 0:n_keys],
-                                        scalar1=-SCALE, scalar2=3.0e38, op0=ALU.mult, op1=ALU.min, accum_out=shift[:])
+                nc.vector.tensor_scalar(
+                    out=scaled[:, 0:n_keys],
+                    in0=bank[:, 0:n_keys],
+                    scalar1=-SCALE,
+                    scalar2=HUGE,
+                    op0=ALU.mult,
+                    op1=ALU.min,
+                    accum_out=shift[:],
+                )
                 shift_of[unit] = shift[:]
-            elif unit % per == 0:
-                rowmax = stats.tile([P, per], F32, name="rowmax%d" % per)
-                nc.vector.tensor_reduce(out=rowmax[:], in_=scores[:, 0 : per * n_keys].rearrange("p (h k) -> p h k", h=per), axis=AXIS.X, op=ALU.max)
+            elif unit % per_bank == 0:
+                rowmax = stats.tile([P, per_bank], F32, name="rowmax%d" % per_bank)
+                nc.vector.tensor_reduce(
+                    out=rowmax[:],
+                    in_=bank[:, 0 : per_bank * n_keys].rearrange("p (h k) -> p h k", h=per_bank),
+                    axis=AXIS.X,
+                    op=ALU.max,
+                )
                 rowmax_of[unit] = rowmax
 
         def scale_maximum(unit):
-            r = block_of(unit)
-            per = PER[r]
-            if r < LOW and unit % per == 0:
-                shift = stats.tile([P, per], F32, name="shift%d" % per)
+            r = strip_of(unit)
+            per_bank = UNITS_PER_BANK[r]
+            if r < LOWER and unit % per_bank == 0:
+                shift = stats.tile([P, per_bank], F32, name="shift%d" % per_bank)
                 nc.scalar.activation(out=shift[:], in_=rowmax_of[unit][:], func=ACT.Copy, scale=-SCALE)
-                for j in range(per):
+                for j in range(per_bank):
                     shift_of[unit + j] = shift[:, j : j + 1]
 
         def exponential(unit):
             step, j = divmod(unit, QUAD)
-            r = block_of(unit)
-            per = PER[r]
+            r = strip_of(unit)
+            per_bank = UNITS_PER_BANK[r]
             n_keys = keys_of(r)
+            e_tile = e_tiles[step % E_TILES]
             if j == 0:
                 rowsum_of[step] = stats.tile([P, QUAD], F32, name="rowsum")
-            if r >= LOW:
+            if r >= LOWER:
                 halves = 1
-                e_out = e_tiles[step % E_TILES][:, j * S : j * S + n_keys].rearrange("p (h k) -> p h k", h=1)
+                e_keys = e_tile[:, j * S : j * S + n_keys].rearrange("p (h k) -> p h k", h=1)
             else:
                 halves = max(1, n_keys // P)
-                e_out = e_tiles[step % E_TILES][:, j // 2 * S : (j // 2 + 1) * S].rearrange("p (h x k) -> p h x k", h=2, x=2)[:, 0:halves, j % 2, 0 : n_keys // halves]
+                g_keys = e_tile[:, j // 2 * S : (j // 2 + 1) * S].rearrange("p (h x k) -> p h x k", h=2, x=2)
+                e_keys = g_keys[:, 0:halves, j % 2, 0 : n_keys // halves]
+            first = unit % per_bank * n_keys
+            scores = bank_of["scores", unit // per_bank][:, first : first + n_keys]
             nc.scalar.activation(
-                out=e_out,
-                in_=bank_of["s", unit // per][:, unit % per * n_keys : (unit % per + 1) * n_keys].rearrange("p (h k) -> p h k", h=halves),
+                out=e_keys,
+                in_=scores.rearrange("p (h k) -> p h k", h=halves),
                 func=ACT.Exp,
                 bias=shift_of[unit],
                 scale=SCALE,
                 accum_out=rowsum_of[step][:, j : j + 1],
             )
-            if (unit + 1) % per == 0:
-                give(("s", unit // per))
+            if (unit + 1) % per_bank == 0:
+                give(("scores", unit // per_bank))
 
         def reciprocal(step):
             rinv = stats.tile([P, QUAD], F32)
@@ -335,67 +363,82 @@ def tile_gemmaattention_pb_kernel(tc, q_rot, k_rot, v, w_o, out):
             rinv_of[step] = rinv
 
         def clear_e(step):
-            if step + E_TILES >= STEPS:
+            follower = step + E_TILES
+            if follower >= STEPS:
                 return
-            r = ORDER[(step + E_TILES) // 2]
+            r = STRIP_ORDER[follower // 2]
             e_tile = e_tiles[step % E_TILES][:]
-            if LOW <= r < RB - 1:
-                nc.gpsimd.memset(e_tile.rearrange("p (j k) -> p j k", j=QUAD)[:, :, (r + 1) * ROWS : min(S, (r + 3) * ROWS)], 0.0)
+            if LOWER <= r < STRIPS - 1:
+                behind_upper = step >= 0 and STRIP_ORDER[step // 2] >= LOWER
+                end = min(S, (r + 3) * STRIP) if behind_upper else S
+                nc.gpsimd.memset(
+                    e_tile.rearrange("p (j k) -> p j k", j=QUAD)[:, :, (r + 1) * STRIP : end], 0.0
+                )
             elif r < 2:
-                halves = e_tile[:, 0 : 2 * S].rearrange("p (g h k) -> p g h k", g=2, h=2)
-                nc.gpsimd.memset(halves[:, :, 1, :], 0.0)
+                e_halves = e_tile[:, 0 : 2 * S].rearrange("p (g h k) -> p g h k", g=2, h=2)
+                nc.gpsimd.memset(e_halves[:, :, 1, :], 0.0)
                 if r == 0:
-                    nc.gpsimd.memset(halves[:, :, 0, :].rearrange("p g (x k) -> p g x k", x=2)[:, :, :, ROWS:P], 0.0)
+                    low_half = e_halves[:, :, 0, :].rearrange("p g (x k) -> p g x k", x=2)
+                    nc.gpsimd.memset(low_half[:, :, :, STRIP:P], 0.0)
+
+        def is_lower(step):
+            return STRIP_ORDER[step // 2] < LOWER
 
         def turn_e(pair):
-            step, half = divmod(pair, 2)
-            low = ORDER[step // 2] < LOW
-            bank = step if low else ("half", pair)
-            if not low or half == 0:
-                turned_e[bank] = take(("e", bank)).rearrange("p (h u i) -> p h u i", h=2, u=2)
+            step, i = divmod(pair, 2)
+            lower = is_lower(step)
             e_words = e_tiles[step % E_TILES][:].bitcast(F32)
-            if low:
-                for u in range(2):
-                    first = (2 * half + u) * P
-                    nc.tensor.transpose(out=turned_e[bank][:, half, u, :], in_=e_words[:, first : first + P], identity=ident_f32[:])
+            if not lower or i == 0:
+                turned_e[pair] = take(("e", pair)).rearrange("p (h u i) -> p h u i", h=2, u=2)
             else:
-                for j in range(2):
-                    for u in range(2):
-                        first = ((2 * half + j) * 2 + u) * P
-                        nc.tensor.transpose(out=turned_e[bank][:, j, u, :], in_=e_words[:, first : first + P], identity=ident_f32[:])
+                turned_e[pair] = turned_e[pair - 1]
+            for j in [i] if lower else [0, 1]:
+                for u in range(2):
+                    first = (2 * j + u) * P if lower else (4 * i + 2 * j + u) * P
+                    nc.tensor.transpose(
+                        out=turned_e[pair][:, j, u, :], in_=e_words[:, first : first + P], identity=ident_f32[:]
+                    )
 
         def copy_e(pair):
-            step, half = divmod(pair, 2)
-            low = ORDER[step // 2] < LOW
-            if low and half == 0:
+            step, i = divmod(pair, 2)
+            lower = is_lower(step)
+            if lower and i == 0:
                 return
-            bank = step if low else ("half", pair)
-            if low or half == 0:
-                e_grouped_of[step] = stage.tile([P, 2 if low else QUAD, P * PACK], BF16, align_bytes=64, name="e_grouped", bufs=3)
-            words = e_grouped_of[step][:].rearrange("p h t -> p (h t)").bitcast(F32).rearrange("p (h i u) -> p h i u", i=P, u=2)
-            first = 0 if low else 2 * half
-            copier(pair % 4 < E_V)(out=words[:, first : first + 2, :, :], in_=turned_e[bank].rearrange("p h u i -> p h i u"))
-            give(("e", bank))
+            if lower or i == 0:
+                e_grouped_of[step] = stage.tile(
+                    [P, 2 if lower else QUAD, P * PACK], BF16, align_bytes=64, name="e_grouped", bufs=3
+                )
+            words = e_grouped_of[step][:].rearrange("p h t -> p (h t)").bitcast(F32)
+            words = words.rearrange("p (h i u) -> p h i u", i=P, u=2)
+            first = 0 if lower else 2 * i
+            nc.scalar.copy(
+                out=words[:, first : first + 2, :, :], in_=turned_e[pair].rearrange("p h u i -> p h i u")
+            )
+            give(("e", pair - 1 if lower else pair))
 
         def quantise_e(step):
-            n = (2 if ORDER[step // 2] < LOW else QUAD) * P
-            e_codes = stage.tile([P, n], U32, align_bytes=64, name="e_codes")
-            e_scales = stage.tile([P, n], U8, align_bytes=64, name="e_scales")
-            nc.vector.quantize_mx(out=e_codes[:].bitcast(FP8X4), scales=e_scales[:], in_=e_grouped_of[step][:].rearrange("p h t -> p (h t)"))
+            columns = (2 if is_lower(step) else QUAD) * P
+            e_codes = stage.tile([P, columns], U32, align_bytes=64, name="e_codes")
+            e_scales = stage.tile([P, columns], U8, align_bytes=64, name="e_scales")
+            nc.vector.quantize_mx(
+                out=e_codes[:].bitcast(FP8X4),
+                scales=e_scales[:],
+                in_=e_grouped_of[step][:].rearrange("p h t -> p (h t)"),
+            )
             e_operand[step] = (e_codes, e_scales)
 
         def multiply_v(step):
             e_codes, e_scales = e_operand[step]
             pv = take(("pv", step))
-            low = ORDER[step // 2] < LOW
-            codes, scales, n = (pair_codes, pair_scales, 2 * D) if low else (v_codes, v_scales, D)
-            for j in range(2 if low else QUAD):
-                g = 2 * (step % 2) + (j if low else j // 2)
-                rows = slice(j * P, (j + 1) * P)
+            lower = is_lower(step)
+            codes, scales, n = (pair_codes, pair_scales, 2 * D) if lower else (v_codes, v_scales, D)
+            for j in range(2 if lower else QUAD):
+                g = 2 * (step % 2) + (j if lower else j // 2)
+                columns = slice(j * P, (j + 1) * P)
                 nc.tensor.matmul_mx(
                     out=pv[:, j * n : (j + 1) * n],
-                    lhsT=e_codes[:, rows].bitcast(FP8X4),
-                    lhsT_scale=e_scales[:, rows],
+                    lhsT=e_codes[:, columns].bitcast(FP8X4),
+                    lhsT_scale=e_scales[:, columns],
                     rhs=codes[:, g * n : (g + 1) * n].bitcast(FP8X4),
                     rhs_scale=scales[:, g * n : (g + 1) * n],
                     start=True,
@@ -423,75 +466,99 @@ def tile_gemmaattention_pb_kernel(tc, q_rot, k_rot, v, w_o, out):
 
         def copy_o(step):
             place, rest = divmod(step, 4)
-            r = ORDER[step // 2]
-            gp = step % 2
+            r = STRIP_ORDER[step // 2]
+            half = 2 * place + step % 2
             if rest < 2:
-                o_grouped_of[place, gp] = stage.tile([P, 2 * P * PACK], BF16, align_bytes=64, name="o_grouped")
-            words = o_grouped_of[place, gp][:].bitcast(F32).rearrange("p (g r q u) -> p g r q u", g=2, r=2, u=2)
-            copier(step % 4 < (O_V if step < STEPS // 2 else O_V_LATE))(out=words[:, :, r % 2, :, :], in_=turned_o[step].rearrange("p g (u q) -> p g q u", u=2))
+                o_grouped_of[half] = stage.tile([P, 2 * P * PACK], BF16, align_bytes=64, name="o_grouped")
+            words = o_grouped_of[half][:].bitcast(F32).rearrange("p (g r q u) -> p g r q u", g=2, r=2, u=2)
+            nc.scalar.copy(
+                out=words[:, :, r % 2, :, :], in_=turned_o[step].rearrange("p g (u q) -> p g q u", u=2)
+            )
             give(("o", step))
 
-        def quantise_o(piece):
-            place, gp = divmod(piece, 2)
-            rows = slice(gp * 2 * P, (gp + 1) * 2 * P)
-            nc.vector.quantize_mx(out=o_codes[place][:, rows].bitcast(FP8X4), scales=o_scales[place][:, rows], in_=o_grouped_of[place, gp][:])
+        def quantise_o(half):
+            place, pair_of_g = divmod(half, 2)
+            columns = slice(pair_of_g * 2 * P, (pair_of_g + 1) * 2 * P)
+            nc.vector.quantize_mx(
+                out=o_codes[place][:, columns].bitcast(FP8X4),
+                scales=o_scales[place][:, columns],
+                in_=o_grouped_of[half][:],
+            )
 
-        def quantise_v(piece):
-            v_grouped = stage.tile([P, HKV * D * PACK], BF16, align_bytes=64, name="grouped", bufs=1)
-            nc.vector.tensor_copy(out=v_grouped[:].rearrange("p (c t) -> p c t", t=PACK), in_=v_sb[:].rearrange("p u (e c) -> p c (u e)", e=2))
-            nc.vector.quantize_mx(out=v_codes[:].bitcast(FP8X4), scales=v_scales[:], in_=v_grouped[:])
+        def group(raw):
+            grouped = stage.tile([P, HKV * D * PACK], BF16, align_bytes=64, name="v_grouped", bufs=1)
+            nc.vector.tensor_copy(
+                out=grouped[:].rearrange("p (c t) -> p c t", t=PACK), in_=raw[:].rearrange("p t c -> p c t")
+            )
+            return grouped
 
-        def group_half(piece):
-            half_grouped["in"] = stage.tile([P, HKV * D * PACK], BF16, align_bytes=64, name="grouped", bufs=1)
-            nc.vector.tensor_copy(out=half_grouped["in"][:].rearrange("p (c t) -> p c t", t=PACK), in_=half_sb[:].rearrange("p t c -> p c t"))
+        def quantise_v():
+            grouped = group(v_sb)
+            nc.vector.quantize_mx(out=v_codes[:].bitcast(FP8X4), scales=v_scales[:], in_=grouped[:])
 
-        def quantise_half(piece):
-            nc.vector.quantize_mx(out=half_codes[:].bitcast(FP8X4), scales=half_scales[:], in_=half_grouped["in"][:])
+        def group_pair():
+            pair_grouped_of["v"] = group(pair_sb)
 
-        def place_half(piece):
+        def quantise_pair():
+            nc.vector.quantize_mx(
+                out=once_codes[:].bitcast(FP8X4), scales=once_scales[:], in_=pair_grouped_of["v"][:]
+            )
+
+        def place_pair():
             to = pair_codes[:].bitcast(I32).rearrange("p (g x d) -> p g x d", g=HKV, x=2)
-            of = half_codes[:].bitcast(I32).rearrange("p (g d) -> p g d", g=HKV)
+            source = once_codes[:].bitcast(I32).rearrange("p (g d) -> p g d", g=HKV)
             for x in range(2):
-                rows = slice(x * ROWS, (x + 1) * ROWS)
-                nc.vector.tensor_copy(out=to[rows, :, x, :], in_=of[rows, :, :])
+                half = slice(x * STRIP, (x + 1) * STRIP)
+                nc.vector.tensor_copy(out=to[half, :, x, :], in_=source[half, :, :])
             for x in range(2):
-                nc.vector.tensor_copy(out=pair_scales[:].bitcast(I32).rearrange("p (g x d) -> p g x d", g=HKV, x=2)[:, :, x, :],
-                                      in_=half_scales[:].bitcast(I32).rearrange("p (g d) -> p g d", g=HKV))
+                nc.vector.tensor_copy(
+                    out=pair_scales[:].bitcast(I32).rearrange("p (g x d) -> p g x d", g=HKV, x=2)[:, :, x, :],
+                    in_=once_scales[:].bitcast(I32).rearrange("p (g d) -> p g d", g=HKV),
+                )
+
+        def w_place(piece):
+            slab, rest = divmod(piece, 2 * PASSES)
+            tiles, g = divmod(rest, PASSES)
+            return slab, tiles, g
 
         def turn_w(piece):
-            nb, rest = divmod(piece, 2 * PASSES)
-            half, g = divmod(rest, PASSES)
+            slab, tiles, g = w_place(piece)
             turned = take(("w", piece)).rearrange("p (r u n) -> p r u n", r=2, u=2)
             for j in range(2):
-                words = w_sb[4 * nb + 2 * half + j][:].bitcast(F32)
+                words = w_sb[4 * slab + 2 * tiles + j][:].bitcast(F32)
                 for u in range(2):
                     first = (2 * g + u) * P
-                    nc.tensor.transpose(out=turned[:, j, u, :], in_=words[:, first : first + P], identity=ident_f32[:])
+                    nc.tensor.transpose(
+                        out=turned[:, j, u, :], in_=words[:, first : first + P], identity=ident_f32[:]
+                    )
             turned_w[piece] = turned
 
         def copy_w(piece):
             w_grouped = stage.tile([P, 2 * P * PACK], BF16, align_bytes=64, bufs=5)
             words = w_grouped[:].bitcast(F32).rearrange("p (r n u) -> p r n u", r=2, u=2)
-            copier(piece % W_V_DEN == W_V_OFF)(out=words, in_=turned_w[piece].rearrange("p r u n -> p r n u"))
+            copier(piece % (2 * PASSES) == PASSES - 1)(out=words, in_=turned_w[piece].rearrange("p r u n -> p r n u"))
             w_grouped_of[piece] = w_grouped
             give(("w", piece))
 
         def quantise_w(piece):
-            nb, rest = divmod(piece, 2 * PASSES)
-            half, g = divmod(rest, PASSES)
-            features = slice(nb * BANK + half * 2 * P, nb * BANK + (half + 1) * 2 * P)
-            nc.vector.quantize_mx(out=w_codes[:, g, features].bitcast(FP8X4), scales=w_scales[:, g, features], in_=w_grouped_of[piece][:])
+            slab, tiles, g = w_place(piece)
+            features = slice(slab * BANK + tiles * 2 * P, slab * BANK + (tiles + 1) * 2 * P)
+            nc.vector.quantize_mx(
+                out=w_codes[:, g, features].bitcast(FP8X4),
+                scales=w_scales[:, g, features],
+                in_=w_grouped_of[piece][:],
+            )
 
         def project_pass(block, g):
-            place, nb = divmod(block, N_BLOCKS)
-            features = slice(nb * BANK, (nb + 1) * BANK)
+            place, slab = divmod(block, SLABS)
+            features = slice(slab * BANK, (slab + 1) * BANK)
             if g == 0:
-                acc_of[block] = take(("acc", block))
-            rows = slice(g * P, (g + 1) * P)
+                acc_of[block] = take(("out", block))
+            columns = slice(g * P, (g + 1) * P)
             nc.tensor.matmul_mx(
                 out=acc_of[block],
-                lhsT=o_codes[place][:, rows].bitcast(FP8X4),
-                lhsT_scale=o_scales[place][:, rows],
+                lhsT=o_codes[place][:, columns].bitcast(FP8X4),
+                lhsT_scale=o_scales[place][:, columns],
                 rhs=w_codes[:, g, features].bitcast(FP8X4),
                 rhs_scale=w_scales[:, g, features],
                 start=(g == 0),
@@ -503,59 +570,65 @@ def tile_gemmaattention_pb_kernel(tc, q_rot, k_rot, v, w_o, out):
                 project_pass(block, g)
 
         def store(block):
-            place, nb = divmod(block, N_BLOCKS)
-            c = ORDER[2 * place] // 2
+            place, slab = divmod(block, SLABS)
+            c = CHUNK_ORDER[place]
             result = results.tile([P, BANK], F32)
-            copier(nb % (2 if place == CHUNKS - 1 else S_V_DEN) == 0)(out=result[:], in_=acc_of[block])
-            give(("acc", block))
-            nc.sync.dma_start(out=out_rows[c * P : (c + 1) * P, nb * BANK : (nb + 1) * BANK], in_=result[:])
+            copier(place < CHUNKS - 1 or slab % 2 == 0)(out=result[:], in_=acc_of[block])
+            give(("out", block))
+            nc.sync.dma_start(out=out_rows[c * P : (c + 1) * P, slab * BANK : (slab + 1) * BANK], in_=result[:])
 
-        by_tick = {}
+        plan = {}
 
-        def due(tick, fn, *piece):
-            by_tick.setdefault(tick, []).append((fn, piece))
+        def due(tick, stage_fn, *piece):
+            plan.setdefault(tick, []).append((stage_fn, piece))
 
-        def every(fn, count, at):
+        def every(stage_fn, count, tick_of):
             for piece in range(count):
-                due(at(piece), fn, piece)
+                due(tick_of(piece), stage_fn, piece)
 
-        every(row_maximum, UNITS, lambda u: unit_tick(u) + MAX_AT)
-        every(reciprocal, STEPS, lambda s: step_tick(s) + RECIPROCAL_AT)
+        last_blocks = range(BLOCKS - SLABS, BLOCKS)
+        start = turn_k_tick(0)
+
         for b in range(E_TILES):
-            due(-100, clear_e, b - E_TILES)
-        every(clear_e, STEPS, lambda s: step_tick(s) + TURN_E_AT + 1)
-        every(copy_e, UNITS // 2, lambda p: unit_tick(2 * p + 1) + COPY_E_AT)
-        every(normalise, STEPS, lambda s: step_tick(s) + NORMALISE_AT)
-        every(copy_o, STEPS, lambda s: step_tick(s) + COPY_O_AT)
-        every(copy_w, W_PIECES, lambda w: w_tick(w) + COPY_W_AT)
-        every(copy_k, HKV, lambda k: TURN_K_AT[k] + FROM_PSUM)
-        every(copy_q, 4 * CHUNKS, lambda q: q_tick(q) + FROM_PSUM)
-        for block in range(OUT_BLOCKS - N_BLOCKS):
-            due(PROJECT_TICK[block] + STORE_LAG, store, block)
-        for nb in range(N_BLOCKS):
-            due(o_ready(CHUNKS - 1, 1) + O_LAG + 1, store, OUT_BLOCKS - N_BLOCKS + nb)
-        every(exponential, UNITS, lambda u: unit_tick(u) + EXP_AT)
-        every(scale_maximum, UNITS, lambda u: unit_tick(u) + MAX_AT)
-        every(quantise_e, STEPS, lambda s: step_tick(s) + QUANTISE_E_AT)
-        every(quantise_o, 2 * CHUNKS, lambda i: o_ready(i // 2, i % 2))
-        every(quantise_w, W_PIECES, lambda w: w_tick(w) + QUANTISE_W_AT)
-        due(QUANTISE_V_AT, quantise_v, 0)
-        due(HALF_AT, group_half, 0)
-        due(HALF_AT + 2, quantise_half, 0)
-        due(HALF_AT + 4, place_half, 0)
-        every(turn_e, UNITS // 2, lambda p: unit_tick(2 * p + 1) + TURN_E_AT)
-        every(turn_o, STEPS, lambda s: step_tick(s) + TURN_O_AT)
-        every(turn_w, W_PIECES, lambda w: w_tick(w) + TURN_W_AT)
-        every(turn_k, HKV, lambda k: TURN_K_AT[k])
-        every(turn_q, 4 * CHUNKS, q_tick)
-        every(score, UNITS, lambda u: unit_tick(u))
-        every(multiply_v, STEPS, lambda s: step_tick(s) + MULTIPLY_V_AT)
-        for block in range(OUT_BLOCKS - N_BLOCKS):
+            due(start, clear_e, b - E_TILES)
+        due(start, warm_up)
+        every(row_maximum, UNITS, lambda unit: unit_tick(unit) + MAX_AT)
+        every(reciprocal, STEPS, lambda step: step_tick(step) + RECIPROCAL_AT)
+        every(clear_e, STEPS, lambda step: step_tick(step) + CLEAR_E_AT)
+        every(copy_e, PAIRS, lambda pair: pair_tick(pair) + COPY_E_AT)
+        every(normalise, STEPS, lambda step: step_tick(step) + NORMALISE_AT)
+        every(copy_o, STEPS, lambda step: step_tick(step) + COPY_O_AT)
+        every(copy_w, W_PIECES, lambda piece: piece + COPY_W_AT)
+        every(copy_k, HKV, lambda g: turn_k_tick(g) + FROM_PSUM)
+        every(copy_q, CHUNKS * HKV, lambda piece: turn_q_tick(piece) + FROM_PSUM)
+        for block in PROJECT_TICK:
+            due(PROJECT_TICK[block] + FROM_PSUM, store, block)
+        for block in last_blocks:
+            due(quantise_o_tick(2 * CHUNKS - 1) + 1 + FROM_PSUM, store, block)
+        every(exponential, UNITS, lambda unit: unit_tick(unit) + EXP_AT)
+        every(scale_maximum, UNITS, lambda unit: unit_tick(unit) + MAX_AT)
+        every(quantise_e, STEPS, lambda step: step_tick(step) + QUANTISE_E_AT)
+        every(quantise_o, 2 * CHUNKS, quantise_o_tick)
+        every(quantise_w, W_PIECES, lambda piece: piece + QUANTISE_W_AT)
+        due(QUANTISE_V_AT, quantise_v)
+        due(GROUP_PAIR_AT, group_pair)
+        due(QUANTISE_PAIR_AT, quantise_pair)
+        due(PLACE_PAIR_AT, place_pair)
+        every(turn_e, PAIRS, lambda pair: pair_tick(pair) + TURN_E_AT)
+        every(turn_o, STEPS, lambda step: step_tick(step) + TURN_O_AT)
+        every(turn_w, W_PIECES, lambda piece: piece + TURN_W_AT)
+        every(turn_k, HKV, turn_k_tick)
+        every(turn_q, CHUNKS * HKV, turn_q_tick)
+        every(score, UNITS, unit_tick)
+        every(multiply_v, STEPS, lambda step: step_tick(step) + MULTIPLY_V_AT)
+        for block in PROJECT_TICK:
             due(PROJECT_TICK[block], project, block)
         for g in range(PASSES):
-            for nb in range(N_BLOCKS):
-                due(max(LAST_AT, o_ready(CHUNKS - 1, g // 2) + O_LAG), project_pass, OUT_BLOCKS - N_BLOCKS + nb, g)
-        due(TURN_W_AT + w_tick(7) + 1, load, LOADS[-1])
-        for tick in sorted(by_tick):
-            for fn, piece in by_tick[tick]:
-                fn(*piece)
+            quantised = quantise_o_tick(2 * CHUNKS - 2 + g // 2) + 1
+            for block in last_blocks:
+                due(max(step_tick(STEPS - 1) + MULTIPLY_V_AT, quantised), project_pass, block, g)
+        due(LAST_W_LOAD_AT, load_w, SLABS - 1)
+
+        for tick in sorted(plan):
+            for stage_fn, piece in plan[tick]:
+                stage_fn(*piece)

@@ -261,7 +261,7 @@ def tile_gemmaattention_pb_kernel(tc, q_rot, k_rot, v, w_o, out):
 
         def copy_q(piece):
             place, g = divmod(piece, HKV)
-            copier(g == 0)(
+            nc.scalar.copy(
                 out=qT[:, CHUNK_ORDER[place], g].rearrange("p m u q -> p u m q"),
                 in_=turned_q[piece].rearrange("p (u x) (r q) -> p u (x r) q", u=2, r=2),
             )
@@ -312,9 +312,10 @@ def tile_gemmaattention_pb_kernel(tc, q_rot, k_rot, v, w_o, out):
                 shift_of[unit] = shift[:]
             elif unit % per_bank == 0:
                 rowmax = stats.tile([P, per_bank], F32, name="rowmax%d" % per_bank)
+                unit_scores = bank[:, 0 : per_bank * n_keys].rearrange("p (h k) -> p h k", h=per_bank)
                 nc.vector.tensor_reduce(
                     out=rowmax[:],
-                    in_=bank[:, 0 : per_bank * n_keys].rearrange("p (h k) -> p h k", h=per_bank),
+                    in_=unit_scores[:, :, 0 : (r + 1) * STRIP],
                     axis=AXIS.X,
                     op=ALU.max,
                 )
@@ -335,8 +336,8 @@ def tile_gemmaattention_pb_kernel(tc, q_rot, k_rot, v, w_o, out):
             per_bank = UNITS_PER_BANK[r]
             n_keys = keys_of(r)
             e_tile = e_tiles[step % E_TILES]
-            if j == 0:
-                rowsum_of[step] = stats.tile([P, QUAD], F32, name="rowsum")
+            if unit % UNITS_PER_STRIP == 0:
+                rowsum_of[step // 2] = stats.tile([P, UNITS_PER_STRIP], F32, name="rowsum")
             if r >= LOWER:
                 halves = 1
                 e_keys = e_tile[:, j * S : j * S + n_keys].rearrange("p (h k) -> p h k", h=1)
@@ -352,15 +353,15 @@ def tile_gemmaattention_pb_kernel(tc, q_rot, k_rot, v, w_o, out):
                 func=ACT.Exp,
                 bias=shift_of[unit],
                 scale=SCALE,
-                accum_out=rowsum_of[step][:, j : j + 1],
+                accum_out=rowsum_of[step // 2][:, unit % UNITS_PER_STRIP : unit % UNITS_PER_STRIP + 1],
             )
             if (unit + 1) % per_bank == 0:
                 give(("scores", unit // per_bank))
 
-        def reciprocal(step):
-            rinv = stats.tile([P, QUAD], F32)
-            nc.vector.reciprocal(out=rinv[:], in_=rowsum_of[step][:])
-            rinv_of[step] = rinv
+        def reciprocal(place):
+            rinv = stats.tile([P, UNITS_PER_STRIP], F32)
+            nc.vector.reciprocal(out=rinv[:], in_=rowsum_of[place][:])
+            rinv_of[place] = rinv
 
         def clear_e(step):
             follower = step + E_TILES
@@ -451,7 +452,7 @@ def tile_gemmaattention_pb_kernel(tc, q_rot, k_rot, v, w_o, out):
             nc.vector.tensor_tensor(
                 out=o_sb[:].rearrange("p (h d) -> p h d", h=QUAD),
                 in0=pv_of[step],
-                in1=rinv_of[step][:].unsqueeze(2).to_broadcast([P, QUAD, D]),
+                in1=rinv_of[step // 2][:, step % 2 * QUAD : (step % 2 + 1) * QUAD].unsqueeze(2).to_broadcast([P, QUAD, D]),
                 op=ALU.mult,
             )
             o_sb_of[step] = o_sb
@@ -536,7 +537,7 @@ def tile_gemmaattention_pb_kernel(tc, q_rot, k_rot, v, w_o, out):
         def copy_w(piece):
             w_grouped = stage.tile([P, 2 * P * PACK], BF16, align_bytes=64, bufs=5)
             words = w_grouped[:].bitcast(F32).rearrange("p (r n u) -> p r n u", r=2, u=2)
-            copier(piece % (2 * PASSES) == PASSES - 1)(out=words, in_=turned_w[piece].rearrange("p r u n -> p r n u"))
+            nc.scalar.copy(out=words, in_=turned_w[piece].rearrange("p r u n -> p r n u"))
             w_grouped_of[piece] = w_grouped
             give(("w", piece))
 
@@ -593,7 +594,7 @@ def tile_gemmaattention_pb_kernel(tc, q_rot, k_rot, v, w_o, out):
             due(start, clear_e, b - E_TILES)
         due(start, warm_up)
         every(row_maximum, UNITS, lambda unit: unit_tick(unit) + MAX_AT)
-        every(reciprocal, STEPS, lambda step: step_tick(step) + RECIPROCAL_AT)
+        every(reciprocal, STRIPS, lambda place: step_tick(2 * place) + RECIPROCAL_AT)
         every(clear_e, STEPS, lambda step: step_tick(step) + CLEAR_E_AT)
         every(copy_e, PAIRS, lambda pair: pair_tick(pair) + COPY_E_AT)
         every(normalise, STEPS, lambda step: step_tick(step) + NORMALISE_AT)

@@ -120,7 +120,7 @@ def project_ticks():
     free = 0
     for block in sorted(ready, key=lambda b: (ready[b], b)):
         ticks[block] = max(free, ready[block])
-        free = ticks[block] + (4 if ticks[block] <= SCORE_TICKS else 2)
+        free = ticks[block] + (3 if ticks[block] <= SCORE_TICKS else 2)
     return ticks
 
 

from contextlib import ExitStack

import concourse.mybir as mybir
from concourse.masks import make_identity

F32 = mybir.dt.float32
BF16 = mybir.dt.bfloat16
U32 = mybir.dt.uint32
I32 = mybir.dt.int32
U8 = mybir.dt.uint8
FP8X4 = mybir.dt.float8_e4m3fn_x4
ACT = mybir.ActivationFunctionType
ALU = mybir.AluOpType
AXIS = mybir.AxisListType

P = 128
S = 512
H = 16
HKV = 4
REP = H // HKV
D = 128
HIDDEN = 2048
PACK = 4
K_PASS = P * PACK
BANK = 512
BANKS = 8
CHUNKS = S // P
STRIP = 64
STRIPS = S // STRIP
LOWER = STRIPS // 2
UNITS_PER_STRIP = 2 * HKV
UNITS = UNITS_PER_STRIP * STRIPS
QUAD = 4
STEPS = UNITS // QUAD
PAIRS = UNITS // 2
SLABS = HIDDEN // BANK
PASSES = HIDDEN // K_PASS
BLOCKS = CHUNKS * SLABS
W_PIECES = 2 * SLABS * PASSES
SCALE = D**-0.5
MASK_NEG = -2.3819763e38
HUGE = 3.0e38

CHUNK_ORDER = [2, 1, 3, 0]
STRIP_ORDER = [2 * c + i for c in CHUNK_ORDER for i in (1, 0)]
UNITS_PER_BANK = [4, 4, 2, 2, 1, 1, 1, 1]
HALF_TICKS = [1, 1, 1, 1, 2, 2, 2, 2]

E_TILES = 4
WARM_UP = 20


def strip_of(unit):
    return STRIP_ORDER[unit // UNITS_PER_STRIP]


def keys_of(r):
    return 2 * P if r == 2 else (r + 1) * STRIP


def unit_tick(unit):
    place, rest = divmod(unit, UNITS_PER_STRIP)
    before = sum(UNITS_PER_STRIP * HALF_TICKS[r] for r in STRIP_ORDER[:place])
    return (before + rest * HALF_TICKS[STRIP_ORDER[place]]) // 2


def pair_tick(pair):
    return unit_tick(2 * pair + 1)


def step_tick(step):
    return unit_tick(QUAD * step + QUAD - 1)


FROM_PSUM = 1
FROM_SBUF = 3
MAX_AT = FROM_PSUM
EXP_AT = MAX_AT + 1
TURN_E_AT = EXP_AT + FROM_SBUF
CLEAR_E_AT = TURN_E_AT + 1
COPY_E_AT = TURN_E_AT + FROM_PSUM
QUANTISE_E_AT = COPY_E_AT
MULTIPLY_V_AT = QUANTISE_E_AT + FROM_SBUF
NORMALISE_AT = MULTIPLY_V_AT + FROM_PSUM
RECIPROCAL_AT = NORMALISE_AT - 2
TURN_O_AT = NORMALISE_AT + 2
COPY_O_AT = TURN_O_AT + FROM_PSUM
QUANTISE_O_AT = COPY_O_AT
TURN_W_AT = 3
COPY_W_AT = TURN_W_AT + FROM_PSUM
QUANTISE_W_AT = COPY_W_AT + 1
LAST_W_LOAD_AT = TURN_W_AT + 2 * PASSES
QUANTISE_V_AT = step_tick(0) + MULTIPLY_V_AT - FROM_SBUF - 1
PLACE_PAIR_AT = step_tick(STEPS // CHUNKS) + MULTIPLY_V_AT - FROM_SBUF
QUANTISE_PAIR_AT = PLACE_PAIR_AT - 2
GROUP_PAIR_AT = QUANTISE_PAIR_AT - 2
SCORE_TICKS = sum(UNITS_PER_STRIP * HALF_TICKS[r] for r in STRIP_ORDER) // 2


def turn_q_tick(piece):
    place, g = divmod(piece, HKV)
    return unit_tick(2 * UNITS_PER_STRIP * place + 2 * g) - (FROM_SBUF if place == 0 else 2 * FROM_SBUF)


def turn_k_tick(g):
    return turn_q_tick(g)


def quantise_o_tick(half):
    place, pair_of_g = divmod(half, 2)
    return QUANTISE_O_AT + step_tick(4 * place + 2 + pair_of_g)


def project_ticks():
    ready = {}
    for block in range(BLOCKS - SLABS):
        place, slab = divmod(block, SLABS)
        ready[block] = max(quantise_o_tick(2 * place + 1), QUANTISE_W_AT + 2 * PASSES * (slab + 1) - 1)
    ticks = {}
    free = 0
    for block in sorted(ready, key=lambda b: (ready[b], b)):
        ticks[block] = max(free, ready[block])
        free = ticks[block] + (3 if ticks[block] <= SCORE_TICKS else 2)
    return ticks


PROJECT_TICK = project_ticks()

FLOPS = 2 * H * S * S * D * 2 + 2 * S * HIDDEN * HIDDEN


def tile_gemmaattention_pb_kernel(tc, q_rot, k_rot, v, w_o, out):
    nc = tc.nc
    q_rows = q_rot.rearrange("b s h d -> (b s) (h d)")
    out_rows = out.rearrange("b s n -> (b s) n")

    with ExitStack() as ctx:
        ctx.enter_context(tc.manual_schedule())
        keep = ctx.enter_context(tc.tile_pool(name="keep", bufs=1))
        stage = ctx.enter_context(tc.tile_pool(name="stage", bufs=4))
        stats = ctx.enter_context(tc.tile_pool(name="stats", bufs=8))
        results = ctx.enter_context(tc.tile_pool(name="results", bufs=5))
        weights = ctx.enter_context(tc.tile_pool(name="weights", bufs=12))
        psum = ctx.enter_context(tc.psum_pool(name="psum", bufs=1))

        free_banks = [psum.tile([P, BANK], F32, name="bank%d" % b) for b in range(BANKS)]
        bank_of = {}

        def take(owner):
            bank_of[owner] = free_banks.pop(0)
            return bank_of[owner][:]

        def give(owner):
            free_banks.append(bank_of.pop(owner))

        e_tiles = [keep.tile([P, QUAD * S], BF16, name="e_sb%d" % b) for b in range(E_TILES)]

        ident_bf = keep.tile([P, P], BF16)
        make_identity(nc, ident_bf[:])
        causal = keep.tile([P, P], F32)
        nc.gpsimd.memset(causal[:], 0.0)
        nc.gpsimd.affine_select(
            out=causal[:],
            in_=causal[:],
            compare_op=ALU.is_ge,
            fill=MASK_NEG,
            base=0,
            pattern=[[-1, P]],
            channel_multiplier=1,
        )
        mask = keep.tile([P, 2 * STRIP], BF16)
        nc.gpsimd.memset(mask[:, STRIP : 2 * STRIP], MASK_NEG)
        for u in range(2):
            half = slice(u * STRIP, (u + 1) * STRIP)
            nc.gpsimd.tensor_copy(out=mask[half, 0:STRIP], in_=causal[half, half])
        ident_f32 = keep.tile([P, P], F32)
        make_identity(nc, ident_f32[:])

        k_sb = keep.tile([P, CHUNKS, HKV * D], BF16)
        q_sb = [keep.tile([P, H * D], BF16, name="q_sb%d" % c) for c in range(CHUNKS)]
        v_sb = keep.tile([P, PACK, HKV * D], BF16)
        pair_sb = keep.tile([P, PACK, HKV * D], BF16)
        w_sb = {}

        def load_q(place, heads):
            c = CHUNK_ORDER[place]
            columns = slice(heads.start * D, heads.stop * D)
            nc.sync.dma_start(out=q_sb[c][:, columns], in_=q_rows[c * P : (c + 1) * P, columns])

        def load_w(slab):
            for nt in range(4 * slab, 4 * slab + 4):
                w_sb[nt] = weights.tile([P, HIDDEN], BF16, name="w_sb")
                nc.sync.dma_start(out=w_sb[nt][:], in_=w_o[nt * P : (nt + 1) * P, :])

        nc.sync.dma_start(out=k_sb[:], in_=k_rot.rearrange("b (t p) g d -> p (b t) (g d)", p=P))
        load_q(0, slice(0, REP))
        load_q(0, slice(REP, H))
        load_w(0)
        nc.sync.dma_start(
            out=v_sb[:].rearrange("p (u e) n -> p u (e n)", u=2),
            in_=v.rearrange("b (u p e) g d -> p (b u) (e g d)", u=2, e=2),
        )
        load_q(1, slice(0, H))
        load_w(1)
        for x in range(2):
            nc.sync.dma_start(
                out=pair_sb[x * STRIP : (x + 1) * STRIP, :, :].rearrange("p (u e) n -> p u (e n)", u=2),
                in_=v[:, 0 : 2 * P].rearrange("b (u p e) g d -> p (b u) (e g d)", u=2, e=2),
            )
        load_q(2, slice(0, H))
        load_w(2)
        load_q(3, slice(0, H))

        kT = keep.tile([P, HKV, S], BF16)
        qT = keep.tile([P, CHUNKS, HKV, 4, 2, STRIP], BF16)
        v_codes = keep.tile([P, HKV * D], U32, align_bytes=64)
        v_scales = keep.tile([P, HKV * D], U8, align_bytes=64)
        once_codes = keep.tile([P, HKV * D], U32, align_bytes=64)
        once_scales = keep.tile([P, HKV * D], U8, align_bytes=64)
        pair_codes = keep.tile([P, HKV * 2 * D], U32, align_bytes=64)
        pair_scales = keep.tile([P, HKV * 2 * D], U8, align_bytes=64)
        nc.gpsimd.memset(pair_codes[:].bitcast(I32), 0)
        w_codes = keep.tile([P, PASSES, HIDDEN], U32, align_bytes=64)
        w_scales = keep.tile([P, PASSES, HIDDEN], U8, align_bytes=64)
        o_codes = [keep.tile([P, PASSES * P], U32, name="o_codes%d" % i, align_bytes=64) for i in range(CHUNKS)]
        o_scales = [keep.tile([P, PASSES * P], U8, name="o_scales%d" % i, align_bytes=64) for i in range(CHUNKS)]
        turned_k, turned_q, rowmax_of, shift_of, rowsum_of, rinv_of = {}, {}, {}, {}, {}, {}
        turned_e, e_grouped_of, e_operand, pv_of, o_sb_of, turned_o, o_grouped_of = {}, {}, {}, {}, {}, {}, {}
        pair_grouped_of, turned_w, w_grouped_of, acc_of = {}, {}, {}, {}

        def copier(on_vector):
            return nc.vector.tensor_copy if on_vector else nc.scalar.copy

        def warm_up():
            bank = take("warm-up")
            for i in range(WARM_UP):
                nc.tensor.matmul(out=bank[:, 0:P], lhsT=ident_bf[:], rhs=ident_bf[:], start=True, stop=True)
            give("warm-up")

        def turn_k(g):
            turned_k[g] = take(("k", g)).bitcast(BF16)[:, 0:S].rearrange("p (t j) -> p t j", t=CHUNKS)
            for t in range(CHUNKS):
                nc.tensor.transpose(
                    out=turned_k[g][:, t, :], in_=k_sb[:, t, g * D : (g + 1) * D], identity=ident_bf[:]
                )

        def copy_k(g):
            copier(g % 2 == 0)(out=kT[:, g, :], in_=turned_k[g].rearrange("p t j -> p (t j)"))
            give(("k", g))

        def turn_q(piece):
            place, g = divmod(piece, HKV)
            turned_q[piece] = take(("q", piece)).bitcast(BF16)[:, 0 : REP * P].rearrange("p (h i) -> p h i", i=P)
            for j in range(REP):
                h = REP * g + j
                nc.tensor.transpose(
                    out=turned_q[piece][:, j, :],
                    in_=q_sb[CHUNK_ORDER[place]][:, h * D : (h + 1) * D],
                    identity=ident_bf[:],
                )

        def copy_q(piece):
            place, g = divmod(piece, HKV)
            nc.scalar.copy(
                out=qT[:, CHUNK_ORDER[place], g].rearrange("p m u q -> p u m q"),
                in_=turned_q[piece].rearrange("p (u x) (r q) -> p u (x r) q", u=2, r=2),
            )
            give(("q", piece))

        def score(unit):
            r = strip_of(unit)
            per_bank = UNITS_PER_BANK[r]
            if unit % per_bank:
                return
            n_keys = keys_of(r)
            bank = take(("scores", unit // per_bank))
            for j in range(per_bank):
                g, x = divmod((unit + j) % UNITS_PER_STRIP, 2)
                scores = bank[:, j * n_keys : (j + 1) * n_keys]
                nc.tensor.matmul(
                    out=scores,
                    lhsT=qT[:, r // 2, g, 2 * x + r % 2].rearrange("p u q -> p (u q)"),
                    rhs=kT[:, g, 0:n_keys],
                    start=True,
                    stop=False,
                )
                nc.tensor.matmul(
                    out=scores[:, r * STRIP : n_keys],
                    lhsT=ident_bf[:],
                    rhs=mask[:, 0 : n_keys - r * STRIP],
                    start=False,
                    stop=True,
                )

        def row_maximum(unit):
            r = strip_of(unit)
            per_bank = UNITS_PER_BANK[r]
            n_keys = keys_of(r)
            bank = bank_of["scores", unit // per_bank]
            if r >= LOWER:
                scaled = stage.tile([P, S], BF16, name="scaled", bufs=2)
                shift = stats.tile([P, 1], F32, name="shift1")
                nc.vector.tensor_scalar(
                    out=scaled[:, 0:n_keys],
                    in0=bank[:, 0:n_keys],
                    scalar1=-SCALE,
                    scalar2=HUGE,
                    op0=ALU.mult,
                    op1=ALU.min,
                    accum_out=shift[:],
                )
                shift_of[unit] = shift[:]
            elif unit % per_bank == 0:
                rowmax = stats.tile([P, per_bank], F32, name="rowmax%d" % per_bank)
                unit_scores = bank[:, 0 : per_bank * n_keys].rearrange("p (h k) -> p h k", h=per_bank)
                nc.vector.tensor_reduce(
                    out=rowmax[:],
                    in_=unit_scores[:, :, 0 : (r + 1) * STRIP],
                    axis=AXIS.X,
                    op=ALU.max,
                )
                rowmax_of[unit] = rowmax

        def scale_maximum(unit):
            r = strip_of(unit)
            per_bank = UNITS_PER_BANK[r]
            if r < LOWER and unit % per_bank == 0:
                shift = stats.tile([P, per_bank], F32, name="shift%d" % per_bank)
                nc.scalar.activation(out=shift[:], in_=rowmax_of[unit][:], func=ACT.Copy, scale=-SCALE)
                for j in range(per_bank):
                    shift_of[unit + j] = shift[:, j : j + 1]

        def exponential(unit):
            step, j = divmod(unit, QUAD)
            r = strip_of(unit)
            per_bank = UNITS_PER_BANK[r]
            n_keys = keys_of(r)
            e_tile = e_tiles[step % E_TILES]
            if unit % UNITS_PER_STRIP == 0:
                rowsum_of[step // 2] = stats.tile([P, UNITS_PER_STRIP], F32, name="rowsum")
            if r >= LOWER:
                halves = 1
                e_keys = e_tile[:, j * S : j * S + n_keys].rearrange("p (h k) -> p h k", h=1)
            else:
                halves = max(1, n_keys // P)
                g_keys = e_tile[:, j // 2 * S : (j // 2 + 1) * S].rearrange("p (h x k) -> p h x k", h=2, x=2)
                e_keys = g_keys[:, 0:halves, j % 2, 0 : n_keys // halves]
            first = unit % per_bank * n_keys
            scores = bank_of["scores", unit // per_bank][:, first : first + n_keys]
            nc.scalar.activation(
                out=e_keys,
                in_=scores.rearrange("p (h k) -> p h k", h=halves),
                func=ACT.Exp,
                bias=shift_of[unit],
                scale=SCALE,
                accum_out=rowsum_of[step // 2][:, unit % UNITS_PER_STRIP : unit % UNITS_PER_STRIP + 1],
            )
            if (unit + 1) % per_bank == 0:
                give(("scores", unit // per_bank))

        def reciprocal(place):
            rinv = stats.tile([P, UNITS_PER_STRIP], F32)
            nc.vector.reciprocal(out=rinv[:], in_=rowsum_of[place][:])
            rinv_of[place] = rinv

        def clear_e(step):
            follower = step + E_TILES
            if follower >= STEPS:
                return
            r = STRIP_ORDER[follower // 2]
            e_tile = e_tiles[step % E_TILES][:]
            if LOWER <= r < STRIPS - 1:
                behind_upper = step >= 0 and STRIP_ORDER[step // 2] >= LOWER
                end = min(S, (r + 3) * STRIP) if behind_upper else S
                nc.gpsimd.memset(
                    e_tile.rearrange("p (j k) -> p j k", j=QUAD)[:, :, (r + 1) * STRIP : end], 0.0
                )
            elif r < 2:
                e_halves = e_tile[:, 0 : 2 * S].rearrange("p (g h k) -> p g h k", g=2, h=2)
                nc.gpsimd.memset(e_halves[:, :, 1, :], 0.0)
                if r == 0:
                    low_half = e_halves[:, :, 0, :].rearrange("p g (x k) -> p g x k", x=2)
                    nc.gpsimd.memset(low_half[:, :, :, STRIP:P], 0.0)

        def is_lower(step):
            return STRIP_ORDER[step // 2] < LOWER

        def turn_e(pair):
            step, i = divmod(pair, 2)
            lower = is_lower(step)
            e_words = e_tiles[step % E_TILES][:].bitcast(F32)
            if not lower or i == 0:
                turned_e[pair] = take(("e", pair)).rearrange("p (h u i) -> p h u i", h=2, u=2)
            else:
                turned_e[pair] = turned_e[pair - 1]
            for j in [i] if lower else [0, 1]:
                for u in range(2):
                    first = (2 * j + u) * P if lower else (4 * i + 2 * j + u) * P
                    nc.tensor.transpose(
                        out=turned_e[pair][:, j, u, :], in_=e_words[:, first : first + P], identity=ident_f32[:]
                    )

        def copy_e(pair):
            step, i = divmod(pair, 2)
            lower = is_lower(step)
            if lower and i == 0:
                return
            if lower or i == 0:
                e_grouped_of[step] = stage.tile(
                    [P, 2 if lower else QUAD, P * PACK], BF16, align_bytes=64, name="e_grouped", bufs=3
                )
            words = e_grouped_of[step][:].rearrange("p h t -> p (h t)").bitcast(F32)
            words = words.rearrange("p (h i u) -> p h i u", i=P, u=2)
            first = 0 if lower else 2 * i
            nc.scalar.copy(
                out=words[:, first : first + 2, :, :], in_=turned_e[pair].rearrange("p h u i -> p h i u")
            )
            give(("e", pair - 1 if lower else pair))

        def quantise_e(step):
            columns = (2 if is_lower(step) else QUAD) * P
            e_codes = stage.tile([P, columns], U32, align_bytes=64, name="e_codes")
            e_scales = stage.tile([P, columns], U8, align_bytes=64, name="e_scales")
            nc.vector.quantize_mx(
                out=e_codes[:].bitcast(FP8X4),
                scales=e_scales[:],
                in_=e_grouped_of[step][:].rearrange("p h t -> p (h t)"),
            )
            e_operand[step] = (e_codes, e_scales)

        def multiply_v(step):
            e_codes, e_scales = e_operand[step]
            pv = take(("pv", step))
            lower = is_lower(step)
            codes, scales, n = (pair_codes, pair_scales, 2 * D) if lower else (v_codes, v_scales, D)
            for j in range(2 if lower else QUAD):
                g = 2 * (step % 2) + (j if lower else j // 2)
                columns = slice(j * P, (j + 1) * P)
                nc.tensor.matmul_mx(
                    out=pv[:, j * n : (j + 1) * n],
                    lhsT=e_codes[:, columns].bitcast(FP8X4),
                    lhsT_scale=e_scales[:, columns],
                    rhs=codes[:, g * n : (g + 1) * n].bitcast(FP8X4),
                    rhs_scale=scales[:, g * n : (g + 1) * n],
                    start=True,
                    stop=True,
                )
            pv_of[step] = pv.rearrange("p (h d) -> p h d", h=QUAD)

        def normalise(step):
            o_sb = stage.tile([P, QUAD * D], BF16)
            nc.vector.tensor_tensor(
                out=o_sb[:].rearrange("p (h d) -> p h d", h=QUAD),
                in0=pv_of[step],
                in1=rinv_of[step // 2][:, step % 2 * QUAD : (step % 2 + 1) * QUAD].unsqueeze(2).to_broadcast([P, QUAD, D]),
                op=ALU.mult,
            )
            o_sb_of[step] = o_sb
            give(("pv", step))

        def turn_o(step):
            o_words = o_sb_of[step][:].bitcast(F32)
            turned = take(("o", step))[:, 0 : 2 * P].rearrange("p (g i) -> p g i", g=2)
            for j in range(2):
                nc.tensor.transpose(out=turned[:, j, :], in_=o_words[:, j * P : (j + 1) * P], identity=ident_f32[:])
            turned_o[step] = turned

        def copy_o(step):
            place, rest = divmod(step, 4)
            r = STRIP_ORDER[step // 2]
            half = 2 * place + step % 2
            if rest < 2:
                o_grouped_of[half] = stage.tile([P, 2 * P * PACK], BF16, align_bytes=64, name="o_grouped")
            words = o_grouped_of[half][:].bitcast(F32).rearrange("p (g r q u) -> p g r q u", g=2, r=2, u=2)
            nc.scalar.copy(
                out=words[:, :, r % 2, :, :], in_=turned_o[step].rearrange("p g (u q) -> p g q u", u=2)
            )
            give(("o", step))

        def quantise_o(half):
            place, pair_of_g = divmod(half, 2)
            columns = slice(pair_of_g * 2 * P, (pair_of_g + 1) * 2 * P)
            nc.vector.quantize_mx(
                out=o_codes[place][:, columns].bitcast(FP8X4),
                scales=o_scales[place][:, columns],
                in_=o_grouped_of[half][:],
            )

        def group(raw):
            grouped = stage.tile([P, HKV * D * PACK], BF16, align_bytes=64, name="v_grouped", bufs=1)
            nc.vector.tensor_copy(
                out=grouped[:].rearrange("p (c t) -> p c t", t=PACK), in_=raw[:].rearrange("p t c -> p c t")
            )
            return grouped

        def quantise_v():
            grouped = group(v_sb)
            nc.vector.quantize_mx(out=v_codes[:].bitcast(FP8X4), scales=v_scales[:], in_=grouped[:])

        def group_pair():
            pair_grouped_of["v"] = group(pair_sb)

        def quantise_pair():
            nc.vector.quantize_mx(
                out=once_codes[:].bitcast(FP8X4), scales=once_scales[:], in_=pair_grouped_of["v"][:]
            )

        def place_pair():
            to = pair_codes[:].bitcast(I32).rearrange("p (g x d) -> p g x d", g=HKV, x=2)
            source = once_codes[:].bitcast(I32).rearrange("p (g d) -> p g d", g=HKV)
            for x in range(2):
                half = slice(x * STRIP, (x + 1) * STRIP)
                nc.vector.tensor_copy(out=to[half, :, x, :], in_=source[half, :, :])
            for x in range(2):
                nc.vector.tensor_copy(
                    out=pair_scales[:].bitcast(I32).rearrange("p (g x d) -> p g x d", g=HKV, x=2)[:, :, x, :],
                    in_=once_scales[:].bitcast(I32).rearrange("p (g d) -> p g d", g=HKV),
                )

        def w_place(piece):
            slab, rest = divmod(piece, 2 * PASSES)
            tiles, g = divmod(rest, PASSES)
            return slab, tiles, g

        def turn_w(piece):
            slab, tiles, g = w_place(piece)
            turned = take(("w", piece)).rearrange("p (r u n) -> p r u n", r=2, u=2)
            for j in range(2):
                words = w_sb[4 * slab + 2 * tiles + j][:].bitcast(F32)
                for u in range(2):
                    first = (2 * g + u) * P
                    nc.tensor.transpose(
                        out=turned[:, j, u, :], in_=words[:, first : first + P], identity=ident_f32[:]
                    )
            turned_w[piece] = turned

        def copy_w(piece):
            w_grouped = stage.tile([P, 2 * P * PACK], BF16, align_bytes=64, bufs=5)
            words = w_grouped[:].bitcast(F32).rearrange("p (r n u) -> p r n u", r=2, u=2)
            nc.scalar.copy(out=words, in_=turned_w[piece].rearrange("p r u n -> p r n u"))
            w_grouped_of[piece] = w_grouped
            give(("w", piece))

        def quantise_w(piece):
            slab, tiles, g = w_place(piece)
            features = slice(slab * BANK + tiles * 2 * P, slab * BANK + (tiles + 1) * 2 * P)
            nc.vector.quantize_mx(
                out=w_codes[:, g, features].bitcast(FP8X4),
                scales=w_scales[:, g, features],
                in_=w_grouped_of[piece][:],
            )

        def project_pass(block, g):
            place, slab = divmod(block, SLABS)
            features = slice(slab * BANK, (slab + 1) * BANK)
            if g == 0:
                acc_of[block] = take(("out", block))
            columns = slice(g * P, (g + 1) * P)
            nc.tensor.matmul_mx(
                out=acc_of[block],
                lhsT=o_codes[place][:, columns].bitcast(FP8X4),
                lhsT_scale=o_scales[place][:, columns],
                rhs=w_codes[:, g, features].bitcast(FP8X4),
                rhs_scale=w_scales[:, g, features],
                start=(g == 0),
                stop=(g == PASSES - 1),
            )

        def project(block):
            for g in range(PASSES):
                project_pass(block, g)

        def store(block):
            place, slab = divmod(block, SLABS)
            c = CHUNK_ORDER[place]
            result = results.tile([P, BANK], F32)
            copier(place < CHUNKS - 1 or slab % 2 == 0)(out=result[:], in_=acc_of[block])
            give(("out", block))
            nc.sync.dma_start(out=out_rows[c * P : (c + 1) * P, slab * BANK : (slab + 1) * BANK], in_=result[:])

        plan = {}

        def due(tick, stage_fn, *piece):
            plan.setdefault(tick, []).append((stage_fn, piece))

        def every(stage_fn, count, tick_of):
            for piece in range(count):
                due(tick_of(piece), stage_fn, piece)

        last_blocks = range(BLOCKS - SLABS, BLOCKS)
        start = turn_k_tick(0)

        for b in range(E_TILES):
            due(start, clear_e, b - E_TILES)
        due(start, warm_up)
        every(row_maximum, UNITS, lambda unit: unit_tick(unit) + MAX_AT)
        every(reciprocal, STRIPS, lambda place: step_tick(2 * place) + RECIPROCAL_AT)
        every(clear_e, STEPS, lambda step: step_tick(step) + CLEAR_E_AT)
        every(copy_e, PAIRS, lambda pair: pair_tick(pair) + COPY_E_AT)
        every(normalise, STEPS, lambda step: step_tick(step) + NORMALISE_AT)
        every(copy_o, STEPS, lambda step: step_tick(step) + COPY_O_AT)
        every(copy_w, W_PIECES, lambda piece: piece + COPY_W_AT)
        every(copy_k, HKV, lambda g: turn_k_tick(g) + FROM_PSUM)
        every(copy_q, CHUNKS * HKV, lambda piece: turn_q_tick(piece) + FROM_PSUM)
        for block in PROJECT_TICK:
            due(PROJECT_TICK[block] + FROM_PSUM, store, block)
        for block in last_blocks:
            due(quantise_o_tick(2 * CHUNKS - 1) + 1 + FROM_PSUM, store, block)
        every(exponential, UNITS, lambda unit: unit_tick(unit) + EXP_AT)
        every(scale_maximum, UNITS, lambda unit: unit_tick(unit) + MAX_AT)
        every(quantise_e, STEPS, lambda step: step_tick(step) + QUANTISE_E_AT)
        every(quantise_o, 2 * CHUNKS, quantise_o_tick)
        every(quantise_w, W_PIECES, lambda piece: piece + QUANTISE_W_AT)
        due(QUANTISE_V_AT, quantise_v)
        due(GROUP_PAIR_AT, group_pair)
        due(QUANTISE_PAIR_AT, quantise_pair)
        due(PLACE_PAIR_AT, place_pair)
        every(turn_e, PAIRS, lambda pair: pair_tick(pair) + TURN_E_AT)
        every(turn_o, STEPS, lambda step: step_tick(step) + TURN_O_AT)
        every(turn_w, W_PIECES, lambda piece: piece + TURN_W_AT)
        every(turn_k, HKV, turn_k_tick)
        every(turn_q, CHUNKS * HKV, turn_q_tick)
        every(score, UNITS, unit_tick)
        every(multiply_v, STEPS, lambda step: step_tick(step) + MULTIPLY_V_AT)
        for block in PROJECT_TICK:
            due(PROJECT_TICK[block], project, block)
        for g in range(PASSES):
            quantised = quantise_o_tick(2 * CHUNKS - 2 + g // 2) + 1
            for block in last_blocks:
                due(max(step_tick(STEPS - 1) + MULTIPLY_V_AT, quantised), project_pass, block, g)
        due(LAST_W_LOAD_AT, load_w, SLABS - 1)

        for tick in sorted(plan):
            for stage_fn, piece in plan[tick]:
                stage_fn(*piece)
